import numpy as np
import ml_dtypes


def mxq(x, axis, fmt="e4m3"):
    dtype, down = {"e4m3": (ml_dtypes.float8_e4m3fn, 7), "e5m2": (ml_dtypes.float8_e5m2, 14)}[fmt]
    v = np.moveaxis(np.asarray(x, np.float32).astype(ml_dtypes.bfloat16).astype(np.float64), axis, -1)
    blocks = v.reshape(v.shape[:-1] + (-1, 32))
    amax = np.abs(blocks).max(-1, keepdims=True)
    byte = np.maximum(np.where(amax > 0, np.frexp(amax)[1] - 1 + 127, 0) - down, 1)
    scale = np.exp2(byte - 127.0)
    codes = (blocks / scale).astype(np.float32).astype(dtype).astype(np.float64)
    return np.moveaxis((codes * scale).reshape(v.shape), -1, axis)


WIDE = False


def mx_kscale(k):
    if not WIDE:
        return np.ones(k)
    levels = np.array([18, -18])
    if k % 512:
        return np.exp2(np.random.permutation(np.resize(levels, k // 32))).repeat(32)
    a = np.empty((k // 512, 16))
    for p in range(k // 512):
        a[p, :8] = np.random.permutation(np.resize(levels, 8))
        for g in range(8):
            far = levels[np.abs(levels - a[p, g]) >= 10]
            a[p, g + 8] = far[np.random.randint(len(far))]
    return np.exp2(a.ravel()).repeat(32)


BF16 = ml_dtypes.bfloat16


def bf(x):
    return np.asarray(x, np.float32).astype(BF16)


def f64(x):
    return np.asarray(x).astype(np.float64)


B, S, H, HO, E = 4, 256, 512, 1024, 4
T = B * S


def softmax_last(l):
    ex = np.exp(l - l.max(-1, keepdims=True))
    return ex / ex.sum(-1, keepdims=True)


def setup_inputs():
    s = mx_kscale(T).reshape(B, S, 1)
    u = mx_kscale(HO)
    h0 = bf(np.random.standard_normal((B, S, H)))
    op_logits = bf(np.random.standard_normal((B, S, E)) * 1.3)
    We0 = bf(np.random.standard_normal((E, H, HO)) / np.sqrt(H))
    be = bf(np.random.standard_normal((E, HO)) * 0.3)
    g0 = bf(np.random.standard_normal((B, S, HO)) * np.exp2(np.random.randint(-6, 1, (B, S, 1))) * 4.0)
    op_w = softmax_last(f64(op_logits))
    return {"hidden_states": bf(f64(h0) * s),
            "op_logits": op_logits,
            "We": bf(f64(We0) / u),
            "be": be,
            "op_w": np.asarray(op_w, np.float32),
            "grad_out": bf(f64(g0) / s * u)}


def reference(hidden_states, op_logits, We, be, op_w, grad_out):
    h = f64(hidden_states).reshape(T, H)
    p = f64(op_w).reshape(T, E)
    g = f64(grad_out).reshape(T, HO)
    dz = (p[:, :, None] * g[:, None, :]).reshape(T, E * HO)
    wt = f64(We).transpose(1, 0, 2).reshape(H, E * HO)
    dh = mxq(dz, 1, "e5m2") @ mxq(wt, 1, "e4m3").T
    dw = mxq(h, 0, "e4m3").T @ mxq(dz, 0, "e5m2")
    return dh.reshape(B, S, H), dw.reshape(H, E, HO).transpose(1, 0, 2)

@@ -1,0 +1,267 @@
+from contextlib import ExitStack
+
+import concourse.mybir as mybir
+from concourse.masks import make_identity
+
+F32 = mybir.dt.float32
+BF16 = mybir.dt.bfloat16
+U32 = mybir.dt.uint32
+U8 = mybir.dt.uint8
+E4M3 = mybir.dt.float8_e4m3fn_x4
+E5M2 = mybir.dt.float8_e5m2_x4
+MULT = mybir.AluOpType.mult
+
+P = 128
+E, H, HO, T = 4, 512, 1024, 1024
+FLOPS = 2 * 2 * T * H * E * HO
+BYTES = 2 * (T * H + E * H * HO + T * HO) + 4 * T * E + 4 * (T * H + E * H * HO)
+
+F_ORDER = [(0, 0), (1, 0), (2, 0), (3, 0), (0, 1), (1, 1), (2, 1), (3, 1)]
+T_ORDER = [(0, 0), (1, 0), (0, 1), (1, 1), (2, 0), (2, 1), (3, 0), (3, 1)]
+
+
+def tile_enhancedmathematicalreasoning_pa_v_kernel(
+    tc, hidden_states, op_logits, We, be, op_w, grad_out, out_0, out_1
+):
+    nc = tc.nc
+    h_view = hidden_states.flatten_outer_dims().rearrange("(g p j) w -> g p j w", g=2, j=4)
+    g_view = grad_out.flatten_outer_dims().rearrange("(g p j) w -> g p j w", g=2, j=4)
+    w_view = We.rearrange("e (a p) w -> e p a w", p=P)
+    p_view = op_w.flatten_outer_dims().rearrange("(g p j) e -> p g (j e)", g=2, j=4)
+    o0_view = out_0.flatten_outer_dims().rearrange("(g p j) w -> g j p w", g=2, j=4)
+    o1_view = out_1.rearrange("e (m p) w -> e m p w", p=P)
+
+    with ExitStack() as ctx:
+        keep = ctx.enter_context(tc.tile_pool(name="keep", bufs=1))
+        wraw_pool = ctx.enter_context(tc.tile_pool(name="wraw", bufs=3))
+        nat_pool = ctx.enter_context(tc.tile_pool(name="nat", bufs=5))
+        int_pool = ctx.enter_context(tc.tile_pool(name="int", bufs=4))
+        gf_pool = ctx.enter_context(tc.tile_pool(name="gf", bufs=6))
+        gw_pool = ctx.enter_context(tc.tile_pool(name="gw", bufs=3))
+        ct_pool = ctx.enter_context(tc.tile_pool(name="ct", bufs=12))
+        cf_pool = ctx.enter_context(tc.tile_pool(name="cf", bufs=4))
+        st_pool = ctx.enter_context(tc.tile_pool(name="st", bufs=5))
+        s0_pool = ctx.enter_context(tc.tile_pool(name="s0", bufs=4))
+        acc_pool = ctx.enter_context(tc.psum_pool(name="acc", bufs=1))
+        rot_pool = ctx.enter_context(tc.psum_pool(name="rot", bufs=4))
+
+        ident = keep.tile([P, P], F32, name="ident")
+        make_identity(nc, ident[:])
+        warm = keep.tile([P, 2], F32, name="warm")
+        nc.gpsimd.memset(warm[:], 0.0)
+        nc.scalar.copy(out=warm[:, 1:2], in_=warm[:, 0:1])
+
+        p_sb = keep.tile([P, 2, 16], F32, name="p_sb")
+        g_sb = [keep.tile([P, 4, HO], BF16, name=f"g_sb{g}") for g in range(2)]
+        h_sb = [keep.tile([P, 4, H], BF16, name=f"h_sb{g}") for g in range(2)]
+        w_raw = {}
+        nc.sync.dma_start(out=p_sb[:], in_=p_view)
+        for j in range(4):
+            nc.sync.dma_start(out=g_sb[0][:, j, :], in_=g_view[0, :, j, :])
+
+        def load_w(e):
+            raw = wraw_pool.tile([P, 4, HO], BF16, name="w_raw", tag="w_raw")
+            for a in (0, 2):
+                nc.sync.dma_start(out=raw[:, a : a + 2, :], in_=w_view[e, :, a : a + 2, :])
+            w_raw[e] = raw
+
+        load_w(0)
+        load_w(1)
+        load_w(2)
+        nc.sync.dma_start(out=h_sb[0][:], in_=h_view[0])
+        nc.sync.dma_start(out=g_sb[1][:], in_=g_view[1])
+        nc.sync.dma_start(out=h_sb[1][:], in_=h_view[1])
+        load_w(3)
+
+        nat = {}
+        gf = {}
+        cf = {}
+        gw = {}
+        cw = {}
+        ti = {}
+        ct = {}
+        gh = {}
+        ch = {}
+        acc = {}
+
+        def ts(cell):
+            e, g = cell
+            tile = nat_pool.tile([P, 4, HO], BF16, name="nat", tag="nat", align_bytes=64)
+            nat[cell] = tile
+            for j in range(4):
+                nc.vector.tensor_scalar(
+                    out=tile[:, j, :].rearrange("p (u w x) -> p u w x", u=2, x=2),
+                    in0=g_sb[g][:, j, :].rearrange("p (w u x) -> p u w x", u=2, x=2),
+                    scalar1=p_sb[:, g, 4 * j + e : 4 * j + e + 1],
+                    scalar2=None,
+                    op0=MULT,
+                )
+
+        def evac(bank, dst):
+            nc.scalar.copy(
+                out=dst.rearrange("p (s r u) -> p s r u", s=2, u=2),
+                in_=bank[:].rearrange("p (s u r) -> p s r u", s=2, u=2),
+            )
+
+        def tr(cell):
+            words = nat[cell][:].rearrange("p j w -> p (j w)").bitcast(F32)
+            for c in range(2):
+                dst = gf_pool.tile([P, 2048], BF16, name="gf", tag="gf", align_bytes=64)
+                gf[cell, c] = dst
+                for jp in range(2):
+                    bank = rot_pool.tile([P, 512], F32, name="rot", tag="rot")
+                    for s in range(2):
+                        for u in range(2):
+                            w0 = (2 * jp + s) * 512 + u * 256 + c * 128
+                            k = (2 * s + u) * 128
+                            nc.tensor.transpose(bank[:, k : k + 128], words[:, w0 : w0 + 128], ident[:])
+                    evac(bank, dst[:].bitcast(F32)[:, jp * 512 : (jp + 1) * 512])
+
+        def trw(e):
+            words = w_raw[e][:].rearrange("p a w -> p (a w)").bitcast(F32)
+            for c in range(2):
+                dst = gw_pool.tile([P, 2048], BF16, name="gw", tag="gw", align_bytes=64)
+                gw[e, c] = dst
+                for ap in range(2):
+                    bank = rot_pool.tile([P, 512], F32, name="rot", tag="rot")
+                    for s in range(2):
+                        for u in range(2):
+                            w0 = (2 * ap + s) * 512 + c * 256 + u
+                            k = (2 * s + u) * 128
+                            nc.tensor.transpose(bank[:, k : k + 128], words[:, w0 : w0 + 255 : 2], ident[:])
+                    evac(bank, dst[:].bitcast(F32)[:, ap * 512 : (ap + 1) * 512])
+
+        def quant(pool, tag, src, fmt):
+            codes = pool.tile([P, 512], U32, name="c_" + tag, tag="c_" + tag, align_bytes=64)
+            scales = pool.tile([P, 512], U8, name="s_" + tag, tag="s_" + tag, align_bytes=64)
+            nc.vector.quantize_mx(out=codes[:].bitcast(fmt), scales=scales[:], in_=src)
+            return codes, scales
+
+        def qf(cell, c):
+            cf[cell, c] = quant(cf_pool, "cf", gf[cell, c][:], E5M2)
+
+        def qw(e, c):
+            cw[e, c] = quant(keep, f"cw{e}{c}", gw[e, c][:], E4M3)
+
+        def int_h(g):
+            tile = gw_pool.tile([P, 2048], BF16, name="gw", tag="gw", align_bytes=64)
+            gh[g] = tile
+            nc.scalar.copy(
+                out=tile[:].rearrange("p (w j) -> p w j", j=4),
+                in_=h_sb[g][:].rearrange("p j w -> p w j"),
+            )
+
+        def qh(g):
+            ch[g] = quant(keep, f"ch{g}", gh[g][:], E4M3)
+
+        def int_t(cell, c):
+            tile = int_pool.tile([P, 2048], BF16, name="ti", tag="ti", align_bytes=64)
+            ti[cell, c] = tile
+            nc.vector.tensor_copy(
+                out=tile[:].rearrange("p (u w j) -> p u w j", u=2, j=4),
+                in_=nat[cell][:].rearrange("p j (u c w) -> p c u w j", u=2, c=2)[:, c],
+            )
+
+        def qt(cell, c):
+            ct[cell, c] = quant(ct_pool, "ct", ti[cell, c][:], E5M2)
+
+        def mx(out, lhs, l0, lfmt, rhs, rfmt, start, stop):
+            nc.tensor.matmul_mx(
+                out=out,
+                lhsT=lhs[0][:, l0 : l0 + 128].bitcast(lfmt),
+                lhsT_scale=lhs[1][:, l0 : l0 + 128],
+                rhs=rhs[0][:].bitcast(rfmt),
+                rhs_scale=rhs[1][:],
+                start=start,
+                stop=stop,
+            )
+
+        def mm0(cell):
+            e, g = cell
+            if e == 0:
+                for j in range(4):
+                    acc[g, j] = acc_pool.tile([P, 512], F32, name=f"acc{j}", tag=f"acc{j}")
+            for c in range(2):
+                for j in range(4):
+                    mx(acc[g, j][:], cf[cell, c], 128 * j, E5M2, cw[e, c], E4M3,
+                       e == 0 and c == 0, e == 3 and c == 1)
+            if e == 3:
+                for j in range(4):
+                    stage = s0_pool.tile([P, 512], F32, name="s0", tag="s0")
+                    nc.scalar.copy(out=stage[:], in_=acc[g, j][:])
+                    nc.sync.dma_start(out=o0_view[g, j], in_=stage[:])
+
+        def ev1(eng, bank, dst):
+            args = dict(
+                out=dst.rearrange("p (w u x) -> p w u x", u=2, x=2),
+                in_=bank[:].rearrange("p (u w x) -> p w u x", u=2, x=2),
+            )
+            if eng == 0:
+                nc.scalar.copy(**args)
+            else:
+                nc.vector.tensor_copy(**args)
+
+        def mm1(e, ms):
+            for m in ms:
+                stage = st_pool.tile([P, HO], F32, name="st", tag="st")
+                for c in range(2):
+                    bank = rot_pool.tile([P, 512], F32, name="rot", tag="rot")
+                    for g in range(2):
+                        mx(bank[:], ch[g], 128 * m, E4M3, ct[(e, g), c], E5M2, g == 0, g == 1)
+                    ev1(0, bank, stage[:, 512 * c : 512 * c + 512])
+                nc.sync.dma_start(out=o1_view[e, m], in_=stage[:])
+
+        with tc.manual_schedule():
+            ts(F_ORDER[0])
+            tr(F_ORDER[0])
+            trw(0)
+            ts(F_ORDER[1])
+            ts(F_ORDER[2])
+            tr(F_ORDER[1])
+            trw(1)
+            banks = {}
+            for i in range(8):
+                if i + 2 < 8:
+                    tr(F_ORDER[i + 2])
+                if i + 2 < 4:
+                    trw(i + 2)
+                if i < 2:
+                    int_h(i)
+                int_t(T_ORDER[i], 0)
+                int_t(T_ORDER[i], 1)
+                qf(F_ORDER[i], 0)
+                qt(T_ORDER[i], 0)
+                qf(F_ORDER[i], 1)
+                qt(T_ORDER[i], 1)
+                if i < 4:
+                    qw(i, 0)
+                    qw(i, 1)
+                if i in (1, 2):
+                    qh(i - 1)
+                if i + 3 < 8:
+                    ts(F_ORDER[i + 3])
+                if i == 3:
+                    mm1(0, range(4))
+                if i == 4:
+                    mm1(1, range(2))
+                if i == 5:
+                    mm1(1, range(2, 4))
+                if i == 6:
+                    mm1(2, range(4))
+                mm0(F_ORDER[i])
+            stages = [st_pool.tile([P, HO], F32, name="st", tag="st") for m in range(4)]
+            for c in range(2):
+                for m in range(4):
+                    if c == 0:
+                        banks[m, c] = rot_pool.tile([P, 512], F32, name="rot", tag="rot")
+                    else:
+                        banks[m, c] = acc_pool.tile([P, 512], F32, name=f"acc{m}", tag=f"acc{m}")
+                    mx(banks[m, c][:], ch[0], 128 * m, E4M3, ct[(3, 0), c], E5M2, True, False)
+            for c in range(2):
+                for m in range(4):
+                    mx(banks[m, c][:], ch[1], 128 * m, E4M3, ct[(3, 1), c], E5M2, False, True)
+                    ev1(m % 2, banks[m, c], stages[m][:, 512 * c : 512 * c + 512])
+                    nc.sync.dma_start(
+                        out=o1_view[3, m][:, 512 * c : 512 * c + 512],
+                        in_=stages[m][:, 512 * c : 512 * c + 512],
+                    )

@@ -16,252 +16,404 @@ E, H, HO, T = 4, 512, 1024, 1024
 FLOPS = 2 * 2 * T * H * E * HO
 BYTES = 2 * (T * H + E * H * HO + T * HO) + 4 * T * E + 4 * (T * H + E * H * HO)
 
-F_ORDER = [(0, 0), (1, 0), (2, 0), (3, 0), (0, 1), (1, 1), (2, 1), (3, 1)]
-T_ORDER = [(0, 0), (1, 0), (0, 1), (1, 1), (2, 0), (2, 1), (3, 0), (3, 1)]
+DEPTH = {"nat": 6, "gf": 4, "gw": 3, "ti": 3, "cf": 5, "ct": 9, "rot": 4, "acc": 4, "st": 8, "ws": 2}
+SORTED = ()
+RUN4 = 0
+SWARM = 0
+NW = 0
+NK = 0
+
+
+def orders():
+    def M(e, g):
+        return [("M", e, g, j) for j in range(4)]
+
+    def TF(e, g):
+        return [("TF", e, g, c, jp) for c in range(2) for jp in range(2)]
+
+    def TW(e, c):
+        return [("TW", e, c, ap) for ap in range(2)]
+
+    def X0(e, g, c):
+        return [("X0", e, g, c, j) for j in range(4)]
+
+    def X1(e, c):
+        return [("X1", e, c, m, g) for m in range(4) for g in range(2)]
+
+    def LW(e):
+        return [("L", "w", e, ap) for ap in range(2)]
+
+    def LG(g):
+        return [("L", "g2", g, jp) for jp in range(2)]
+
+    def I(e, g, c):
+        return [("I", e, g, c)]
+
+    def QT(e, g, c):
+        return [("QT", e, g, c)]
+
+    def QF(e, g, c):
+        return [("QF", e, g, c)]
+
+    def QW(e, c):
+        return [("QW", e, c)]
+
+    def QH(g):
+        return [("QH", g)]
+
+    F = [(e, g) for g in range(2) for e in range(4)]
+    U = [(e, c) for e in range(4) for c in range(2)]
+
+    def HM(g, u):
+        return [("HM", g, u)]
+
+    def IM(e, g, c, u):
+        return [("IM", e, g, c, u)]
+
+    def EI(e, g, c, u):
+        return [("EI", e, g, c, u)]
+
+    def SW(e, a):
+        return [("SW", e, a)]
+
+    def IH(g, q):
+        return [("IH", g, q)]
+
+    def WU(a, n):
+        return [("WU", a, i) for i in range(n)]
+
+    def T(e, c):
+        return I(e, 0, c) + I(e, 1, c) + QT(e, 0, c) + QT(e, 1, c)
+
+    def I2(e, g, c, u):
+        return [("I2", e, g, c, u)]
+
+    loads = [("L", "p")] + [("L", "g", 0, j) for j in range(4)] + LW(0) + LW(1) + [("L", "h", 0)] + LG(1) + LW(2) + [("L", "h", 1)] + LW(3)
+    t0 = [("TF", 0, 0, c, jp) for jp in range(2) for c in range(2)]
+    pe = WU(0, NW) + t0[:2] + WU(1, NK) + t0[2:] + WU(2, NK) + [("TW", 0, 0, 0), ("TW", 0, 1, 0)] + WU(3, NK) + [("TW", 0, 0, 1), ("TW", 0, 1, 1)] + WU(4, NK) + TF(1, 0)
+    pe += X0(0, 0, 0) + TW(1, 0) + X0(0, 0, 1) + TW(1, 1) + TF(2, 0)
+    pe += X0(1, 0, 0) + TW(2, 0) + X0(1, 0, 1) + TW(2, 1) + TF(3, 0)
+    pe += X0(2, 0, 0) + TW(3, 0) + X0(2, 0, 1) + TW(3, 1) + TF(0, 1)
+    pe += X1(0, 0) + X0(3, 0, 0) + TF(1, 1) + X1(0, 1) + X0(3, 0, 1)
+    pe += X1(1, 0) + X0(0, 1, 0) + X0(0, 1, 1) + TF(2, 1)
+    pe += X0(1, 1, 0) + X1(1, 1) + X0(1, 1, 1) + TF(3, 1)
+    pe += X0(2, 1, 0) + X1(2, 0) + X0(2, 1, 1) + X1(2, 1)
+    pe += X0(3, 1, 0)[:2] + X0(3, 1, 1)[:2] + X1(3, 0) + X0(3, 1, 0)[2:3] + X0(3, 1, 1)[2:3] + X0(3, 1, 0)[3:] + X0(3, 1, 1)[3:] + X1(3, 1)
+    vec = M(0, 0) + M(1, 0) + I(0, 0, 0) + QF(0, 0, 0) + QT(0, 0, 0) + QF(0, 0, 1) + QW(0, 0) + QW(0, 1) + M(2, 0) + I(0, 0, 1) + QF(1, 0, 0) + QT(0, 0, 1) + QF(1, 0, 1)
+    vec += QW(1, 0) + M(0, 1) + M(3, 0) + QW(1, 1) + I(0, 1, 0) + QF(2, 0, 0) + QT(0, 1, 0) + QF(2, 0, 1) + QW(2, 0) + I(0, 1, 1)
+    vec += M(1, 1) + QW(2, 1) + QT(0, 1, 1) + QH(0) + I(1, 0, 0) + QF(3, 0, 0) + QF(3, 0, 1) + QH(1) + QW(3, 0) + I(1, 1, 0) + QT(1, 0, 0) + QT(1, 1, 0)
+    vec += QW(3, 1) + M(2, 1) + I(1, 0, 1) + QF(0, 1, 0) + QF(0, 1, 1) + I(1, 1, 1) + QT(1, 0, 1) + QT(1, 1, 1) + M(3, 1)
+    vec += T(2, 0) + QF(1, 1, 0) + QF(1, 1, 1) + T(2, 1) + QF(2, 1, 0) + QF(2, 1, 1) + T(3, 0) + QF(3, 1, 0) + QF(3, 1, 1) + T(3, 1)
+    vec += [("E1", 3, 1, 1), ("E1", 3, 1, 3)]
+    act_extra = {("EW", 1, 0, 1): IH(0, 0), ("EF", 2, 0, 1, 1): IH(0, 1), ("EW", 2, 0, 1): IH(1, 0), ("EF", 3, 0, 1, 1): IH(1, 1)}
+
+    return loads, pe, vec, act_extra
 
 
 def tile_enhancedmathematicalreasoning_pa_v_kernel(
     tc, hidden_states, op_logits, We, be, op_w, grad_out, out_0, out_1
 ):
     nc = tc.nc
-    h_view = hidden_states.flatten_outer_dims().rearrange("(g p j) w -> g p j w", g=2, j=4)
-    g_view = grad_out.flatten_outer_dims().rearrange("(g p j) w -> g p j w", g=2, j=4)
-    w_view = We.rearrange("e (a p) w -> e p a w", p=P)
+    h_view = hidden_states.flatten_outer_dims().rearrange("(g p j) w -> g p (j w)", g=2, j=4)
+    g_view = grad_out.flatten_outer_dims().rearrange("(g p j) w -> g p (j w)", g=2, j=4)
+    w_view = We.rearrange("e (p a) w -> e p (a w)", a=4)
     p_view = op_w.flatten_outer_dims().rearrange("(g p j) e -> p g (j e)", g=2, j=4)
     o0_view = out_0.flatten_outer_dims().rearrange("(g p j) w -> g j p w", g=2, j=4)
     o1_view = out_1.rearrange("e (m p) w -> e m p w", p=P)
 
+    loads, pe, vec, act_extra = orders()
+
+    def writes(job):
+        k = job[0]
+        if k == "M":
+            return [("nat", job[1], job[2])]
+        if k in ("TF", "TW", "IM", "HM"):
+            return [("rot",) + job]
+        if k == "EF":
+            return [("gf", job[1], job[2], job[3])]
+        if k == "EW":
+            return [("gw", job[1], job[2])]
+        if k == "SW":
+            return [("ws", job[1], job[2])]
+        if k in ("I", "EI", "I2"):
+            return [("ti", job[1], job[2], job[3])]
+        if k in ("IH", "EH"):
+            return [("gh", job[1])]
+        if k == "QF":
+            return [("cf",) + job[1:]]
+        if k == "QT":
+            return [("ct",) + job[1:]]
+        if k == "QW":
+            return [("cw",) + job[1:]]
+        if k == "QH":
+            return [("ch",) + job[1:]]
+        if k == "X0":
+            return [("acc", job[2], job[4])]
+        if k == "X1":
+            return [("rot", "X1", job[1], job[2], job[3])]
+        if k == "E0":
+            return [("st", 0, job[1], job[2])]
+        if k == "E1":
+            return [("st", 1, job[1], job[2], job[3])]
+        if k == "L":
+            return [job[1:]]
+        return []
+
+    def g_piece(g, j):
+        return ("g", g, j) if ("L", "g", g, j) in loads else ("g2", g, j // 2)
+
+    def reads(job):
+        k = job[0]
+        if k == "M":
+            return [g_piece(job[2], job[3]), ("p",)]
+        if k == "TF":
+            return [("nat", job[1], job[2])]
+        if k == "TW":
+            return [("ws" if job[1] in SORTED else "w", job[1], job[3])]
+        if k == "SW":
+            return [("w", job[1], job[2])]
+        if k in ("I", "IM", "I2"):
+            return [("nat", job[1], job[2])]
+        if k in ("IH", "HM"):
+            return [("h", job[1])]
+        if k == "EF":
+            return [("rot", "TF") + job[1:]]
+        if k == "EW":
+            return [("rot", "TW") + job[1:]]
+        if k == "EI":
+            return [("rot", "IM") + job[1:]]
+        if k == "EH":
+            return [("rot", "HM") + job[1:]]
+        if k == "QF":
+            return [("gf",) + job[1:]]
+        if k == "QT":
+            return [("ti",) + job[1:]]
+        if k == "QW":
+            return [("gw",) + job[1:]]
+        if k == "QH":
+            return [("gh", job[1])]
+        if k == "X0":
+            return [("cf", job[1], job[2], job[3]), ("cw", job[1], job[3])]
+        if k == "X1":
+            return [("ct", job[1], job[4], job[2]), ("ch", job[4])]
+        if k == "E0":
+            return [("acc", job[1], job[2])]
+        if k == "E1":
+            return [("rot", "X1") + job[1:]]
+        if k == "S":
+            return [("st",) + job[1:]]
+        return []
+
+    def evac_of(job):
+        k = job[0]
+        if k in ("TF", "TW", "IM", "HM"):
+            return ({"TF": "EF", "TW": "EW", "IM": "EI", "HM": "EH"}[k],) + job[1:]
+        if k == "X1" and job[4] == 1:
+            return ("E1",) + job[1:4]
+        if k == "X0" and job[1] == 3 and job[3] == 1:
+            return ("E0", job[2], job[4])
+        return None
+
+    evacs = [evac_of(job) for job in pe if evac_of(job)]
+    act = []
+    for job in evacs:
+        if job not in vec:
+            act.append(job)
+        act.extend(act_extra.get(job, []))
+    act = act_extra.get("first", []) + act
+    stores = [("S", 0 if job[0] == "E0" else 1) + job[1:] for job in evacs if job[0] in ("E0", "E1")]
+    queues = [loads + [("ID",)] + stores, pe, vec, act]
+    jobs = [job for q in queues for job in q]
+    assert len(set(jobs)) == len(jobs)
+    writers, readers = {}, {}
+    for job in jobs:
+        for b in writes(job):
+            writers.setdefault(b, []).append(job)
+        for b in reads(job):
+            readers.setdefault(b, []).append(job)
+    order_of = {}
+    for job in pe + [j for j in evacs] + [("I",) + j[1:] for j in vec if j[0] == "QT"] + vec + act:
+        for b in writes(job):
+            if b[0] in DEPTH and b not in order_of.setdefault(b[0], []):
+                order_of[b[0]].append(b)
+    slot, before = {}, {}
+    for kind, bufs in order_of.items():
+        for n, b in enumerate(bufs):
+            slot[b] = n % DEPTH[kind]
+            if n >= DEPTH[kind]:
+                before[b] = bufs[n - DEPTH[kind]]
+
+    def needs(job):
+        out = []
+        for b in reads(job):
+            ws = writers[b]
+            if job[0] == "TF":
+                ws = [w for w in ws if w[3] // 2 == job[4]]
+            out.extend(ws)
+        for b in writes(job):
+            if b in before:
+                out.extend(readers[before[b]])
+        return out
+
     with ExitStack() as ctx:
-        keep = ctx.enter_context(tc.tile_pool(name="keep", bufs=1))
-        wraw_pool = ctx.enter_context(tc.tile_pool(name="wraw", bufs=3))
-        nat_pool = ctx.enter_context(tc.tile_pool(name="nat", bufs=5))
-        int_pool = ctx.enter_context(tc.tile_pool(name="int", bufs=4))
-        gf_pool = ctx.enter_context(tc.tile_pool(name="gf", bufs=6))
-        gw_pool = ctx.enter_context(tc.tile_pool(name="gw", bufs=3))
-        ct_pool = ctx.enter_context(tc.tile_pool(name="ct", bufs=12))
-        cf_pool = ctx.enter_context(tc.tile_pool(name="cf", bufs=4))
-        st_pool = ctx.enter_context(tc.tile_pool(name="st", bufs=5))
-        s0_pool = ctx.enter_context(tc.tile_pool(name="s0", bufs=4))
-        acc_pool = ctx.enter_context(tc.psum_pool(name="acc", bufs=1))
-        rot_pool = ctx.enter_context(tc.psum_pool(name="rot", bufs=4))
+        sb = ctx.enter_context(tc.tile_pool(name="sb", bufs=1))
+        ps = ctx.enter_context(tc.psum_pool(name="ps", bufs=1))
+        tiles = {}
 
-        ident = keep.tile([P, P], F32, name="ident")
-        make_identity(nc, ident[:])
-        warm = keep.tile([P, 2], F32, name="warm")
-        nc.gpsimd.memset(warm[:], 0.0)
-        nc.scalar.copy(out=warm[:, 1:2], in_=warm[:, 0:1])
+        def buf(b, shape, dtype, pool=sb, part=""):
+            if (b, part) not in tiles:
+                tag = f"{b[0]}{part}{slot[b]}" if b in slot else "_".join(str(x) for x in b) + part
+                if pool is sb:
+                    tiles[b, part] = pool.tile(shape, dtype, name=tag, tag=tag, align_bytes=64)
+                else:
+                    tiles[b, part] = pool.tile(shape, dtype, name=tag, tag=tag)
+            return tiles[b, part]
 
-        p_sb = keep.tile([P, 2, 16], F32, name="p_sb")
-        g_sb = [keep.tile([P, 4, HO], BF16, name=f"g_sb{g}") for g in range(2)]
-        h_sb = [keep.tile([P, 4, H], BF16, name=f"h_sb{g}") for g in range(2)]
-        w_raw = {}
-        nc.sync.dma_start(out=p_sb[:], in_=p_view)
-        for j in range(4):
-            nc.sync.dma_start(out=g_sb[0][:, j, :], in_=g_view[0, :, j, :])
+        def get(b, part=""):
+            return tiles[b, part]
 
-        def load_w(e):
-            raw = wraw_pool.tile([P, 4, HO], BF16, name="w_raw", tag="w_raw")
-            for a in (0, 2):
-                nc.sync.dma_start(out=raw[:, a : a + 2, :], in_=w_view[e, :, a : a + 2, :])
-            w_raw[e] = raw
+        ident = sb.tile([P, P], F32, name="ident")
+        ident_bf = sb.tile([P, P], BF16, name="ident_bf")
 
-        load_w(0)
-        load_w(1)
-        load_w(2)
-        nc.sync.dma_start(out=h_sb[0][:], in_=h_view[0])
-        nc.sync.dma_start(out=g_sb[1][:], in_=g_view[1])
-        nc.sync.dma_start(out=h_sb[1][:], in_=h_view[1])
-        load_w(3)
+        def run_len(e):
+            return 16 if e in SORTED else 2
 
-        nat = {}
-        gf = {}
-        cf = {}
-        gw = {}
-        cw = {}
-        ti = {}
-        ct = {}
-        gh = {}
-        ch = {}
-        acc = {}
+        def copy(job, out, in_):
+            if job in vec:
+                nc.vector.tensor_copy(out=out, in_=in_)
+            else:
+                nc.scalar.copy(out=out, in_=in_)
 
-        def ts(cell):
-            e, g = cell
-            tile = nat_pool.tile([P, 4, HO], BF16, name="nat", tag="nat", align_bytes=64)
-            nat[cell] = tile
-            for j in range(4):
-                nc.vector.tensor_scalar(
-                    out=tile[:, j, :].rearrange("p (u w x) -> p u w x", u=2, x=2),
-                    in0=g_sb[g][:, j, :].rearrange("p (w u x) -> p u w x", u=2, x=2),
-                    scalar1=p_sb[:, g, 4 * j + e : 4 * j + e + 1],
-                    scalar2=None,
-                    op0=MULT,
-                )
-
-        def evac(bank, dst):
-            nc.scalar.copy(
-                out=dst.rearrange("p (s r u) -> p s r u", s=2, u=2),
-                in_=bank[:].rearrange("p (s u r) -> p s r u", s=2, u=2),
-            )
-
-        def tr(cell):
-            words = nat[cell][:].rearrange("p j w -> p (j w)").bitcast(F32)
-            for c in range(2):
-                dst = gf_pool.tile([P, 2048], BF16, name="gf", tag="gf", align_bytes=64)
-                gf[cell, c] = dst
-                for jp in range(2):
-                    bank = rot_pool.tile([P, 512], F32, name="rot", tag="rot")
-                    for s in range(2):
-                        for u in range(2):
-                            w0 = (2 * jp + s) * 512 + u * 256 + c * 128
-                            k = (2 * s + u) * 128
-                            nc.tensor.transpose(bank[:, k : k + 128], words[:, w0 : w0 + 128], ident[:])
-                    evac(bank, dst[:].bitcast(F32)[:, jp * 512 : (jp + 1) * 512])
-
-        def trw(e):
-            words = w_raw[e][:].rearrange("p a w -> p (a w)").bitcast(F32)
-            for c in range(2):
-                dst = gw_pool.tile([P, 2048], BF16, name="gw", tag="gw", align_bytes=64)
-                gw[e, c] = dst
-                for ap in range(2):
-                    bank = rot_pool.tile([P, 512], F32, name="rot", tag="rot")
-                    for s in range(2):
-                        for u in range(2):
-                            w0 = (2 * ap + s) * 512 + c * 256 + u
-                            k = (2 * s + u) * 128
-                            nc.tensor.transpose(bank[:, k : k + 128], words[:, w0 : w0 + 255 : 2], ident[:])
-                    evac(bank, dst[:].bitcast(F32)[:, ap * 512 : (ap + 1) * 512])
-
-        def quant(pool, tag, src, fmt):
-            codes = pool.tile([P, 512], U32, name="c_" + tag, tag="c_" + tag, align_bytes=64)
-            scales = pool.tile([P, 512], U8, name="s_" + tag, tag="s_" + tag, align_bytes=64)
-            nc.vector.quantize_mx(out=codes[:].bitcast(fmt), scales=scales[:], in_=src)
-            return codes, scales
-
-        def qf(cell, c):
-            cf[cell, c] = quant(cf_pool, "cf", gf[cell, c][:], E5M2)
-
-        def qw(e, c):
-            cw[e, c] = quant(keep, f"cw{e}{c}", gw[e, c][:], E4M3)
-
-        def int_h(g):
-            tile = gw_pool.tile([P, 2048], BF16, name="gw", tag="gw", align_bytes=64)
-            gh[g] = tile
-            nc.scalar.copy(
-                out=tile[:].rearrange("p (w j) -> p w j", j=4),
-                in_=h_sb[g][:].rearrange("p j w -> p w j"),
-            )
-
-        def qh(g):
-            ch[g] = quant(keep, f"ch{g}", gh[g][:], E4M3)
-
-        def int_t(cell, c):
-            tile = int_pool.tile([P, 2048], BF16, name="ti", tag="ti", align_bytes=64)
-            ti[cell, c] = tile
-            nc.vector.tensor_copy(
-                out=tile[:].rearrange("p (u w j) -> p u w j", u=2, j=4),
-                in_=nat[cell][:].rearrange("p j (u c w) -> p c u w j", u=2, c=2)[:, c],
-            )
-
-        def qt(cell, c):
-            ct[cell, c] = quant(ct_pool, "ct", ti[cell, c][:], E5M2)
+        def quant(dst, src, fmt):
+            codes = buf(dst, [P, 512], U32)
+            scales = buf(dst, [P, 512], U8, part="s")
+            nc.vector.quantize_mx(out=codes[:].bitcast(fmt), scales=scales[:], in_=get(src)[:])
 
         def mx(out, lhs, l0, lfmt, rhs, rfmt, start, stop):
             nc.tensor.matmul_mx(
                 out=out,
-                lhsT=lhs[0][:, l0 : l0 + 128].bitcast(lfmt),
-                lhsT_scale=lhs[1][:, l0 : l0 + 128],
-                rhs=rhs[0][:].bitcast(rfmt),
-                rhs_scale=rhs[1][:],
+                lhsT=get(lhs)[:, l0 : l0 + P].bitcast(lfmt),
+                lhsT_scale=get(lhs, "s")[:, l0 : l0 + P],
+                rhs=get(rhs)[:].bitcast(rfmt),
+                rhs_scale=get(rhs, "s")[:],
                 start=start,
                 stop=stop,
             )
 
-        def mm0(cell):
-            e, g = cell
-            if e == 0:
-                for j in range(4):
-                    acc[g, j] = acc_pool.tile([P, 512], F32, name=f"acc{j}", tag=f"acc{j}")
-            for c in range(2):
-                for j in range(4):
-                    mx(acc[g, j][:], cf[cell, c], 128 * j, E5M2, cw[e, c], E4M3,
-                       e == 0 and c == 0, e == 3 and c == 1)
-            if e == 3:
-                for j in range(4):
-                    stage = s0_pool.tile([P, 512], F32, name="s0", tag="s0")
-                    nc.scalar.copy(out=stage[:], in_=acc[g, j][:])
-                    nc.sync.dma_start(out=o0_view[g, j], in_=stage[:])
+        def interleave_views(dst, src):
+            if RUN4:
+                return (dst.rearrange("p (u w i j) -> p u w j i", u=2, i=4, j=4), src.rearrange("p u (w i) j -> p u w j i", i=4))
+            return dst.rearrange("p (u w j) -> p u w j", u=2, j=4), src
 
-        def ev1(eng, bank, dst):
-            args = dict(
-                out=dst.rearrange("p (w u x) -> p w u x", u=2, x=2),
-                in_=bank[:].rearrange("p (u w x) -> p w u x", u=2, x=2),
-            )
-            if eng == 0:
-                nc.scalar.copy(**args)
-            else:
-                nc.vector.tensor_copy(**args)
-
-        def mm1(e, ms):
-            for m in ms:
-                stage = st_pool.tile([P, HO], F32, name="st", tag="st")
-                for c in range(2):
-                    bank = rot_pool.tile([P, 512], F32, name="rot", tag="rot")
-                    for g in range(2):
-                        mx(bank[:], ch[g], 128 * m, E4M3, ct[(e, g), c], E5M2, g == 0, g == 1)
-                    ev1(0, bank, stage[:, 512 * c : 512 * c + 512])
-                nc.sync.dma_start(out=o1_view[e, m], in_=stage[:])
+        def emit(job):
+            k = job[0]
+            w = writes(job)[0] if writes(job) else None
+            r = reads(job)[0] if reads(job) else None
+            if k == "ID":
+                make_identity(nc, ident[:])
+                if any(x[0] in ("IM", "HM") for x in pe):
+                    nc.scalar.copy(out=ident_bf[:], in_=ident[:])
+                elif SWARM:
+                    nc.scalar.copy(out=ident_bf[:, 0:2], in_=ident[:, 0:2])
+            elif k == "L":
+                if w[0] == "p":
+                    nc.scalar.dma_start(out=buf(w, [P, 2, 16], F32)[:], in_=p_view)
+                elif w[0] == "g":
+                    nc.sync.dma_start(out=buf(w, [P, HO], BF16)[:], in_=g_view[w[1], :, w[2] * HO : (w[2] + 1) * HO])
+                elif w[0] == "g2":
+                    nc.sync.dma_start(out=buf(w, [P, 2 * HO], BF16)[:], in_=g_view[w[1], :, w[2] * 2 * HO : (w[2] + 1) * 2 * HO])
+                elif w[0] == "w":
+                    nc.sync.dma_start(out=buf(w, [P, 2 * HO], BF16)[:], in_=w_view[w[1], :, w[2] * 2 * HO : (w[2] + 1) * 2 * HO])
+                else:
+                    nc.sync.dma_start(out=buf(w, [P, 4 * H], BF16)[:], in_=h_view[w[1]])
+            elif k == "M":
+                e, g, j = job[1:]
+                x = run_len(e)
+                src = get(r)[:] if r[0] == "g" else get(r)[:, (j % 2) * HO : (j % 2 + 1) * HO]
+                nc.vector.tensor_scalar(
+                    out=buf(w, [P, 4 * HO], BF16)[:, j * HO : (j + 1) * HO].rearrange("p (u w x) -> p u w x", u=2, x=x),
+                    in0=src.rearrange("p (w u x) -> p u w x", u=2, x=x),
+                    scalar1=get(("p",))[:, g, 4 * j + e : 4 * j + e + 1],
+                    scalar2=None,
+                    op0=MULT,
+                )
+            elif k == "SW":
+                copy(job, buf(w, [P, 2 * HO], BF16)[:].rearrange("p (a u w x) -> p a u w x", a=2, u=2, x=16),
+                     get(r)[:].rearrange("p (a w u x) -> p a u w x", a=2, u=2, x=16))
+            elif k in ("TF", "TW"):
+                c, half = job[-2:]
+                bank = buf(w, [P, 512], F32, ps)
+                words = get(r)[:].bitcast(F32)
+                for s in range(2):
+                    for u in range(2):
+                        row = (2 * half + s if k == "TF" else s) * 512
+                        if k == "TF" or job[1] in SORTED:
+                            src = words[:, row + u * 256 + c * P : row + u * 256 + (c + 1) * P]
+                        else:
+                            src = words[:, row + c * 256 + u : row + c * 256 + u + 255 : 2]
+                        nc.tensor.transpose(bank[:, (2 * s + u) * P : (2 * s + u + 1) * P], src, ident[:])
+            elif k in ("EF", "EW"):
+                half = job[-1]
+                dst = buf(w, [P, 2048], BF16)[:].bitcast(F32)[:, half * 512 : (half + 1) * 512]
+                copy(job, dst.rearrange("p (s r u) -> p s r u", s=2, u=2), get(r)[:].rearrange("p (s u r) -> p s r u", s=2, u=2))
+            elif k == "I":
+                c = job[3]
+                src = get(r)[:].rearrange("p (j u c w) -> p c u w j", j=4, u=2, c=2)[:, c]
+                copy(job, *interleave_views(buf(w, [P, 2048], BF16)[:], src))
+            elif k == "I2":
+                c, u = job[3:]
+                src = get(r)[:].rearrange("p (j u c q w) -> p c u q w j", j=4, u=2, c=2, q=2)[:, c, u]
+                copy(job, *interleave_views(buf(w, [P, 2048], BF16)[:, u * 1024 : (u + 1) * 1024], src))
+            elif k == "IH":
+                q = job[2]
+                src = get(r)[:].rearrange("p (j q u w) -> p q u w j", j=4, q=2, u=2)[:, q]
+                copy(job, *interleave_views(buf(w, [P, 2048], BF16)[:, q * 1024 : (q + 1) * 1024], src))
+            elif k == "WU":
+                if ("wu", "") not in tiles:
+                    tiles["wu", ""] = ps.tile([P, 512], F32, name="acc3", tag="acc3")
+                nc.tensor.matmul(out=get("wu")[:, 0:P], lhsT=ident[:], rhs=ident[:], start=True, stop=True)
+            elif k in ("IM", "HM"):
+                u = job[-1]
+                bank = buf(w, [P, 1024], BF16, ps)
+                if k == "IM":
+                    src = get(r)[:].rearrange("p (j u c w) -> p c u w j", j=4, u=2, c=2)[:, job[3], u]
+                else:
+                    src = get(r)[:].rearrange("p (j u w) -> p u w j", j=4, u=2)[:, u]
+                for n in range(2):
+                    nc.tensor.matmul(out=bank[:, n * 512 : (n + 1) * 512], lhsT=ident_bf[:], rhs=src[:, n * P : (n + 1) * P, :], start=True, stop=True)
+            elif k in ("EI", "EH"):
+                u = job[-1]
+                copy(job, buf(w, [P, 2048], BF16)[:, u * 1024 : (u + 1) * 1024], get(r)[:])
+            elif k in ("QF", "QT"):
+                quant(w, r, E5M2)
+            elif k in ("QW", "QH"):
+                quant(w, r, E4M3)
+            elif k == "X0":
+                e, g, c, j = job[1:]
+                mx(buf(w, [P, 512], F32, ps)[:], r, P * j, E5M2, ("cw", e, c), E4M3, e == 0 and c == 0, e == 3 and c == 1)
+            elif k == "X1":
+                e, c, m, g = job[1:]
+                mx(buf(w, [P, 512], F32, ps)[:], ("ch", g), P * m, E4M3, r, E5M2, g == 0, g == 1)
+            elif k == "E0":
+                copy(job, buf(w, [P, 512], F32)[:].rearrange("p (r a) -> p r a", a=4), get(r)[:].rearrange("p (a r) -> p r a", a=4))
+            elif k == "E1":
+                x = run_len(job[1])
+                copy(job, buf(w, [P, 512], F32)[:].rearrange("p (w u x) -> p w u x", u=2, x=x), get(r)[:].rearrange("p (u w x) -> p w u x", u=2, x=x))
+            elif k == "S":
+                if job[1] == 0:
+                    dst = o0_view[job[2], job[3]]
+                else:
+                    dst = o1_view[job[2], job[4]][:, job[3] * 512 : (job[3] + 1) * 512]
+                nc.sync.dma_start(out=dst, in_=get(r)[:])
 
         with tc.manual_schedule():
-            ts(F_ORDER[0])
-            tr(F_ORDER[0])
-            trw(0)
-            ts(F_ORDER[1])
-            ts(F_ORDER[2])
-            tr(F_ORDER[1])
-            trw(1)
-            banks = {}
-            for i in range(8):
-                if i + 2 < 8:
-                    tr(F_ORDER[i + 2])
-                if i + 2 < 4:
-                    trw(i + 2)
-                if i < 2:
-                    int_h(i)
-                int_t(T_ORDER[i], 0)
-                int_t(T_ORDER[i], 1)
-                qf(F_ORDER[i], 0)
-                qt(T_ORDER[i], 0)
-                qf(F_ORDER[i], 1)
-                qt(T_ORDER[i], 1)
-                if i < 4:
-                    qw(i, 0)
-                    qw(i, 1)
-                if i in (1, 2):
-                    qh(i - 1)
-                if i + 3 < 8:
-                    ts(F_ORDER[i + 3])
-                if i == 3:
-                    mm1(0, range(4))
-                if i == 4:
-                    mm1(1, range(2))
-                if i == 5:
-                    mm1(1, range(2, 4))
-                if i == 6:
-                    mm1(2, range(4))
-                mm0(F_ORDER[i])
-            stages = [st_pool.tile([P, HO], F32, name="st", tag="st") for m in range(4)]
-            for c in range(2):
-                for m in range(4):
-                    if c == 0:
-                        banks[m, c] = rot_pool.tile([P, 512], F32, name="rot", tag="rot")
-                    else:
-                        banks[m, c] = acc_pool.tile([P, 512], F32, name=f"acc{m}", tag=f"acc{m}")
-                    mx(banks[m, c][:], ch[0], 128 * m, E4M3, ct[(3, 0), c], E5M2, True, False)
-            for c in range(2):
-                for m in range(4):
-                    mx(banks[m, c][:], ch[1], 128 * m, E4M3, ct[(3, 1), c], E5M2, False, True)
-                    ev1(m % 2, banks[m, c], stages[m][:, 512 * c : 512 * c + 512])
-                    nc.sync.dma_start(
-                        out=o1_view[3, m][:, 512 * c : 512 * c + 512],
-                        in_=stages[m][:, 512 * c : 512 * c + 512],
-                    )
+            done = set()
+            heads = [0] * len(queues)
+            while len(done) < len(jobs):
+                before_round = len(done)
+                for q, queue in enumerate(queues):
+                    while heads[q] < len(queue) and all(n in done for n in needs(queue[heads[q]])):
+                        emit(queue[heads[q]])
+                        done.add(queue[heads[q]])
+                        heads[q] = heads[q] + 1
+                assert len(done) > before_round, [queue[h] if h < len(queue) else None for queue, h in zip(queues, heads)]

@@ -20,8 +20,8 @@ DEPTH = {"nat": 6, "gf": 4, "gw": 3, "ti": 3, "cf": 5, "ct": 9, "rot": 4, "acc":
 SORTED = ()
 RUN4 = 0
 SWARM = 0
-NW = 0
-NK = 0
+NW = 3
+NKS = (2, 1, 2, 1)
 
 
 def orders():
@@ -90,7 +90,7 @@ def orders():
 
     loads = [("L", "p")] + [("L", "g", 0, j) for j in range(4)] + LW(0) + LW(1) + [("L", "h", 0)] + LG(1) + LW(2) + [("L", "h", 1)] + LW(3)
     t0 = [("TF", 0, 0, c, jp) for jp in range(2) for c in range(2)]
-    pe = WU(0, NW) + t0[:2] + WU(1, NK) + t0[2:] + WU(2, NK) + [("TW", 0, 0, 0), ("TW", 0, 1, 0)] + WU(3, NK) + [("TW", 0, 0, 1), ("TW", 0, 1, 1)] + WU(4, NK) + TF(1, 0)
+    pe = WU(0, NW) + t0[:2] + WU(1, NKS[0]) + t0[2:] + WU(2, NKS[1]) + [("TW", 0, 0, 0), ("TW", 0, 1, 0)] + WU(3, NKS[2]) + [("TW", 0, 0, 1), ("TW", 0, 1, 1)] + WU(4, NKS[3]) + TF(1, 0)
     pe += X0(0, 0, 0) + TW(1, 0) + X0(0, 0, 1) + TW(1, 1) + TF(2, 0)
     pe += X0(1, 0, 0) + TW(2, 0) + X0(1, 0, 1) + TW(2, 1) + TF(3, 0)
     pe += X0(2, 0, 0) + TW(3, 0) + X0(2, 0, 1) + TW(3, 1) + TF(0, 1)

@@ -16,12 +16,12 @@ E, H, HO, T = 4, 512, 1024, 1024
 FLOPS = 2 * 2 * T * H * E * HO
 BYTES = 2 * (T * H + E * H * HO + T * HO) + 4 * T * E + 4 * (T * H + E * H * HO)
 
-DEPTH = {"nat": 6, "gf": 4, "gw": 3, "ti": 3, "cf": 5, "ct": 9, "rot": 4, "acc": 4, "st": 8, "ws": 2}
+DEPTH = {"wc": 4, "nat": 7, "gf": 4, "gw": 3, "ti": 4, "cf": 5, "ct": 8, "rot": 4, "acc": 4, "st": 8, "ws": 2}
 SORTED = ()
-RUN4 = 0
+RUN4 = 1
 SWARM = 0
 NW = 3
-NKS = (2, 1, 2, 1)
+NKS = (0, 2, 2, 0, 0)
 
 
 def orders():
@@ -88,24 +88,34 @@ def orders():
     def I2(e, g, c, u):
         return [("I2", e, g, c, u)]
 
-    loads = [("L", "p")] + [("L", "g", 0, j) for j in range(4)] + LW(0) + LW(1) + [("L", "h", 0)] + LG(1) + LW(2) + [("L", "h", 1)] + LW(3)
+    def E0(g, j):
+        return [("E0", g, j)]
+
+    def LC(e, c):
+        return [("L", "wc", e, c)]
+
+    loads = [("L", "p")] + [("L", "g", 0, j) for j in range(4)] + LC(0, 0) + LC(0, 1) + LC(1, 0) + [("L", "h", 0)] + LC(1, 1) + LG(1) + LC(2, 0) + LC(2, 1) + [("L", "h", 1)] + LC(3, 0) + LC(3, 1)
     t0 = [("TF", 0, 0, c, jp) for jp in range(2) for c in range(2)]
-    pe = WU(0, NW) + t0[:2] + WU(1, NKS[0]) + t0[2:] + WU(2, NKS[1]) + [("TW", 0, 0, 0), ("TW", 0, 1, 0)] + WU(3, NKS[2]) + [("TW", 0, 0, 1), ("TW", 0, 1, 1)] + WU(4, NKS[3]) + TF(1, 0)
-    pe += X0(0, 0, 0) + TW(1, 0) + X0(0, 0, 1) + TW(1, 1) + TF(2, 0)
-    pe += X0(1, 0, 0) + TW(2, 0) + X0(1, 0, 1) + TW(2, 1) + TF(3, 0)
-    pe += X0(2, 0, 0) + TW(3, 0) + X0(2, 0, 1) + TW(3, 1) + TF(0, 1)
-    pe += X1(0, 0) + X0(3, 0, 0) + TF(1, 1) + X1(0, 1) + X0(3, 0, 1)
-    pe += X1(1, 0) + X0(0, 1, 0) + X0(0, 1, 1) + TF(2, 1)
-    pe += X0(1, 1, 0) + X1(1, 1) + X0(1, 1, 1) + TF(3, 1)
-    pe += X0(2, 1, 0) + X1(2, 0) + X0(2, 1, 1) + X1(2, 1)
-    pe += X0(3, 1, 0)[:2] + X0(3, 1, 1)[:2] + X1(3, 0) + X0(3, 1, 0)[2:3] + X0(3, 1, 1)[2:3] + X0(3, 1, 0)[3:] + X0(3, 1, 1)[3:] + X1(3, 1)
-    vec = M(0, 0) + M(1, 0) + I(0, 0, 0) + QF(0, 0, 0) + QT(0, 0, 0) + QF(0, 0, 1) + QW(0, 0) + QW(0, 1) + M(2, 0) + I(0, 0, 1) + QF(1, 0, 0) + QT(0, 0, 1) + QF(1, 0, 1)
-    vec += QW(1, 0) + M(0, 1) + M(3, 0) + QW(1, 1) + I(0, 1, 0) + QF(2, 0, 0) + QT(0, 1, 0) + QF(2, 0, 1) + QW(2, 0) + I(0, 1, 1)
-    vec += M(1, 1) + QW(2, 1) + QT(0, 1, 1) + QH(0) + I(1, 0, 0) + QF(3, 0, 0) + QF(3, 0, 1) + QH(1) + QW(3, 0) + I(1, 1, 0) + QT(1, 0, 0) + QT(1, 1, 0)
-    vec += QW(3, 1) + M(2, 1) + I(1, 0, 1) + QF(0, 1, 0) + QF(0, 1, 1) + I(1, 1, 1) + QT(1, 0, 1) + QT(1, 1, 1) + M(3, 1)
-    vec += T(2, 0) + QF(1, 1, 0) + QF(1, 1, 1) + T(2, 1) + QF(2, 1, 0) + QF(2, 1, 1) + T(3, 0) + QF(3, 1, 0) + QF(3, 1, 1) + T(3, 1)
-    vec += [("E1", 3, 1, 1), ("E1", 3, 1, 3)]
-    act_extra = {("EW", 1, 0, 1): IH(0, 0), ("EF", 2, 0, 1, 1): IH(0, 1), ("EW", 2, 0, 1): IH(1, 0), ("EF", 3, 0, 1, 1): IH(1, 1)}
+    pe = WU(0, NW) + t0[:2] + WU(1, NKS[0]) + t0[2:] + WU(2, NKS[1]) + TW(0, 0) + WU(3, NKS[2]) + TW(0, 1) + WU(4, NKS[3]) + TF(1, 0)[:2] + WU(5, NKS[4])
+    pe += X0(0, 0, 0) + TW(1, 0) + TF(1, 0)[2:] + X0(0, 0, 1) + TW(1, 1) + TF(2, 0)[:2]
+    pe += X0(1, 0, 0) + TW(2, 0) + TF(2, 0)[2:] + X0(1, 0, 1) + TW(2, 1) + TF(3, 0)[:2]
+    pe += X0(2, 0, 0) + TW(3, 0) + TF(3, 0)[2:] + X0(2, 0, 1) + TW(3, 1) + TF(0, 1)[:2]
+    pe += X0(3, 0, 0) + X1(0, 0) + TF(0, 1)[2:] + TF(1, 1)[:2] + X1(0, 1) + X0(3, 0, 1)
+    pe += X1(1, 0) + X0(0, 1, 0) + X0(0, 1, 1) + X1(1, 1) + TF(1, 1)[2:] + TF(2, 1)[:2]
+    pe += X0(1, 1, 0) + X1(2, 0) + X0(1, 1, 1) + X1(2, 1) + TF(2, 1)[2:] + TF(3, 1)[:2]
+    pe += X0(2, 1, 0) + X1(3, 0) + TF(3, 1)[2:] + X0(2, 1, 1) + X1(3, 1)
+    pe += [("X0", 3, 1, c, j) for j in range(4) for c in range(2)]
+    vec = M(0, 0) + M(1, 0) + I(0, 0, 0) + QF(0, 0, 0) + QW(0, 0) + QF(0, 0, 1) + QT(0, 0, 0) + QW(0, 1) + M(2, 0) + QF(1, 0, 0) + I(0, 0, 1)
+    vec += QW(1, 0) + QT(0, 0, 1) + QF(1, 0, 1) + M(0, 1)
+    vec += QW(1, 1) + QF(2, 0, 0) + M(3, 0) + I(0, 1, 0)
+    vec += QW(2, 0) + QF(2, 0, 1) + QT(0, 1, 0) + I(0, 1, 1)
+    vec += QW(2, 1) + QF(3, 0, 0) + IH(1, 2) + IH(1, 3) + QT(0, 1, 1) + QH(0)
+    vec += QW(3, 0) + M(1, 1) + QH(1) + QF(3, 0, 1) + I(1, 0, 0)
+    vec += QW(3, 1) + QT(1, 0, 0) + I(1, 1, 0) + QF(0, 1, 0) + QT(1, 1, 0)
+    vec += I(1, 0, 1) + I(1, 1, 1) + QF(0, 1, 1) + QT(1, 0, 1) + QT(1, 1, 1) + M(2, 1) + QF(1, 1, 0)
+    vec += T(2, 0) + M(3, 1) + I(2, 0, 1) + QF(1, 1, 1) + I(2, 1, 1) + QT(2, 0, 1) + QT(2, 1, 1) + QF(2, 1, 0) + T(3, 0) + QF(2, 1, 1) + T(3, 1) + QF(3, 1, 0) + QF(3, 1, 1)
+    vec += [("E0", 1, 1), ("E0", 1, 3)]
+    act_extra = {("EF", 1, 0, 0, 1): IH(0, 0), ("EF", 1, 0, 1, 1): IH(0, 1), ("EF", 2, 0, 0, 1): IH(0, 2), ("EF", 2, 0, 1, 1): IH(0, 3), ("EF", 3, 0, 0, 1): IH(1, 0), ("EF", 3, 0, 1, 1): IH(1, 1)}
 
     return loads, pe, vec, act_extra
 
@@ -166,9 +176,13 @@ def tile_enhancedmathematicalreasoning_pa_v_kernel(
         k = job[0]
         if k == "M":
             return [g_piece(job[2], job[3]), ("p",)]
+        if k == "WU":
+            return [("g", 0, 0)]
         if k == "TF":
             return [("nat", job[1], job[2])]
         if k == "TW":
+            if ("L", "wc", job[1], job[2]) in loads:
+                return [("wc", job[1], job[2])]
             return [("ws" if job[1] in SORTED else "w", job[1], job[3])]
         if k == "SW":
             return [("w", job[1], job[2])]
@@ -217,12 +231,12 @@ def tile_enhancedmathematicalreasoning_pa_v_kernel(
     evacs = [evac_of(job) for job in pe if evac_of(job)]
     act = []
     for job in evacs:
-        if job not in vec:
+        if job not in vec and not any(job in x for x in act_extra.values()):
             act.append(job)
         act.extend(act_extra.get(job, []))
     act = act_extra.get("first", []) + act
     stores = [("S", 0 if job[0] == "E0" else 1) + job[1:] for job in evacs if job[0] in ("E0", "E1")]
-    queues = [loads + [("ID",)] + stores, pe, vec, act]
+    queues = [loads[:1] + [("ID",)] + loads[1:] + stores, pe, vec, act]
     jobs = [job for q in queues for job in q]
     assert len(set(jobs)) == len(jobs)
     writers, readers = {}, {}
@@ -232,7 +246,7 @@ def tile_enhancedmathematicalreasoning_pa_v_kernel(
         for b in reads(job):
             readers.setdefault(b, []).append(job)
     order_of = {}
-    for job in pe + [j for j in evacs] + [("I",) + j[1:] for j in vec if j[0] == "QT"] + vec + act:
+    for job in loads + pe + [j for j in evacs] + [("I",) + j[1:] for j in vec if j[0] == "QT"] + vec + act:
         for b in writes(job):
             if b[0] in DEPTH and b not in order_of.setdefault(b[0], []):
                 order_of[b[0]].append(b)
@@ -322,6 +336,8 @@ def tile_enhancedmathematicalreasoning_pa_v_kernel(
                     nc.sync.dma_start(out=buf(w, [P, HO], BF16)[:], in_=g_view[w[1], :, w[2] * HO : (w[2] + 1) * HO])
                 elif w[0] == "g2":
                     nc.sync.dma_start(out=buf(w, [P, 2 * HO], BF16)[:], in_=g_view[w[1], :, w[2] * 2 * HO : (w[2] + 1) * 2 * HO])
+                elif w[0] == "wc":
+                    nc.sync.dma_start(out=buf(w, [P, 2 * HO], BF16)[:].rearrange("p (a w) -> p a w", a=4), in_=w_view[w[1]].rearrange("p (a w) -> p a w", a=4)[:, :, w[2] * 512 : (w[2] + 1) * 512])
                 elif w[0] == "w":
                     nc.sync.dma_start(out=buf(w, [P, 2 * HO], BF16)[:], in_=w_view[w[1], :, w[2] * 2 * HO : (w[2] + 1) * 2 * HO])
                 else:
@@ -349,6 +365,8 @@ def tile_enhancedmathematicalreasoning_pa_v_kernel(
                         row = (2 * half + s if k == "TF" else s) * 512
                         if k == "TF" or job[1] in SORTED:
                             src = words[:, row + u * 256 + c * P : row + u * 256 + (c + 1) * P]
+                        elif r[0] == "wc":
+                            src = words[:, (2 * half + s) * 256 + u : (2 * half + s) * 256 + u + 255 : 2]
                         else:
                             src = words[:, row + c * 256 + u : row + c * 256 + u + 255 : 2]
                         nc.tensor.transpose(bank[:, (2 * s + u) * P : (2 * s + u + 1) * P], src, ident[:])
@@ -366,12 +384,13 @@ def tile_enhancedmathematicalreasoning_pa_v_kernel(
                 copy(job, *interleave_views(buf(w, [P, 2048], BF16)[:, u * 1024 : (u + 1) * 1024], src))
             elif k == "IH":
                 q = job[2]
-                src = get(r)[:].rearrange("p (j q u w) -> p q u w j", j=4, q=2, u=2)[:, q]
-                copy(job, *interleave_views(buf(w, [P, 2048], BF16)[:, q * 1024 : (q + 1) * 1024], src))
+                src = get(r)[:].rearrange("p (j q u w) -> p q u w j", j=4, q=4, u=2)[:, q]
+                copy(job, *interleave_views(buf(w, [P, 2048], BF16)[:, q * 512 : (q + 1) * 512], src))
             elif k == "WU":
                 if ("wu", "") not in tiles:
                     tiles["wu", ""] = ps.tile([P, 512], F32, name="acc3", tag="acc3")
-                nc.tensor.matmul(out=get("wu")[:, 0:P], lhsT=ident[:], rhs=ident[:], start=True, stop=True)
+                first = get(r)
+                nc.tensor.matmul(out=get("wu")[:], lhsT=first[:, 0:P], rhs=first[:, 0:512], start=True, stop=True)
             elif k in ("IM", "HM"):
                 u = job[-1]
                 bank = buf(w, [P, 1024], BF16, ps)

@@ -19,6 +19,7 @@ BYTES = 2 * (T * H + E * H * HO + T * HO) + 4 * T * E + 4 * (T * H + E * H * HO)
 DEPTH = {"wc": 4, "nat": 7, "gf": 4, "gw": 3, "ti": 4, "cf": 5, "ct": 8, "rot": 4, "acc": 4, "st": 8, "ws": 2}
 SORTED = ()
 RUN4 = 1
+LAST_PARTS = 2
 SWARM = 0
 NW = 3
 NKS = (0, 2, 2, 0, 0)
@@ -103,8 +104,8 @@ def orders():
     pe += X0(3, 0, 0) + X1(0, 0) + TF(0, 1)[2:] + TF(1, 1)[:2] + X1(0, 1) + X0(3, 0, 1)
     pe += X1(1, 0) + X0(0, 1, 0) + X0(0, 1, 1) + X1(1, 1) + TF(1, 1)[2:] + TF(2, 1)[:2]
     pe += X0(1, 1, 0) + X1(2, 0) + X0(1, 1, 1) + X1(2, 1) + TF(2, 1)[2:] + TF(3, 1)[:2]
-    pe += X0(2, 1, 0) + X1(3, 0) + TF(3, 1)[2:] + X0(2, 1, 1) + X1(3, 1)
-    pe += [("X0", 3, 1, c, j) for j in range(4) for c in range(2)]
+    pe += X0(2, 1, 0) + X1(3, 0) + TF(3, 1)[2:] + X1(3, 1)
+    pe += [("X0", e, 1, c, j) for j in range(4) for e, c in ((2, 1), (3, 0), (3, 1))]
     vec = M(0, 0) + M(1, 0) + I(0, 0, 0) + QF(0, 0, 0) + QW(0, 0) + QF(0, 0, 1) + QT(0, 0, 0) + QW(0, 1) + M(2, 0) + QF(1, 0, 0) + I(0, 0, 1)
     vec += QW(1, 0) + QT(0, 0, 1) + QF(1, 0, 1) + M(0, 1)
     vec += QW(1, 1) + QF(2, 0, 0) + M(3, 0) + I(0, 1, 0)
@@ -113,7 +114,7 @@ def orders():
     vec += QW(3, 0) + M(1, 1) + QH(1) + QF(3, 0, 1) + I(1, 0, 0)
     vec += QW(3, 1) + QT(1, 0, 0) + I(1, 1, 0) + QF(0, 1, 0) + QT(1, 1, 0)
     vec += I(1, 0, 1) + I(1, 1, 1) + QF(0, 1, 1) + QT(1, 0, 1) + QT(1, 1, 1) + M(2, 1) + QF(1, 1, 0)
-    vec += T(2, 0) + M(3, 1) + I(2, 0, 1) + QF(1, 1, 1) + I(2, 1, 1) + QT(2, 0, 1) + QT(2, 1, 1) + QF(2, 1, 0) + T(3, 0) + QF(2, 1, 1) + T(3, 1) + QF(3, 1, 0) + QF(3, 1, 1)
+    vec += T(2, 0) + M(3, 1) + I(2, 0, 1) + QF(1, 1, 1) + I(2, 1, 1) + QT(2, 0, 1) + QT(2, 1, 1) + QF(2, 1, 0) + T(3, 0) + T(3, 1) + QF(2, 1, 1) + QF(3, 1, 0) + QF(3, 1, 1)
     vec += [("E0", 1, 1), ("E0", 1, 3)]
     act_extra = {("EF", 1, 0, 0, 1): IH(0, 0), ("EF", 1, 0, 1, 1): IH(0, 1), ("EF", 2, 0, 0, 1): IH(0, 2), ("EF", 2, 0, 1, 1): IH(0, 3), ("EF", 3, 0, 0, 1): IH(1, 0), ("EF", 3, 0, 1, 1): IH(1, 1)}
 
@@ -145,7 +146,7 @@ def tile_enhancedmathematicalreasoning_pa_v_kernel(
             return [("gw", job[1], job[2])]
         if k == "SW":
             return [("ws", job[1], job[2])]
-        if k in ("I", "EI", "I2"):
+        if k in ("I", "EI", "I2", "I4"):
             return [("ti", job[1], job[2], job[3])]
         if k in ("IH", "EH"):
             return [("gh", job[1])]
@@ -177,16 +178,16 @@ def tile_enhancedmathematicalreasoning_pa_v_kernel(
         if k == "M":
             return [g_piece(job[2], job[3]), ("p",)]
         if k == "WU":
-            return [("g", 0, 0)]
+            return [loads[1][1:]]
         if k == "TF":
             return [("nat", job[1], job[2])]
         if k == "TW":
-            if ("L", "wc", job[1], job[2]) in loads:
-                return [("wc", job[1], job[2])]
-            return [("ws" if job[1] in SORTED else "w", job[1], job[3])]
+            if ("L", "wh") + job[1:] in loads:
+                return [("wh",) + job[1:]]
+            return [("ws" if job[1] in SORTED else "wc", job[1], job[2])]
         if k == "SW":
-            return [("w", job[1], job[2])]
-        if k in ("I", "IM", "I2"):
+            return [("wc", job[1], job[2])]
+        if k in ("I", "IM", "I2", "I4"):
             return [("nat", job[1], job[2])]
         if k in ("IH", "HM"):
             return [("h", job[1])]
@@ -336,6 +337,8 @@ def tile_enhancedmathematicalreasoning_pa_v_kernel(
                     nc.sync.dma_start(out=buf(w, [P, HO], BF16)[:], in_=g_view[w[1], :, w[2] * HO : (w[2] + 1) * HO])
                 elif w[0] == "g2":
                     nc.sync.dma_start(out=buf(w, [P, 2 * HO], BF16)[:], in_=g_view[w[1], :, w[2] * 2 * HO : (w[2] + 1) * 2 * HO])
+                elif w[0] == "wh":
+                    nc.sync.dma_start(out=buf(w, [P, HO], BF16)[:].rearrange("p (a w) -> p a w", a=2), in_=w_view[w[1]].rearrange("p (a w) -> p a w", a=4)[:, 2 * w[3] : 2 * w[3] + 2, w[2] * 512 : (w[2] + 1) * 512])
                 elif w[0] == "wc":
                     nc.sync.dma_start(out=buf(w, [P, 2 * HO], BF16)[:].rearrange("p (a w) -> p a w", a=4), in_=w_view[w[1]].rearrange("p (a w) -> p a w", a=4)[:, :, w[2] * 512 : (w[2] + 1) * 512])
                 elif w[0] == "w":
@@ -354,21 +357,21 @@ def tile_enhancedmathematicalreasoning_pa_v_kernel(
                     op0=MULT,
                 )
             elif k == "SW":
-                copy(job, buf(w, [P, 2 * HO], BF16)[:].rearrange("p (a u w x) -> p a u w x", a=2, u=2, x=16),
-                     get(r)[:].rearrange("p (a w u x) -> p a u w x", a=2, u=2, x=16))
+                copy(job, buf(w, [P, 2 * HO], BF16)[:].rearrange("p (a u w x) -> p a u w x", a=4, u=2, x=16),
+                     get(r)[:].rearrange("p (a w u x) -> p a u w x", a=4, u=2, x=16))
             elif k in ("TF", "TW"):
                 c, half = job[-2:]
                 bank = buf(w, [P, 512], F32, ps)
                 words = get(r)[:].bitcast(F32)
                 for s in range(2):
                     for u in range(2):
-                        row = (2 * half + s if k == "TF" else s) * 512
-                        if k == "TF" or job[1] in SORTED:
-                            src = words[:, row + u * 256 + c * P : row + u * 256 + (c + 1) * P]
-                        elif r[0] == "wc":
-                            src = words[:, (2 * half + s) * 256 + u : (2 * half + s) * 256 + u + 255 : 2]
+                        row = s if r[0] == "wh" else 2 * half + s
+                        if k == "TF":
+                            src = words[:, row * 512 + u * 256 + c * P : row * 512 + u * 256 + (c + 1) * P]
+                        elif job[1] in SORTED:
+                            src = words[:, row * 256 + u * P : row * 256 + (u + 1) * P]
                         else:
-                            src = words[:, row + c * 256 + u : row + c * 256 + u + 255 : 2]
+                            src = words[:, row * 256 + u : row * 256 + u + 255 : 2]
                         nc.tensor.transpose(bank[:, (2 * s + u) * P : (2 * s + u + 1) * P], src, ident[:])
             elif k in ("EF", "EW"):
                 half = job[-1]
@@ -382,6 +385,10 @@ def tile_enhancedmathematicalreasoning_pa_v_kernel(
                 c, u = job[3:]
                 src = get(r)[:].rearrange("p (j u c q w) -> p c u q w j", j=4, u=2, c=2, q=2)[:, c, u]
                 copy(job, *interleave_views(buf(w, [P, 2048], BF16)[:, u * 1024 : (u + 1) * 1024], src))
+            elif k == "I4":
+                c, n = job[3:]
+                src = get(r)[:].rearrange("p (j u c h q w) -> p c u h q w j", j=4, u=2, c=2, h=2, q=2)[:, c, n // 2, n % 2]
+                copy(job, *interleave_views(buf(w, [P, 2048], BF16)[:, n * 512 : (n + 1) * 512], src))
             elif k == "IH":
                 q = job[2]
                 src = get(r)[:].rearrange("p (j q u w) -> p q u w j", j=4, q=4, u=2)[:, q]
@@ -414,7 +421,10 @@ def tile_enhancedmathematicalreasoning_pa_v_kernel(
                 e, c, m, g = job[1:]
                 mx(buf(w, [P, 512], F32, ps)[:], ("ch", g), P * m, E4M3, r, E5M2, g == 0, g == 1)
             elif k == "E0":
-                copy(job, buf(w, [P, 512], F32)[:].rearrange("p (r a) -> p r a", a=4), get(r)[:].rearrange("p (a r) -> p r a", a=4))
+                parts = LAST_PARTS if job == evacs[-1] else 1
+                for n in range(parts):
+                    rows = slice(n * P // parts, (n + 1) * P // parts)
+                    copy(job, buf(w, [P, 512], F32)[:].rearrange("p (r a) -> p r a", a=4)[:, rows], get(r)[:].rearrange("p (a r) -> p r a", a=4)[:, rows])
             elif k == "E1":
                 x = run_len(job[1])
                 copy(job, buf(w, [P, 512], F32)[:].rearrange("p (w u x) -> p w u x", u=2, x=x), get(r)[:].rearrange("p (u w x) -> p w u x", u=2, x=x))
@@ -423,7 +433,10 @@ def tile_enhancedmathematicalreasoning_pa_v_kernel(
                     dst = o0_view[job[2], job[3]]
                 else:
                     dst = o1_view[job[2], job[4]][:, job[3] * 512 : (job[3] + 1) * 512]
-                nc.sync.dma_start(out=dst, in_=get(r)[:])
+                parts = LAST_PARTS if job == stores[-1] else 1
+                for n in range(parts):
+                    cols = slice(n * 512 // parts, (n + 1) * 512 // parts)
+                    nc.sync.dma_start(out=dst[:, cols], in_=get(r)[:, cols])
 
         with tc.manual_schedule():
             done = set()

@@ -22,7 +22,7 @@ RUN4 = 1
 LAST_PARTS = 2
 SWARM = 0
 NW = 3
-NKS = (0, 2, 2, 0, 0)
+NKS = (1, 1, 1, 0, 0)
 
 
 def orders():
@@ -101,22 +101,22 @@ def orders():
     pe += X0(0, 0, 0) + TW(1, 0) + TF(1, 0)[2:] + X0(0, 0, 1) + TW(1, 1) + TF(2, 0)[:2]
     pe += X0(1, 0, 0) + TW(2, 0) + TF(2, 0)[2:] + X0(1, 0, 1) + TW(2, 1) + TF(3, 0)[:2]
     pe += X0(2, 0, 0) + TW(3, 0) + TF(3, 0)[2:] + X0(2, 0, 1) + TW(3, 1) + TF(0, 1)[:2]
-    pe += X0(3, 0, 0) + X1(0, 0) + TF(0, 1)[2:] + TF(1, 1)[:2] + X1(0, 1) + X0(3, 0, 1)
-    pe += X1(1, 0) + X0(0, 1, 0) + X0(0, 1, 1) + X1(1, 1) + TF(1, 1)[2:] + TF(2, 1)[:2]
-    pe += X0(1, 1, 0) + X1(2, 0) + X0(1, 1, 1) + X1(2, 1) + TF(2, 1)[2:] + TF(3, 1)[:2]
-    pe += X0(2, 1, 0) + X1(3, 0) + TF(3, 1)[2:] + X1(3, 1)
+    pe += X0(3, 0, 0)[:2] + X1(0, 0) + X0(3, 0, 0)[2:] + TF(0, 1)[2:] + TF(1, 1)[:2] + X0(3, 0, 1)[:2] + X1(0, 1) + X0(3, 0, 1)[2:]
+    pe += X1(1, 0) + X0(0, 1, 0) + X1(1, 1) + X0(0, 1, 1)[:2] + TF(1, 1)[2:] + TF(2, 1)[:2] + X0(0, 1, 1)[2:]
+    pe += X1(2, 0) + X0(1, 1, 0) + X1(2, 1) + X0(1, 1, 1)[:2] + TF(2, 1)[2:] + TF(3, 1)[:2] + X0(1, 1, 1)[2:]
+    pe += X1(3, 0) + X0(2, 1, 0)[:2] + TF(3, 1)[2:] + X0(2, 1, 0)[2:] + X1(3, 1)
     pe += [("X0", e, 1, c, j) for j in range(4) for e, c in ((2, 1), (3, 0), (3, 1))]
-    vec = M(0, 0) + M(1, 0) + I(0, 0, 0) + QF(0, 0, 0) + QW(0, 0) + QF(0, 0, 1) + QT(0, 0, 0) + QW(0, 1) + M(2, 0) + QF(1, 0, 0) + I(0, 0, 1)
+    vec = M(0, 0) + M(1, 0) + I(0, 0, 0) + QF(0, 0, 0) + QT(0, 0, 0) + QW(0, 0) + QF(0, 0, 1) + QW(0, 1) + M(2, 0) + QF(1, 0, 0) + I(0, 0, 1)
     vec += QW(1, 0) + QT(0, 0, 1) + QF(1, 0, 1) + M(0, 1)
     vec += QW(1, 1) + QF(2, 0, 0) + M(3, 0) + I(0, 1, 0)
     vec += QW(2, 0) + QF(2, 0, 1) + QT(0, 1, 0) + I(0, 1, 1)
     vec += QW(2, 1) + QF(3, 0, 0) + IH(1, 2) + IH(1, 3) + QT(0, 1, 1) + QH(0)
-    vec += QW(3, 0) + M(1, 1) + QH(1) + QF(3, 0, 1) + I(1, 0, 0)
-    vec += QW(3, 1) + QT(1, 0, 0) + I(1, 1, 0) + QF(0, 1, 0) + QT(1, 1, 0)
-    vec += I(1, 0, 1) + I(1, 1, 1) + QF(0, 1, 1) + QT(1, 0, 1) + QT(1, 1, 1) + M(2, 1) + QF(1, 1, 0)
-    vec += T(2, 0) + M(3, 1) + I(2, 0, 1) + QF(1, 1, 1) + I(2, 1, 1) + QT(2, 0, 1) + QT(2, 1, 1) + QF(2, 1, 0) + T(3, 0) + T(3, 1) + QF(2, 1, 1) + QF(3, 1, 0) + QF(3, 1, 1)
+    vec += QW(3, 0) + QH(1) + M(1, 1) + QF(3, 0, 1) + QW(3, 1)
+    vec += T(1, 0) + QF(0, 1, 0) + T(1, 1) + QF(0, 1, 1) + M(2, 1)
+    vec += T(2, 0) + QF(1, 1, 0) + T(2, 1) + QF(1, 1, 1) + M(3, 1)
+    vec += I2(3, 0, 0, 1) + I(3, 1, 0) + QT(3, 0, 0) + QT(3, 1, 0) + QF(2, 1, 0) + T(3, 1) + QF(2, 1, 1) + QF(3, 1, 0) + QF(3, 1, 1)
     vec += [("E0", 1, 1), ("E0", 1, 3)]
-    act_extra = {("EF", 1, 0, 0, 1): IH(0, 0), ("EF", 1, 0, 1, 1): IH(0, 1), ("EF", 2, 0, 0, 1): IH(0, 2), ("EF", 2, 0, 1, 1): IH(0, 3), ("EF", 3, 0, 0, 1): IH(1, 0), ("EF", 3, 0, 1, 1): IH(1, 1)}
+    act_extra = {("E1", 2, 0, 3): [("I2", 3, 0, 0, 0)], ("EF", 1, 0, 0, 1): IH(0, 0), ("EF", 1, 0, 1, 1): IH(0, 1), ("EF", 2, 0, 0, 1): IH(0, 2), ("EF", 2, 0, 1, 1): IH(0, 3), ("EF", 3, 0, 0, 1): IH(1, 0), ("EF", 3, 0, 1, 1): IH(1, 1)}
 
     return loads, pe, vec, act_extra
 

@@ -20,8 +20,9 @@ DEPTH = {"wc": 4, "nat": 7, "gf": 4, "gw": 3, "ti": 4, "cf": 5, "ct": 8, "rot": 
 SORTED = ()
 RUN4 = 1
 LAST_PARTS = 2
+EARLY = 1
 SWARM = 0
-NW = 3
+NW = 6
 NKS = (1, 1, 1, 0, 0)
 
 
@@ -95,9 +96,9 @@ def orders():
     def LC(e, c):
         return [("L", "wc", e, c)]
 
-    loads = [("L", "p")] + [("L", "g", 0, j) for j in range(4)] + LC(0, 0) + LC(0, 1) + LC(1, 0) + [("L", "h", 0)] + LC(1, 1) + LG(1) + LC(2, 0) + LC(2, 1) + [("L", "h", 1)] + LC(3, 0) + LC(3, 1)
+    loads = [("L", "p")] + [("L", "g", 0, j) for j in range(2)] + LC(0, 0) + [("L", "g", 0, j) for j in range(2, 4)] + LC(0, 1) + LC(1, 0) + [("L", "h", 0)] + LC(1, 1) + LG(1) + LC(2, 0) + LC(2, 1) + [("L", "h", 1)] + LC(3, 0) + LC(3, 1)
     t0 = [("TF", 0, 0, c, jp) for jp in range(2) for c in range(2)]
-    pe = WU(0, NW) + t0[:2] + WU(1, NKS[0]) + t0[2:] + WU(2, NKS[1]) + TW(0, 0) + WU(3, NKS[2]) + TW(0, 1) + WU(4, NKS[3]) + TF(1, 0)[:2] + WU(5, NKS[4])
+    pe = WU(0, NW) + t0[:2] + WU(1, NKS[0]) + TW(0, 0) + WU(2, NKS[1]) + t0[2:] + WU(3, NKS[2]) + TW(0, 1) + WU(4, NKS[3]) + TF(1, 0)[:2]
     pe += X0(0, 0, 0) + TW(1, 0) + TF(1, 0)[2:] + X0(0, 0, 1) + TW(1, 1) + TF(2, 0)[:2]
     pe += X0(1, 0, 0) + TW(2, 0) + TF(2, 0)[2:] + X0(1, 0, 1) + TW(2, 1) + TF(3, 0)[:2]
     pe += X0(2, 0, 0) + TW(3, 0) + TF(3, 0)[2:] + X0(2, 0, 1) + TW(3, 1) + TF(0, 1)[:2]
@@ -106,9 +107,9 @@ def orders():
     pe += X1(2, 0) + X0(1, 1, 0) + X1(2, 1) + X0(1, 1, 1)[:2] + TF(2, 1)[2:] + TF(3, 1)[:2] + X0(1, 1, 1)[2:]
     pe += X1(3, 0) + X0(2, 1, 0)[:2] + TF(3, 1)[2:] + X0(2, 1, 0)[2:] + X1(3, 1)
     pe += [("X0", e, 1, c, j) for j in range(4) for e, c in ((2, 1), (3, 0), (3, 1))]
-    vec = M(0, 0) + M(1, 0) + I(0, 0, 0) + QF(0, 0, 0) + QT(0, 0, 0) + QW(0, 0) + QF(0, 0, 1) + QW(0, 1) + M(2, 0) + QF(1, 0, 0) + I(0, 0, 1)
+    vec = M(0, 0)[:2] + M(1, 0)[:2] + M(2, 0)[:2] + M(3, 0)[:2] + M(0, 0)[2:] + M(1, 0)[2:] + QW(0, 0) + QF(0, 0, 0) + QF(0, 0, 1) + I(0, 0, 0) + QW(0, 1) + M(2, 0)[2:] + QT(0, 0, 0) + QF(1, 0, 0) + I(0, 0, 1)
     vec += QW(1, 0) + QT(0, 0, 1) + QF(1, 0, 1) + M(0, 1)
-    vec += QW(1, 1) + QF(2, 0, 0) + M(3, 0) + I(0, 1, 0)
+    vec += QW(1, 1) + QF(2, 0, 0) + M(3, 0)[2:] + I(0, 1, 0)
     vec += QW(2, 0) + QF(2, 0, 1) + QT(0, 1, 0) + I(0, 1, 1)
     vec += QW(2, 1) + QF(3, 0, 0) + IH(1, 2) + IH(1, 3) + QT(0, 1, 1) + QH(0)
     vec += QW(3, 0) + QH(1) + M(1, 1) + QF(3, 0, 1) + QW(3, 1)
@@ -116,7 +117,7 @@ def orders():
     vec += T(2, 0) + QF(1, 1, 0) + T(2, 1) + QF(1, 1, 1) + M(3, 1)
     vec += I2(3, 0, 0, 1) + I(3, 1, 0) + QT(3, 0, 0) + QT(3, 1, 0) + QF(2, 1, 0) + T(3, 1) + QF(2, 1, 1) + QF(3, 1, 0) + QF(3, 1, 1)
     vec += [("E0", 1, 1), ("E0", 1, 3)]
-    act_extra = {("E1", 2, 0, 3): [("I2", 3, 0, 0, 0)], ("EF", 1, 0, 0, 1): IH(0, 0), ("EF", 1, 0, 1, 1): IH(0, 1), ("EF", 2, 0, 0, 1): IH(0, 2), ("EF", 2, 0, 1, 1): IH(0, 3), ("EF", 3, 0, 0, 1): IH(1, 0), ("EF", 3, 0, 1, 1): IH(1, 1)}
+    act_extra = {("E1", 0, 1, 3): E0(0, 0) + E0(0, 1), ("E1", 2, 0, 3): [("I2", 3, 0, 0, 0)], ("EF", 1, 0, 0, 1): IH(0, 0), ("EF", 1, 0, 1, 1): IH(0, 1), ("EF", 2, 0, 0, 1): IH(0, 2), ("EF", 2, 0, 1, 1): IH(0, 3), ("EF", 3, 0, 0, 1): IH(1, 0), ("EF", 3, 0, 1, 1): IH(1, 1)}
 
     return loads, pe, vec, act_extra
 
@@ -236,6 +237,8 @@ def tile_enhancedmathematicalreasoning_pa_v_kernel(
             act.append(job)
         act.extend(act_extra.get(job, []))
     act = act_extra.get("first", []) + act
+    moved = [x for extra in act_extra.values() for x in extra if x in evacs]
+    evacs = [x for job in evacs if job not in moved for x in [job] + [y for y in act_extra.get(job, []) if y in moved]]
     stores = [("S", 0 if job[0] == "E0" else 1) + job[1:] for job in evacs if job[0] in ("E0", "E1")]
     queues = [loads[:1] + [("ID",)] + loads[1:] + stores, pe, vec, act]
     jobs = [job for q in queues for job in q]
@@ -397,6 +400,10 @@ def tile_enhancedmathematicalreasoning_pa_v_kernel(
                 if ("wu", "") not in tiles:
                     tiles["wu", ""] = ps.tile([P, 512], F32, name="acc3", tag="acc3")
                 first = get(r)
+                if job[1] == 0 and EARLY:
+                    halves = ident[:].bitcast(BF16)
+                    nc.tensor.matmul(out=get("wu")[:], lhsT=halves[:, 0:P], rhs=halves.unsqueeze(1).to_broadcast([P, 2, 2 * P]), start=True, stop=True)
+                    return
                 nc.tensor.matmul(out=get("wu")[:], lhsT=first[:, 0:P], rhs=first[:, 0:512], start=True, stop=True)
             elif k in ("IM", "HM"):
                 u = job[-1]

@@ -16,11 +16,12 @@ E, H, HO, T = 4, 512, 1024, 1024
 FLOPS = 2 * 2 * T * H * E * HO
 BYTES = 2 * (T * H + E * H * HO + T * HO) + 4 * T * E + 4 * (T * H + E * H * HO)
 
-DEPTH = {"wc": 4, "nat": 7, "gf": 4, "gw": 3, "ti": 4, "cf": 5, "ct": 8, "rot": 4, "acc": 4, "st": 8, "ws": 2}
+DEPTH = {"wc": 4, "nat": 7, "gf": 4, "gw": 3, "ti": 2, "cf": 5, "ct": 4, "rot": 4, "acc": 4, "st": 8, "ws": 2}
 SORTED = ()
 RUN4 = 1
 LAST_PARTS = 2
 EARLY = 1
+ALIGN = 64
 SWARM = 0
 NW = 6
 NKS = (1, 1, 1, 0, 0)
@@ -107,17 +108,17 @@ def orders():
     pe += X1(2, 0) + X0(1, 1, 0) + X1(2, 1) + X0(1, 1, 1)[:2] + TF(2, 1)[2:] + TF(3, 1)[:2] + X0(1, 1, 1)[2:]
     pe += X1(3, 0) + X0(2, 1, 0)[:2] + TF(3, 1)[2:] + X0(2, 1, 0)[2:] + X1(3, 1)
     pe += [("X0", e, 1, c, j) for j in range(4) for e, c in ((2, 1), (3, 0), (3, 1))]
-    vec = M(0, 0)[:2] + M(1, 0)[:2] + M(2, 0)[:2] + M(3, 0)[:2] + M(0, 0)[2:] + M(1, 0)[2:] + QW(0, 0) + QF(0, 0, 0) + QF(0, 0, 1) + I(0, 0, 0) + QW(0, 1) + M(2, 0)[2:] + QT(0, 0, 0) + QF(1, 0, 0) + I(0, 0, 1)
+    vec = M(0, 0)[:2] + M(1, 0)[:2] + M(2, 0)[:2] + M(3, 0)[:2] + M(0, 0)[2:] + M(1, 0)[2:] + M(2, 0)[2:] + QW(0, 0) + QF(0, 0, 0) + QF(0, 0, 1) + I(0, 0, 0) + QW(0, 1) + QT(0, 0, 0) + QF(1, 0, 0) + I(0, 0, 1)
     vec += QW(1, 0) + QT(0, 0, 1) + QF(1, 0, 1) + M(0, 1)
     vec += QW(1, 1) + QF(2, 0, 0) + M(3, 0)[2:] + I(0, 1, 0)
     vec += QW(2, 0) + QF(2, 0, 1) + QT(0, 1, 0) + I(0, 1, 1)
-    vec += QW(2, 1) + QF(3, 0, 0) + IH(1, 2) + IH(1, 3) + QT(0, 1, 1) + QH(0)
-    vec += QW(3, 0) + QH(1) + M(1, 1) + QF(3, 0, 1) + QW(3, 1)
-    vec += T(1, 0) + QF(0, 1, 0) + T(1, 1) + QF(0, 1, 1) + M(2, 1)
+    vec += QW(2, 1) + QF(3, 0, 0) + IH(1, 3) + QT(0, 1, 1) + QH(0)
+    vec += QW(3, 0) + QH(1) + M(1, 1) + QF(3, 0, 1) + I(1, 0, 0) + QW(3, 1)
+    vec += QT(1, 0, 0) + I(1, 1, 0) + QF(0, 1, 0) + QT(1, 1, 0) + T(1, 1) + QF(0, 1, 1) + M(2, 1)
     vec += T(2, 0) + QF(1, 1, 0) + T(2, 1) + QF(1, 1, 1) + M(3, 1)
     vec += I2(3, 0, 0, 1) + I(3, 1, 0) + QT(3, 0, 0) + QT(3, 1, 0) + QF(2, 1, 0) + T(3, 1) + QF(2, 1, 1) + QF(3, 1, 0) + QF(3, 1, 1)
     vec += [("E0", 1, 1), ("E0", 1, 3)]
-    act_extra = {("E1", 0, 1, 3): E0(0, 0) + E0(0, 1), ("E1", 2, 0, 3): [("I2", 3, 0, 0, 0)], ("EF", 1, 0, 0, 1): IH(0, 0), ("EF", 1, 0, 1, 1): IH(0, 1), ("EF", 2, 0, 0, 1): IH(0, 2), ("EF", 2, 0, 1, 1): IH(0, 3), ("EF", 3, 0, 0, 1): IH(1, 0), ("EF", 3, 0, 1, 1): IH(1, 1)}
+    act_extra = {("E1", 0, 1, 3): E0(0, 0) + E0(0, 1), ("E1", 2, 0, 3): [("I2", 3, 0, 0, 0)], ("EF", 1, 0, 0, 1): IH(0, 0), ("EF", 1, 0, 1, 1): IH(0, 1) + IH(0, 2), ("EF", 2, 0, 0, 1): IH(0, 3), ("EF", 2, 0, 1, 1): IH(1, 0) + IH(1, 1), ("EF", 3, 0, 0, 1): IH(1, 2)}
 
     return loads, pe, vec, act_extra
 
@@ -128,7 +129,7 @@ def tile_enhancedmathematicalreasoning_pa_v_kernel(
     nc = tc.nc
     h_view = hidden_states.flatten_outer_dims().rearrange("(g p j) w -> g p (j w)", g=2, j=4)
     g_view = grad_out.flatten_outer_dims().rearrange("(g p j) w -> g p (j w)", g=2, j=4)
-    w_view = We.rearrange("e (p a) w -> e p (a w)", a=4)
+    w_view = We.rearrange("e (a p) w -> e p a w", a=4)
     p_view = op_w.flatten_outer_dims().rearrange("(g p j) e -> p g (j e)", g=2, j=4)
     o0_view = out_0.flatten_outer_dims().rearrange("(g p j) w -> g j p w", g=2, j=4)
     o1_view = out_1.rearrange("e (m p) w -> e m p w", p=P)
@@ -148,13 +149,13 @@ def tile_enhancedmathematicalreasoning_pa_v_kernel(
         if k == "SW":
             return [("ws", job[1], job[2])]
         if k in ("I", "EI", "I2", "I4"):
-            return [("ti", job[1], job[2], job[3])]
+            return [("ti", job[1], job[3])]
         if k in ("IH", "EH"):
             return [("gh", job[1])]
         if k == "QF":
             return [("cf",) + job[1:]]
         if k == "QT":
-            return [("ct",) + job[1:]]
+            return [("ct", job[1], job[3])]
         if k == "QW":
             return [("cw",) + job[1:]]
         if k == "QH":
@@ -203,7 +204,7 @@ def tile_enhancedmathematicalreasoning_pa_v_kernel(
         if k == "QF":
             return [("gf",) + job[1:]]
         if k == "QT":
-            return [("ti",) + job[1:]]
+            return [("ti", job[1], job[3])]
         if k == "QW":
             return [("gw",) + job[1:]]
         if k == "QH":
@@ -211,7 +212,7 @@ def tile_enhancedmathematicalreasoning_pa_v_kernel(
         if k == "X0":
             return [("cf", job[1], job[2], job[3]), ("cw", job[1], job[3])]
         if k == "X1":
-            return [("ct", job[1], job[4], job[2]), ("ch", job[4])]
+            return [("ct", job[1], job[2]), ("ch", job[4])]
         if k == "E0":
             return [("acc", job[1], job[2])]
         if k == "E1":
@@ -267,6 +268,10 @@ def tile_enhancedmathematicalreasoning_pa_v_kernel(
             ws = writers[b]
             if job[0] == "TF":
                 ws = [w for w in ws if w[3] // 2 == job[4]]
+            if job[0] == "QT" and job[2] != 2:
+                ws = [w for w in ws if w[2] == job[2]]
+            if job[0] == "X1" and b[0] == "ct":
+                ws = [w for w in ws if w[2] in (job[4], 2)]
             out.extend(ws)
         for b in writes(job):
             if b in before:
@@ -282,7 +287,7 @@ def tile_enhancedmathematicalreasoning_pa_v_kernel(
             if (b, part) not in tiles:
                 tag = f"{b[0]}{part}{slot[b]}" if b in slot else "_".join(str(x) for x in b) + part
                 if pool is sb:
-                    tiles[b, part] = pool.tile(shape, dtype, name=tag, tag=tag, align_bytes=64)
+                    tiles[b, part] = pool.tile(shape, dtype, name=tag, tag=tag, align_bytes=ALIGN)
                 else:
                     tiles[b, part] = pool.tile(shape, dtype, name=tag, tag=tag)
             return tiles[b, part]
@@ -307,13 +312,13 @@ def tile_enhancedmathematicalreasoning_pa_v_kernel(
             scales = buf(dst, [P, 512], U8, part="s")
             nc.vector.quantize_mx(out=codes[:].bitcast(fmt), scales=scales[:], in_=get(src)[:])
 
-        def mx(out, lhs, l0, lfmt, rhs, rfmt, start, stop):
+        def mx(out, lhs, l0, lfmt, rhs, rfmt, start, stop, r0=0):
             nc.tensor.matmul_mx(
                 out=out,
                 lhsT=get(lhs)[:, l0 : l0 + P].bitcast(lfmt),
                 lhsT_scale=get(lhs, "s")[:, l0 : l0 + P],
-                rhs=get(rhs)[:].bitcast(rfmt),
-                rhs_scale=get(rhs, "s")[:],
+                rhs=get(rhs)[:, r0 : r0 + 512].bitcast(rfmt),
+                rhs_scale=get(rhs, "s")[:, r0 : r0 + 512],
                 start=start,
                 stop=stop,
             )
@@ -343,7 +348,7 @@ def tile_enhancedmathematicalreasoning_pa_v_kernel(
                 elif w[0] == "wh":
                     nc.sync.dma_start(out=buf(w, [P, HO], BF16)[:].rearrange("p (a w) -> p a w", a=2), in_=w_view[w[1]].rearrange("p (a w) -> p a w", a=4)[:, 2 * w[3] : 2 * w[3] + 2, w[2] * 512 : (w[2] + 1) * 512])
                 elif w[0] == "wc":
-                    nc.sync.dma_start(out=buf(w, [P, 2 * HO], BF16)[:].rearrange("p (a w) -> p a w", a=4), in_=w_view[w[1]].rearrange("p (a w) -> p a w", a=4)[:, :, w[2] * 512 : (w[2] + 1) * 512])
+                    nc.sync.dma_start(out=buf(w, [P, 2 * HO], BF16)[:].rearrange("p (a w) -> p a w", a=4), in_=w_view[w[1]][:, :, w[2] * 512 : (w[2] + 1) * 512])
                 elif w[0] == "w":
                     nc.sync.dma_start(out=buf(w, [P, 2 * HO], BF16)[:], in_=w_view[w[1], :, w[2] * 2 * HO : (w[2] + 1) * 2 * HO])
                 else:
@@ -383,11 +388,11 @@ def tile_enhancedmathematicalreasoning_pa_v_kernel(
             elif k == "I":
                 c = job[3]
                 src = get(r)[:].rearrange("p (j u c w) -> p c u w j", j=4, u=2, c=2)[:, c]
-                copy(job, *interleave_views(buf(w, [P, 2048], BF16)[:], src))
+                copy(job, *interleave_views(buf(w, [P, 4096], BF16)[:, job[2] * 2048 : (job[2] + 1) * 2048], src))
             elif k == "I2":
                 c, u = job[3:]
                 src = get(r)[:].rearrange("p (j u c q w) -> p c u q w j", j=4, u=2, c=2, q=2)[:, c, u]
-                copy(job, *interleave_views(buf(w, [P, 2048], BF16)[:, u * 1024 : (u + 1) * 1024], src))
+                copy(job, *interleave_views(buf(w, [P, 4096], BF16)[:, job[2] * 2048 + u * 1024 : job[2] * 2048 + (u + 1) * 1024], src))
             elif k == "I4":
                 c, n = job[3:]
                 src = get(r)[:].rearrange("p (j u c h q w) -> p c u h q w j", j=4, u=2, c=2, h=2, q=2)[:, c, n // 2, n % 2]
@@ -417,7 +422,12 @@ def tile_enhancedmathematicalreasoning_pa_v_kernel(
             elif k in ("EI", "EH"):
                 u = job[-1]
                 copy(job, buf(w, [P, 2048], BF16)[:, u * 1024 : (u + 1) * 1024], get(r)[:])
-            elif k in ("QF", "QT"):
+            elif k == "QT":
+                lo, hi = (0, 1024) if job[2] == 2 else (job[2] * 512, (job[2] + 1) * 512)
+                codes = buf(w, [P, 1024], U32)
+                scales = buf(w, [P, 1024], U8, part="s")
+                nc.vector.quantize_mx(out=codes[:, lo:hi].bitcast(E5M2), scales=scales[:, lo:hi], in_=get(r)[:, 4 * lo : 4 * hi])
+            elif k == "QF":
                 quant(w, r, E5M2)
             elif k in ("QW", "QH"):
                 quant(w, r, E4M3)
@@ -426,12 +436,12 @@ def tile_enhancedmathematicalreasoning_pa_v_kernel(
                 mx(buf(w, [P, 512], F32, ps)[:], r, P * j, E5M2, ("cw", e, c), E4M3, e == 0 and c == 0, e == 3 and c == 1)
             elif k == "X1":
                 e, c, m, g = job[1:]
-                mx(buf(w, [P, 512], F32, ps)[:], ("ch", g), P * m, E4M3, r, E5M2, g == 0, g == 1)
+                mx(buf(w, [P, 512], F32, ps)[:], ("ch", g), P * m, E4M3, r, E5M2, g == 0, g == 1, 512 * g)
             elif k == "E0":
                 parts = LAST_PARTS if job == evacs[-1] else 1
                 for n in range(parts):
-                    rows = slice(n * P // parts, (n + 1) * P // parts)
-                    copy(job, buf(w, [P, 512], F32)[:].rearrange("p (r a) -> p r a", a=4)[:, rows], get(r)[:].rearrange("p (a r) -> p r a", a=4)[:, rows])
+                    cols = slice(n * 512 // parts, (n + 1) * 512 // parts)
+                    copy(job, buf(w, [P, 512], F32)[:, cols], get(r)[:, cols])
             elif k == "E1":
                 x = run_len(job[1])
                 copy(job, buf(w, [P, 512], F32)[:].rearrange("p (w u x) -> p w u x", u=2, x=x), get(r)[:].rearrange("p (u w x) -> p w u x", u=2, x=x))

@@ -9,460 +9,344 @@ U32 = mybir.dt.uint32
 U8 = mybir.dt.uint8
 E4M3 = mybir.dt.float8_e4m3fn_x4
 E5M2 = mybir.dt.float8_e5m2_x4
-MULT = mybir.AluOpType.mult
 
 P = 128
 E, H, HO, T = 4, 512, 1024, 1024
+SLOTS = 4
+HALF = 512
 FLOPS = 2 * 2 * T * H * E * HO
 BYTES = 2 * (T * H + E * H * HO + T * HO) + 4 * T * E + 4 * (T * H + E * H * HO)
 
-DEPTH = {"wc": 4, "nat": 7, "gf": 4, "gw": 3, "ti": 2, "cf": 5, "ct": 4, "rot": 4, "acc": 4, "st": 8, "ws": 2}
-SORTED = ()
-RUN4 = 1
-LAST_PARTS = 2
-EARLY = 1
-ALIGN = 64
-SWARM = 0
-NW = 6
-NKS = (1, 1, 1, 0, 0)
+DEPTH = {"w_raw": 4, "dz": 7, "dz_flip": 4, "w_flip": 3, "dz_weave": 2, "dz_feat": 5, "dz_tok": 4,
+         "bank": 4, "sum0": 4, "stage": 8}
+AHEAD = 3
+SPACER = 2
+WARM_FIRST = 3
+H_PIECES = 4
+LAST_PIECES = 2
 
 
-def orders():
-    def M(e, g):
-        return [("M", e, g, j) for j in range(4)]
+def job_lists():
+    def scale(e, g, slots=range(SLOTS)):
+        return [("scale", e, g, s) for s in slots]
 
-    def TF(e, g):
-        return [("TF", e, g, c, jp) for c in range(2) for jp in range(2)]
+    def flip_dz(e, g, c, pairs=(0, 1)):
+        return [("flip_dz", e, g, c, pair) for pair in pairs]
 
-    def TW(e, c):
-        return [("TW", e, c, ap) for ap in range(2)]
+    def flip_w(e, c):
+        return [("flip_w", e, c, pair) for pair in (0, 1)]
 
-    def X0(e, g, c):
-        return [("X0", e, g, c, j) for j in range(4)]
+    def mm0(e, g, c):
+        return [("mm0", e, g, c, s) for s in range(SLOTS)]
 
-    def X1(e, c):
-        return [("X1", e, c, m, g) for m in range(4) for g in range(2)]
+    def mm1(e, c):
+        return [("mm1", e, c, m, g) for m in range(H // P) for g in (0, 1)]
 
-    def LW(e):
-        return [("L", "w", e, ap) for ap in range(2)]
+    def weave(e, g, c, us=(0, 1)):
+        return [("weave", e, g, c, us)]
 
-    def LG(g):
-        return [("L", "g2", g, jp) for jp in range(2)]
+    def weave_h(g, pieces):
+        return [("weave_h", g, n) for n in pieces]
 
-    def I(e, g, c):
-        return [("I", e, g, c)]
+    def token_side(e, c):
+        return weave(e, 0, c) + weave(e, 1, c) + [("q_tok", e, 0, c), ("q_tok", e, 1, c)]
 
-    def QT(e, g, c):
-        return [("QT", e, g, c)]
+    passes = [(e, g, c) for g in (0, 1) for e in range(E) for c in (0, 1)]
+    w_halves = [(e, c) for e in range(E) for c in (0, 1)]
 
-    def QF(e, g, c):
-        return [("QF", e, g, c)]
+    loads = [("load_p",), ("load_g", 0, 0, 1), ("load_g", 0, 1, 1), ("load_w", 0, 0), ("load_g", 0, 2, 1)]
+    loads += [("load_g", 0, 3, 1), ("load_w", 0, 1), ("load_w", 1, 0), ("load_h", 0), ("load_w", 1, 1)]
+    loads += [("load_g", 1, 0, 2), ("load_g", 1, 2, 2), ("load_w", 2, 0), ("load_w", 2, 1), ("load_h", 1)]
+    loads += [("load_w", 3, 0), ("load_w", 3, 1)]
 
-    def QW(e, c):
-        return [("QW", e, c)]
+    tensor = [("warm", n) for n in range(WARM_FIRST)]
+    head = [flip_dz(0, 0, 0, (0,)) + flip_dz(0, 0, 1, (0,)), flip_w(0, 0),
+            flip_dz(0, 0, 0, (1,)) + flip_dz(0, 0, 1, (1,)), flip_w(0, 1) + flip_dz(*passes[2])]
+    for n, banks in enumerate(head):
+        tensor += banks + ([("warm", WARM_FIRST + n)] if n + 1 < len(head) else [])
+    for n in range(6):
+        tensor += mm0(*passes[n]) + flip_w(*w_halves[n + 2]) + flip_dz(*passes[n + AHEAD])
+    for e in range(E):
+        first, second = mm0(*passes[2 * e + 6]), mm0(*passes[2 * e + 7])
+        flips = [job for item in passes[2 * e + 6 + AHEAD : 2 * e + 8 + AHEAD] for job in flip_dz(*item)]
+        if e == 0:
+            tensor += first[:SPACER] + mm1(e, 0) + first[SPACER:] + flips
+            tensor += second[:SPACER] + mm1(e, 1) + second[SPACER:]
+        elif e < E - 1:
+            tensor += mm1(e, 0) + first + mm1(e, 1) + second[:SPACER] + flips + second[SPACER:]
+        else:
+            tensor += mm1(e, 0) + first[:SPACER] + flips + first[SPACER:] + mm1(e, 1)
+    tensor += [("mm0",) + item + (s,) for s in range(SLOTS) for item in passes[13:]]
 
-    def QH(g):
-        return [("QH", g)]
+    vector = [job for e in range(E) for job in scale(e, 0, (0, 1))]
+    vector += [job for e in range(E - 1) for job in scale(e, 0, (2, 3))]
+    vector += [("q_w", 0, 0), ("q_feat", 0, 0, 0), ("q_feat", 0, 0, 1)] + weave(0, 0, 0)
+    vector += [("q_w", 0, 1), ("q_tok", 0, 0, 0), ("q_feat", 1, 0, 0)] + weave(0, 0, 1)
+    fill = [
+        [("q_tok", 0, 0, 1)] + scale(0, 1),
+        scale(3, 0, (2, 3)) + weave(0, 1, 0),
+        [("q_tok", 0, 1, 0)] + weave(0, 1, 1),
+        weave_h(1, (3,)) + [("q_h", 0), ("q_h", 1)],
+        scale(1, 1) + [("q_tok", 0, 1, 1)] + token_side(1, 0)[:2],
+        token_side(1, 0)[2:],
+    ]
+    for n in range(6):
+        vector += [("q_w",) + w_halves[n + 2], ("q_feat",) + passes[n + AHEAD]] + fill[n]
+    vector += token_side(1, 1) + [("q_feat",) + passes[9]] + scale(2, 1)
+    vector += token_side(2, 0) + [("q_feat",) + passes[10]] + token_side(2, 1) + [("q_feat",) + passes[11]]
+    vector += scale(3, 1) + weave(3, 0, 0, (1,)) + token_side(3, 0)[1:] + [("q_feat",) + passes[12]]
+    vector += token_side(3, 1) + [("q_feat",) + item for item in passes[13:]]
+    vector += [("drain0", 1, 1), ("drain0", 1, 3)]
 
-    F = [(e, g) for g in range(2) for e in range(4)]
-    U = [(e, c) for e in range(4) for c in range(2)]
+    behind = {
+        ("drain_dz", 1, 0, 0, 1): weave_h(0, (0,)),
+        ("drain_dz", 1, 0, 1, 1): weave_h(0, (1, 2)),
+        ("drain_dz", 2, 0, 0, 1): weave_h(0, (3,)),
+        ("drain_dz", 2, 0, 1, 1): weave_h(1, (0, 1)),
+        ("drain_dz", 3, 0, 0, 1): weave_h(1, (2,)),
+        ("drain1", 0, 1, 3): [("drain0", 0, 0), ("drain0", 0, 1)],
+        ("drain1", 2, 0, 3): weave(3, 0, 0, (0,)),
+    }
+    closing = [drain_of(job) for job in tensor if drain_of(job)]
+    moved = [job for extra in behind.values() for job in extra]
+    scalar = [job for drain in closing if drain not in moved for job in [drain] + behind.get(drain, [])]
+    stores = [("store",) + job for job in scalar if job[0] in ("drain0", "drain1")]
+    scalar = [job for job in scalar if job not in vector]
+    return loads, tensor, vector, scalar, stores
 
-    def HM(g, u):
-        return [("HM", g, u)]
 
-    def IM(e, g, c, u):
-        return [("IM", e, g, c, u)]
+def drain_of(job):
+    if job[0] == "flip_dz":
+        return ("drain_dz",) + job[1:]
+    if job[0] == "flip_w":
+        return ("drain_w",) + job[1:]
+    if job[0] == "mm1" and job[4] == 1:
+        return ("drain1",) + job[1:4]
+    if job[0] == "mm0" and job[1] == E - 1 and job[3] == 1:
+        return ("drain0", job[2], job[4])
+    return None
 
-    def EI(e, g, c, u):
-        return [("EI", e, g, c, u)]
 
-    def SW(e, a):
-        return [("SW", e, a)]
-
-    def IH(g, q):
-        return [("IH", g, q)]
-
-    def WU(a, n):
-        return [("WU", a, i) for i in range(n)]
-
-    def T(e, c):
-        return I(e, 0, c) + I(e, 1, c) + QT(e, 0, c) + QT(e, 1, c)
-
-    def I2(e, g, c, u):
-        return [("I2", e, g, c, u)]
-
-    def E0(g, j):
-        return [("E0", g, j)]
-
-    def LC(e, c):
-        return [("L", "wc", e, c)]
-
-    loads = [("L", "p")] + [("L", "g", 0, j) for j in range(2)] + LC(0, 0) + [("L", "g", 0, j) for j in range(2, 4)] + LC(0, 1) + LC(1, 0) + [("L", "h", 0)] + LC(1, 1) + LG(1) + LC(2, 0) + LC(2, 1) + [("L", "h", 1)] + LC(3, 0) + LC(3, 1)
-    t0 = [("TF", 0, 0, c, jp) for jp in range(2) for c in range(2)]
-    pe = WU(0, NW) + t0[:2] + WU(1, NKS[0]) + TW(0, 0) + WU(2, NKS[1]) + t0[2:] + WU(3, NKS[2]) + TW(0, 1) + WU(4, NKS[3]) + TF(1, 0)[:2]
-    pe += X0(0, 0, 0) + TW(1, 0) + TF(1, 0)[2:] + X0(0, 0, 1) + TW(1, 1) + TF(2, 0)[:2]
-    pe += X0(1, 0, 0) + TW(2, 0) + TF(2, 0)[2:] + X0(1, 0, 1) + TW(2, 1) + TF(3, 0)[:2]
-    pe += X0(2, 0, 0) + TW(3, 0) + TF(3, 0)[2:] + X0(2, 0, 1) + TW(3, 1) + TF(0, 1)[:2]
-    pe += X0(3, 0, 0)[:2] + X1(0, 0) + X0(3, 0, 0)[2:] + TF(0, 1)[2:] + TF(1, 1)[:2] + X0(3, 0, 1)[:2] + X1(0, 1) + X0(3, 0, 1)[2:]
-    pe += X1(1, 0) + X0(0, 1, 0) + X1(1, 1) + X0(0, 1, 1)[:2] + TF(1, 1)[2:] + TF(2, 1)[:2] + X0(0, 1, 1)[2:]
-    pe += X1(2, 0) + X0(1, 1, 0) + X1(2, 1) + X0(1, 1, 1)[:2] + TF(2, 1)[2:] + TF(3, 1)[:2] + X0(1, 1, 1)[2:]
-    pe += X1(3, 0) + X0(2, 1, 0)[:2] + TF(3, 1)[2:] + X0(2, 1, 0)[2:] + X1(3, 1)
-    pe += [("X0", e, 1, c, j) for j in range(4) for e, c in ((2, 1), (3, 0), (3, 1))]
-    vec = M(0, 0)[:2] + M(1, 0)[:2] + M(2, 0)[:2] + M(3, 0)[:2] + M(0, 0)[2:] + M(1, 0)[2:] + M(2, 0)[2:] + QW(0, 0) + QF(0, 0, 0) + QF(0, 0, 1) + I(0, 0, 0) + QW(0, 1) + QT(0, 0, 0) + QF(1, 0, 0) + I(0, 0, 1)
-    vec += QW(1, 0) + QT(0, 0, 1) + QF(1, 0, 1) + M(0, 1)
-    vec += QW(1, 1) + QF(2, 0, 0) + M(3, 0)[2:] + I(0, 1, 0)
-    vec += QW(2, 0) + QF(2, 0, 1) + QT(0, 1, 0) + I(0, 1, 1)
-    vec += QW(2, 1) + QF(3, 0, 0) + IH(1, 3) + QT(0, 1, 1) + QH(0)
-    vec += QW(3, 0) + QH(1) + M(1, 1) + QF(3, 0, 1) + I(1, 0, 0) + QW(3, 1)
-    vec += QT(1, 0, 0) + I(1, 1, 0) + QF(0, 1, 0) + QT(1, 1, 0) + T(1, 1) + QF(0, 1, 1) + M(2, 1)
-    vec += T(2, 0) + QF(1, 1, 0) + T(2, 1) + QF(1, 1, 1) + M(3, 1)
-    vec += I2(3, 0, 0, 1) + I(3, 1, 0) + QT(3, 0, 0) + QT(3, 1, 0) + QF(2, 1, 0) + T(3, 1) + QF(2, 1, 1) + QF(3, 1, 0) + QF(3, 1, 1)
-    vec += [("E0", 1, 1), ("E0", 1, 3)]
-    act_extra = {("E1", 0, 1, 3): E0(0, 0) + E0(0, 1), ("E1", 2, 0, 3): [("I2", 3, 0, 0, 0)], ("EF", 1, 0, 0, 1): IH(0, 0), ("EF", 1, 0, 1, 1): IH(0, 1) + IH(0, 2), ("EF", 2, 0, 0, 1): IH(0, 3), ("EF", 2, 0, 1, 1): IH(1, 0) + IH(1, 1), ("EF", 3, 0, 0, 1): IH(1, 2)}
-
-    return loads, pe, vec, act_extra
+def buffers_of(job, loads):
+    kind, a = job[0], job[1:]
+    if kind == "scale":
+        g_piece = [("g_raw",) + x[1:] for x in loads if x[0] == "load_g" and x[1] == a[1] and x[2] <= a[2] < x[2] + x[3]]
+        return ("dz",) + a[:2], g_piece + [("p_raw",)]
+    table = {
+        "load_p": lambda: (("p_raw",), []),
+        "load_g": lambda: (("g_raw",) + a, []),
+        "load_w": lambda: (("w_raw",) + a, []),
+        "load_h": lambda: (("h_raw",) + a, []),
+        "identity": lambda: (("identity",), []),
+        "warm": lambda: (("unread",), [("p_raw",), ("identity",)]),
+        "flip_dz": lambda: (("bank",) + job, [("dz",) + a[:2], ("identity",)]),
+        "flip_w": lambda: (("bank",) + job, [("w_raw",) + a[:2], ("identity",)]),
+        "drain_dz": lambda: (("dz_flip",) + a[:3], [("bank", "flip_dz") + a]),
+        "drain_w": lambda: (("w_flip",) + a[:2], [("bank", "flip_w") + a]),
+        "weave": lambda: (("dz_weave", a[0], a[2]), [("dz",) + a[:2]]),
+        "weave_h": lambda: (("h_weave", a[0]), [("h_raw", a[0])]),
+        "q_feat": lambda: (("dz_feat",) + a, [("dz_flip",) + a]),
+        "q_tok": lambda: (("dz_tok", a[0], a[2]), [("dz_weave", a[0], a[2])]),
+        "q_w": lambda: (("w_codes",) + a, [("w_flip",) + a]),
+        "q_h": lambda: (("h_codes",) + a, [("h_weave",) + a]),
+        "mm0": lambda: (("sum0", a[1], a[3]), [("dz_feat",) + a[:3], ("w_codes", a[0], a[2])]),
+        "mm1": lambda: (("bank", "mm1") + a[:3], [("dz_tok",) + a[:2], ("h_codes", a[3])]),
+        "drain0": lambda: (("stage",) + job, [("sum0",) + a]),
+        "drain1": lambda: (("stage",) + job, [("bank", "mm1") + a]),
+        "store": lambda: (None, [("stage",) + a]),
+    }
+    return table[kind]()
 
 
 def tile_enhancedmathematicalreasoning_pa_v_kernel(
     tc, hidden_states, op_logits, We, be, op_w, grad_out, out_0, out_1
 ):
     nc = tc.nc
-    h_view = hidden_states.flatten_outer_dims().rearrange("(g p j) w -> g p (j w)", g=2, j=4)
-    g_view = grad_out.flatten_outer_dims().rearrange("(g p j) w -> g p (j w)", g=2, j=4)
-    w_view = We.rearrange("e (a p) w -> e p a w", a=4)
-    p_view = op_w.flatten_outer_dims().rearrange("(g p j) e -> p g (j e)", g=2, j=4)
-    o0_view = out_0.flatten_outer_dims().rearrange("(g p j) w -> g j p w", g=2, j=4)
-    o1_view = out_1.rearrange("e (m p) w -> e m p w", p=P)
+    h_view = hidden_states.flatten_outer_dims().rearrange("(g p s) i -> g p (s i)", g=2, s=SLOTS)
+    g_view = grad_out.flatten_outer_dims().rearrange("(g p s) j -> g p (s j)", g=2, s=SLOTS)
+    p_view = op_w.flatten_outer_dims().rearrange("(g p s) e -> p g (s e)", g=2, s=SLOTS)
+    w_view = We.rearrange("e (a p) j -> e p a j", p=P)
+    out0_view = out_0.flatten_outer_dims().rearrange("(g p s) i -> g s p i", g=2, s=SLOTS)
+    out1_view = out_1.rearrange("e (m p) j -> e m p j", p=P)
 
-    loads, pe, vec, act_extra = orders()
-
-    def writes(job):
-        k = job[0]
-        if k == "M":
-            return [("nat", job[1], job[2])]
-        if k in ("TF", "TW", "IM", "HM"):
-            return [("rot",) + job]
-        if k == "EF":
-            return [("gf", job[1], job[2], job[3])]
-        if k == "EW":
-            return [("gw", job[1], job[2])]
-        if k == "SW":
-            return [("ws", job[1], job[2])]
-        if k in ("I", "EI", "I2", "I4"):
-            return [("ti", job[1], job[3])]
-        if k in ("IH", "EH"):
-            return [("gh", job[1])]
-        if k == "QF":
-            return [("cf",) + job[1:]]
-        if k == "QT":
-            return [("ct", job[1], job[3])]
-        if k == "QW":
-            return [("cw",) + job[1:]]
-        if k == "QH":
-            return [("ch",) + job[1:]]
-        if k == "X0":
-            return [("acc", job[2], job[4])]
-        if k == "X1":
-            return [("rot", "X1", job[1], job[2], job[3])]
-        if k == "E0":
-            return [("st", 0, job[1], job[2])]
-        if k == "E1":
-            return [("st", 1, job[1], job[2], job[3])]
-        if k == "L":
-            return [job[1:]]
-        return []
-
-    def g_piece(g, j):
-        return ("g", g, j) if ("L", "g", g, j) in loads else ("g2", g, j // 2)
-
-    def reads(job):
-        k = job[0]
-        if k == "M":
-            return [g_piece(job[2], job[3]), ("p",)]
-        if k == "WU":
-            return [loads[1][1:]]
-        if k == "TF":
-            return [("nat", job[1], job[2])]
-        if k == "TW":
-            if ("L", "wh") + job[1:] in loads:
-                return [("wh",) + job[1:]]
-            return [("ws" if job[1] in SORTED else "wc", job[1], job[2])]
-        if k == "SW":
-            return [("wc", job[1], job[2])]
-        if k in ("I", "IM", "I2", "I4"):
-            return [("nat", job[1], job[2])]
-        if k in ("IH", "HM"):
-            return [("h", job[1])]
-        if k == "EF":
-            return [("rot", "TF") + job[1:]]
-        if k == "EW":
-            return [("rot", "TW") + job[1:]]
-        if k == "EI":
-            return [("rot", "IM") + job[1:]]
-        if k == "EH":
-            return [("rot", "HM") + job[1:]]
-        if k == "QF":
-            return [("gf",) + job[1:]]
-        if k == "QT":
-            return [("ti", job[1], job[3])]
-        if k == "QW":
-            return [("gw",) + job[1:]]
-        if k == "QH":
-            return [("gh", job[1])]
-        if k == "X0":
-            return [("cf", job[1], job[2], job[3]), ("cw", job[1], job[3])]
-        if k == "X1":
-            return [("ct", job[1], job[2]), ("ch", job[4])]
-        if k == "E0":
-            return [("acc", job[1], job[2])]
-        if k == "E1":
-            return [("rot", "X1") + job[1:]]
-        if k == "S":
-            return [("st",) + job[1:]]
-        return []
-
-    def evac_of(job):
-        k = job[0]
-        if k in ("TF", "TW", "IM", "HM"):
-            return ({"TF": "EF", "TW": "EW", "IM": "EI", "HM": "EH"}[k],) + job[1:]
-        if k == "X1" and job[4] == 1:
-            return ("E1",) + job[1:4]
-        if k == "X0" and job[1] == 3 and job[3] == 1:
-            return ("E0", job[2], job[4])
-        return None
-
-    evacs = [evac_of(job) for job in pe if evac_of(job)]
-    act = []
-    for job in evacs:
-        if job not in vec and not any(job in x for x in act_extra.values()):
-            act.append(job)
-        act.extend(act_extra.get(job, []))
-    act = act_extra.get("first", []) + act
-    moved = [x for extra in act_extra.values() for x in extra if x in evacs]
-    evacs = [x for job in evacs if job not in moved for x in [job] + [y for y in act_extra.get(job, []) if y in moved]]
-    stores = [("S", 0 if job[0] == "E0" else 1) + job[1:] for job in evacs if job[0] in ("E0", "E1")]
-    queues = [loads[:1] + [("ID",)] + loads[1:] + stores, pe, vec, act]
-    jobs = [job for q in queues for job in q]
-    assert len(set(jobs)) == len(jobs)
+    loads, tensor, vector, scalar, stores = job_lists()
+    queues = [loads[:1] + [("identity",)] + loads[1:] + stores, tensor, vector, scalar]
+    jobs = [job for queue in queues for job in queue]
+    uses = {job: buffers_of(job, loads) for job in jobs}
     writers, readers = {}, {}
     for job in jobs:
-        for b in writes(job):
-            writers.setdefault(b, []).append(job)
-        for b in reads(job):
-            readers.setdefault(b, []).append(job)
-    order_of = {}
-    for job in loads + pe + [j for j in evacs] + [("I",) + j[1:] for j in vec if j[0] == "QT"] + vec + act:
-        for b in writes(job):
-            if b[0] in DEPTH and b not in order_of.setdefault(b[0], []):
-                order_of[b[0]].append(b)
-    slot, before = {}, {}
-    for kind, bufs in order_of.items():
-        for n, b in enumerate(bufs):
-            slot[b] = n % DEPTH[kind]
+        writers.setdefault(uses[job][0], []).append(job)
+        for item in uses[job][1]:
+            readers.setdefault(item, []).append(job)
+
+    turns = {}
+    for item in [uses[job][1][0] for job in stores] + [uses[job][0] for job in loads + tensor + vector + scalar]:
+        if item[0] in DEPTH and item not in turns.setdefault(item[0], []):
+            turns[item[0]].append(item)
+    place, replaces = {}, {}
+    for kind, items in turns.items():
+        for n, item in enumerate(items):
+            place[item] = n % DEPTH[kind]
             if n >= DEPTH[kind]:
-                before[b] = bufs[n - DEPTH[kind]]
+                replaces[item] = items[n - DEPTH[kind]]
 
     def needs(job):
-        out = []
-        for b in reads(job):
-            ws = writers[b]
-            if job[0] == "TF":
-                ws = [w for w in ws if w[3] // 2 == job[4]]
-            if job[0] == "QT" and job[2] != 2:
-                ws = [w for w in ws if w[2] == job[2]]
-            if job[0] == "X1" and b[0] == "ct":
-                ws = [w for w in ws if w[2] in (job[4], 2)]
-            out.extend(ws)
-        for b in writes(job):
-            if b in before:
-                out.extend(readers[before[b]])
-        return out
+        written, read = uses[job]
+        before = list(readers[replaces[written]]) if written in replaces else []
+        for item in read:
+            makers = writers[item]
+            if item[0] == "dz" and job[0] == "flip_dz":
+                makers = [other for other in makers if other[3] // 2 == job[4]]
+            if item[0] == "dz_weave":
+                makers = [other for other in makers if other[2] == job[2]]
+            if item[0] == "dz_tok":
+                makers = [other for other in makers if other[2] == job[4]]
+            before.extend(makers)
+        return before
 
     with ExitStack() as ctx:
-        sb = ctx.enter_context(tc.tile_pool(name="sb", bufs=1))
-        ps = ctx.enter_context(tc.psum_pool(name="ps", bufs=1))
+        sbuf = ctx.enter_context(tc.tile_pool(name="sbuf", bufs=1))
+        psum = ctx.enter_context(tc.psum_pool(name="psum", bufs=1))
         tiles = {}
 
-        def buf(b, shape, dtype, pool=sb, part=""):
-            if (b, part) not in tiles:
-                tag = f"{b[0]}{part}{slot[b]}" if b in slot else "_".join(str(x) for x in b) + part
-                if pool is sb:
-                    tiles[b, part] = pool.tile(shape, dtype, name=tag, tag=tag, align_bytes=ALIGN)
+        def tile_of(item, shape, dtype, part=""):
+            if (item, part) not in tiles:
+                tag = f"{item[0]}{place[item]}{part}" if item in place else "".join(str(x) for x in item) + part
+                if item[0] in ("bank", "sum0"):
+                    tiles[item, part] = psum.tile(shape, dtype, name=tag, tag=tag)
                 else:
-                    tiles[b, part] = pool.tile(shape, dtype, name=tag, tag=tag)
-            return tiles[b, part]
-
-        def get(b, part=""):
-            return tiles[b, part]
-
-        ident = sb.tile([P, P], F32, name="ident")
-        ident_bf = sb.tile([P, P], BF16, name="ident_bf")
-
-        def run_len(e):
-            return 16 if e in SORTED else 2
+                    tiles[item, part] = sbuf.tile(shape, dtype, name=tag, tag=tag, align_bytes=64)
+            return tiles[item, part]
 
         def copy(job, out, in_):
-            if job in vec:
+            if job in vector:
                 nc.vector.tensor_copy(out=out, in_=in_)
             else:
                 nc.scalar.copy(out=out, in_=in_)
 
-        def quant(dst, src, fmt):
-            codes = buf(dst, [P, 512], U32)
-            scales = buf(dst, [P, 512], U8, part="s")
-            nc.vector.quantize_mx(out=codes[:].bitcast(fmt), scales=scales[:], in_=get(src)[:])
+        def weave_copy(job, dst, src):
+            copy(job, dst.rearrange("p (o w x s) -> p o w s x", o=2, x=4, s=SLOTS),
+                 src.rearrange("p o (w x) s -> p o w s x", x=4))
 
-        def mx(out, lhs, l0, lfmt, rhs, rfmt, start, stop, r0=0):
+        def quantize(item, width, cols, src, fmt):
+            codes = tile_of(item, [P, width], U32)
+            scales = tile_of(item, [P, width], U8, "_scales")
+            nc.vector.quantize_mx(out=codes[:, cols].bitcast(fmt), scales=scales[:, cols], in_=src)
+
+        def matmul_mx(out, lhs, lhs_cols, lhs_fmt, rhs, rhs_cols, rhs_fmt, start, stop):
             nc.tensor.matmul_mx(
                 out=out,
-                lhsT=get(lhs)[:, l0 : l0 + P].bitcast(lfmt),
-                lhsT_scale=get(lhs, "s")[:, l0 : l0 + P],
-                rhs=get(rhs)[:, r0 : r0 + 512].bitcast(rfmt),
-                rhs_scale=get(rhs, "s")[:, r0 : r0 + 512],
+                lhsT=tiles[lhs, ""][:, lhs_cols].bitcast(lhs_fmt),
+                lhsT_scale=tiles[lhs, "_scales"][:, lhs_cols],
+                rhs=tiles[rhs, ""][:, rhs_cols].bitcast(rhs_fmt),
+                rhs_scale=tiles[rhs, "_scales"][:, rhs_cols],
                 start=start,
                 stop=stop,
             )
 
-        def interleave_views(dst, src):
-            if RUN4:
-                return (dst.rearrange("p (u w i j) -> p u w j i", u=2, i=4, j=4), src.rearrange("p u (w i) j -> p u w j i", i=4))
-            return dst.rearrange("p (u w j) -> p u w j", u=2, j=4), src
+        def span(n, width):
+            return slice(n * width, (n + 1) * width)
 
         def emit(job):
-            k = job[0]
-            w = writes(job)[0] if writes(job) else None
-            r = reads(job)[0] if reads(job) else None
-            if k == "ID":
-                make_identity(nc, ident[:])
-                if any(x[0] in ("IM", "HM") for x in pe):
-                    nc.scalar.copy(out=ident_bf[:], in_=ident[:])
-                elif SWARM:
-                    nc.scalar.copy(out=ident_bf[:, 0:2], in_=ident[:, 0:2])
-            elif k == "L":
-                if w[0] == "p":
-                    nc.scalar.dma_start(out=buf(w, [P, 2, 16], F32)[:], in_=p_view)
-                elif w[0] == "g":
-                    nc.sync.dma_start(out=buf(w, [P, HO], BF16)[:], in_=g_view[w[1], :, w[2] * HO : (w[2] + 1) * HO])
-                elif w[0] == "g2":
-                    nc.sync.dma_start(out=buf(w, [P, 2 * HO], BF16)[:], in_=g_view[w[1], :, w[2] * 2 * HO : (w[2] + 1) * 2 * HO])
-                elif w[0] == "wh":
-                    nc.sync.dma_start(out=buf(w, [P, HO], BF16)[:].rearrange("p (a w) -> p a w", a=2), in_=w_view[w[1]].rearrange("p (a w) -> p a w", a=4)[:, 2 * w[3] : 2 * w[3] + 2, w[2] * 512 : (w[2] + 1) * 512])
-                elif w[0] == "wc":
-                    nc.sync.dma_start(out=buf(w, [P, 2 * HO], BF16)[:].rearrange("p (a w) -> p a w", a=4), in_=w_view[w[1]][:, :, w[2] * 512 : (w[2] + 1) * 512])
-                elif w[0] == "w":
-                    nc.sync.dma_start(out=buf(w, [P, 2 * HO], BF16)[:], in_=w_view[w[1], :, w[2] * 2 * HO : (w[2] + 1) * 2 * HO])
-                else:
-                    nc.sync.dma_start(out=buf(w, [P, 4 * H], BF16)[:], in_=h_view[w[1]])
-            elif k == "M":
-                e, g, j = job[1:]
-                x = run_len(e)
-                src = get(r)[:] if r[0] == "g" else get(r)[:, (j % 2) * HO : (j % 2 + 1) * HO]
+            kind = job[0]
+            written, read = uses[job]
+            src = tiles[read[0], ""] if read else None
+            if kind == "identity":
+                make_identity(nc, tile_of(written, [P, P], F32)[:])
+            elif kind == "load_p":
+                nc.scalar.dma_start(out=tile_of(written, [P, 2, SLOTS * E], F32)[:], in_=p_view)
+            elif kind == "load_g":
+                g, s, count = job[1:]
+                nc.sync.dma_start(out=tile_of(written, [P, count * HO], BF16)[:],
+                                  in_=g_view[g, :, s * HO : (s + count) * HO])
+            elif kind == "load_w":
+                e, c = job[1:]
+                raw = tile_of(written, [P, SLOTS * HALF], BF16)
+                nc.sync.dma_start(out=raw[:].rearrange("p (a j) -> p a j", j=HALF), in_=w_view[e][:, :, span(c, HALF)])
+            elif kind == "load_h":
+                nc.sync.dma_start(out=tile_of(written, [P, SLOTS * H], BF16)[:], in_=h_view[job[1]])
+            elif kind == "warm":
+                if (written, "") not in tiles:
+                    tiles[written, ""] = psum.tile([P, HALF], F32, name="sum03", tag="sum03")
+                any_column = src[:, 0, 0:1].bitcast(BF16)[:, 1:2].to_broadcast([P, P])
+                any_rows = tiles[read[1], ""][:].bitcast(BF16).unsqueeze(1).to_broadcast([P, 2, 2 * P])
+                nc.tensor.matmul(out=tiles[written, ""][:], lhsT=any_column, rhs=any_rows, start=True, stop=True)
+            elif kind == "scale":
+                e, g, s = job[1:]
+                row = src[:, span(s - read[0][2], HO)]
                 nc.vector.tensor_scalar(
-                    out=buf(w, [P, 4 * HO], BF16)[:, j * HO : (j + 1) * HO].rearrange("p (u w x) -> p u w x", u=2, x=x),
-                    in0=src.rearrange("p (w u x) -> p u w x", u=2, x=x),
-                    scalar1=get(("p",))[:, g, 4 * j + e : 4 * j + e + 1],
+                    out=tile_of(written, [P, SLOTS * HO], BF16)[:, span(s, HO)].rearrange("p (u w x) -> p u w x", u=2, x=2),
+                    in0=row.rearrange("p (w u x) -> p u w x", u=2, x=2),
+                    scalar1=tiles[read[1], ""][:, g, E * s + e : E * s + e + 1],
                     scalar2=None,
-                    op0=MULT,
+                    op0=mybir.AluOpType.mult,
                 )
-            elif k == "SW":
-                copy(job, buf(w, [P, 2 * HO], BF16)[:].rearrange("p (a u w x) -> p a u w x", a=4, u=2, x=16),
-                     get(r)[:].rearrange("p (a w u x) -> p a u w x", a=4, u=2, x=16))
-            elif k in ("TF", "TW"):
-                c, half = job[-2:]
-                bank = buf(w, [P, 512], F32, ps)
-                words = get(r)[:].bitcast(F32)
-                for s in range(2):
+            elif kind in ("flip_dz", "flip_w"):
+                c, pair = job[-2:]
+                bank = tile_of(written, [P, HALF], F32)
+                words = src[:].bitcast(F32)
+                for r in range(2):
                     for u in range(2):
-                        row = s if r[0] == "wh" else 2 * half + s
-                        if k == "TF":
-                            src = words[:, row * 512 + u * 256 + c * P : row * 512 + u * 256 + (c + 1) * P]
-                        elif job[1] in SORTED:
-                            src = words[:, row * 256 + u * P : row * 256 + (u + 1) * P]
+                        if kind == "flip_dz":
+                            start = (2 * pair + r) * (HO // 2) + u * (HO // 4) + c * P
+                            block = words[:, start : start + P]
                         else:
-                            src = words[:, row * 256 + u : row * 256 + u + 255 : 2]
-                        nc.tensor.transpose(bank[:, (2 * s + u) * P : (2 * s + u + 1) * P], src, ident[:])
-            elif k in ("EF", "EW"):
-                half = job[-1]
-                dst = buf(w, [P, 2048], BF16)[:].bitcast(F32)[:, half * 512 : (half + 1) * 512]
-                copy(job, dst.rearrange("p (s r u) -> p s r u", s=2, u=2), get(r)[:].rearrange("p (s u r) -> p s r u", s=2, u=2))
-            elif k == "I":
-                c = job[3]
-                src = get(r)[:].rearrange("p (j u c w) -> p c u w j", j=4, u=2, c=2)[:, c]
-                copy(job, *interleave_views(buf(w, [P, 4096], BF16)[:, job[2] * 2048 : (job[2] + 1) * 2048], src))
-            elif k == "I2":
-                c, u = job[3:]
-                src = get(r)[:].rearrange("p (j u c q w) -> p c u q w j", j=4, u=2, c=2, q=2)[:, c, u]
-                copy(job, *interleave_views(buf(w, [P, 4096], BF16)[:, job[2] * 2048 + u * 1024 : job[2] * 2048 + (u + 1) * 1024], src))
-            elif k == "I4":
-                c, n = job[3:]
-                src = get(r)[:].rearrange("p (j u c h q w) -> p c u h q w j", j=4, u=2, c=2, h=2, q=2)[:, c, n // 2, n % 2]
-                copy(job, *interleave_views(buf(w, [P, 2048], BF16)[:, n * 512 : (n + 1) * 512], src))
-            elif k == "IH":
-                q = job[2]
-                src = get(r)[:].rearrange("p (j q u w) -> p q u w j", j=4, q=4, u=2)[:, q]
-                copy(job, *interleave_views(buf(w, [P, 2048], BF16)[:, q * 512 : (q + 1) * 512], src))
-            elif k == "WU":
-                if ("wu", "") not in tiles:
-                    tiles["wu", ""] = ps.tile([P, 512], F32, name="acc3", tag="acc3")
-                first = get(r)
-                if job[1] == 0 and EARLY:
-                    halves = ident[:].bitcast(BF16)
-                    nc.tensor.matmul(out=get("wu")[:], lhsT=halves[:, 0:P], rhs=halves.unsqueeze(1).to_broadcast([P, 2, 2 * P]), start=True, stop=True)
-                    return
-                nc.tensor.matmul(out=get("wu")[:], lhsT=first[:, 0:P], rhs=first[:, 0:512], start=True, stop=True)
-            elif k in ("IM", "HM"):
-                u = job[-1]
-                bank = buf(w, [P, 1024], BF16, ps)
-                if k == "IM":
-                    src = get(r)[:].rearrange("p (j u c w) -> p c u w j", j=4, u=2, c=2)[:, job[3], u]
+                            start = (2 * pair + r) * (HALF // 2) + u
+                            block = words[:, start : start + 2 * P - 1 : 2]
+                        nc.tensor.transpose(bank[:, span(2 * r + u, P)], block, tiles[read[1], ""][:])
+            elif kind in ("drain_dz", "drain_w"):
+                words = tile_of(written, [P, SLOTS * HALF], BF16)[:].bitcast(F32)[:, span(job[-1], HALF)]
+                copy(job, words.rearrange("p (r n u) -> p r n u", r=2, u=2),
+                     src[:].rearrange("p (r u n) -> p r n u", r=2, u=2))
+            elif kind == "weave":
+                g, c, us = job[2:]
+                dst = tile_of(written, [P, 2 * SLOTS * HALF], BF16)[:, span(g, SLOTS * HALF)]
+                if len(us) == 2:
+                    weave_copy(job, dst, src[:].rearrange("p (s u c w) -> p c u w s", s=SLOTS, u=2, c=2)[:, c])
                 else:
-                    src = get(r)[:].rearrange("p (j u w) -> p u w j", j=4, u=2)[:, u]
-                for n in range(2):
-                    nc.tensor.matmul(out=bank[:, n * 512 : (n + 1) * 512], lhsT=ident_bf[:], rhs=src[:, n * P : (n + 1) * P, :], start=True, stop=True)
-            elif k in ("EI", "EH"):
-                u = job[-1]
-                copy(job, buf(w, [P, 2048], BF16)[:, u * 1024 : (u + 1) * 1024], get(r)[:])
-            elif k == "QT":
-                lo, hi = (0, 1024) if job[2] == 2 else (job[2] * 512, (job[2] + 1) * 512)
-                codes = buf(w, [P, 1024], U32)
-                scales = buf(w, [P, 1024], U8, part="s")
-                nc.vector.quantize_mx(out=codes[:, lo:hi].bitcast(E5M2), scales=scales[:, lo:hi], in_=get(r)[:, 4 * lo : 4 * hi])
-            elif k == "QF":
-                quant(w, r, E5M2)
-            elif k in ("QW", "QH"):
-                quant(w, r, E4M3)
-            elif k == "X0":
-                e, g, c, j = job[1:]
-                mx(buf(w, [P, 512], F32, ps)[:], r, P * j, E5M2, ("cw", e, c), E4M3, e == 0 and c == 0, e == 3 and c == 1)
-            elif k == "X1":
-                e, c, m, g = job[1:]
-                mx(buf(w, [P, 512], F32, ps)[:], ("ch", g), P * m, E4M3, r, E5M2, g == 0, g == 1, 512 * g)
-            elif k == "E0":
-                parts = LAST_PARTS if job == evacs[-1] else 1
-                for n in range(parts):
-                    cols = slice(n * 512 // parts, (n + 1) * 512 // parts)
-                    copy(job, buf(w, [P, 512], F32)[:, cols], get(r)[:, cols])
-            elif k == "E1":
-                x = run_len(job[1])
-                copy(job, buf(w, [P, 512], F32)[:].rearrange("p (w u x) -> p w u x", u=2, x=x), get(r)[:].rearrange("p (u w x) -> p w u x", u=2, x=x))
-            elif k == "S":
-                if job[1] == 0:
-                    dst = o0_view[job[2], job[3]]
+                    cols = src[:].rearrange("p (s u c o w) -> p c u o w s", s=SLOTS, u=2, c=2, o=2)[:, c, us[0]]
+                    weave_copy(job, dst[:, span(us[0], SLOTS * HALF // 2)], cols)
+            elif kind == "weave_h":
+                cols = src[:].rearrange("p (s n o w) -> p n o w s", s=SLOTS, n=H_PIECES, o=2)[:, job[2]]
+                weave_copy(job, tile_of(written, [P, SLOTS * H], BF16)[:, span(job[2], SLOTS * H // H_PIECES)], cols)
+            elif kind == "q_tok":
+                quantize(written, 2 * HALF, span(job[2], HALF), src[:, span(job[2], SLOTS * HALF)], E5M2)
+            elif kind in ("q_feat", "q_w", "q_h"):
+                quantize(written, HALF, span(0, HALF), src[:], E5M2 if kind == "q_feat" else E4M3)
+            elif kind == "mm0":
+                e, g, c, s = job[1:]
+                matmul_mx(tile_of(written, [P, HALF], F32)[:], read[0], span(s, P), E5M2, read[1], span(0, HALF), E4M3,
+                          (e, c) == (0, 0), (e, c) == (E - 1, 1))
+            elif kind == "mm1":
+                m, g = job[3:]
+                matmul_mx(tile_of(written, [P, HALF], F32)[:], read[1], span(m, P), E4M3, read[0], span(g, HALF), E5M2,
+                          g == 0, g == 1)
+            elif kind == "drain0":
+                pieces = LAST_PIECES if ("store",) + job == stores[-1] else 1
+                for n in range(pieces):
+                    cols = span(n, HALF // pieces)
+                    copy(job, tile_of(written, [P, HALF], F32)[:, cols], src[:, cols])
+            elif kind == "drain1":
+                copy(job, tile_of(written, [P, HALF], F32)[:].rearrange("p (w u x) -> p w u x", u=2, x=2),
+                     src[:].rearrange("p (u w x) -> p w u x", u=2, x=2))
+            else:
+                if job[1] == "drain0":
+                    dst = out0_view[job[2], job[3]]
                 else:
-                    dst = o1_view[job[2], job[4]][:, job[3] * 512 : (job[3] + 1) * 512]
-                parts = LAST_PARTS if job == stores[-1] else 1
-                for n in range(parts):
-                    cols = slice(n * 512 // parts, (n + 1) * 512 // parts)
-                    nc.sync.dma_start(out=dst[:, cols], in_=get(r)[:, cols])
+                    dst = out1_view[job[2], job[4]][:, span(job[3], HALF)]
+                pieces = LAST_PIECES if job == stores[-1] else 1
+                for n in range(pieces):
+                    cols = span(n, HALF // pieces)
+                    nc.sync.dma_start(out=dst[:, cols], in_=src[:, cols])
 
         with tc.manual_schedule():
             done = set()
             heads = [0] * len(queues)
             while len(done) < len(jobs):
-                before_round = len(done)
+                count = len(done)
                 for q, queue in enumerate(queues):
-                    while heads[q] < len(queue) and all(n in done for n in needs(queue[heads[q]])):
+                    while heads[q] < len(queue) and all(other in done for other in needs(queue[heads[q]])):
                         emit(queue[heads[q]])
                         done.add(queue[heads[q]])
                         heads[q] = heads[q] + 1
-                assert len(done) > before_round, [queue[h] if h < len(queue) else None for queue, h in zip(queues, heads)]
+                assert len(done) > count, "the job lists wait for each other"

@@ -21,7 +21,7 @@ DEPTH = {"w_raw": 4, "dz": 7, "dz_flip": 4, "w_flip": 3, "dz_weave": 2, "dz_feat
          "bank": 4, "sum0": 4, "stage": 8}
 AHEAD = 3
 SPACER = 2
-WARM_FIRST = 3
+WARM_FIRST = 5
 H_PIECES = 4
 LAST_PIECES = 2
 
@@ -87,8 +87,8 @@ def job_lists():
         scale(3, 0, (2, 3)) + weave(0, 1, 0),
         [("q_tok", 0, 1, 0)] + weave(0, 1, 1),
         weave_h(1, (3,)) + [("q_h", 0), ("q_h", 1)],
-        scale(1, 1) + [("q_tok", 0, 1, 1)] + token_side(1, 0)[:2],
-        token_side(1, 0)[2:],
+        scale(1, 1) + [("q_tok", 0, 1, 1)] + token_side(1, 0)[:1],
+        token_side(1, 0)[1:],
     ]
     for n in range(6):
         vector += [("q_w",) + w_halves[n + 2], ("q_feat",) + passes[n + AHEAD]] + fill[n]
@@ -138,7 +138,7 @@ def buffers_of(job, loads):
         "load_w": lambda: (("w_raw",) + a, []),
         "load_h": lambda: (("h_raw",) + a, []),
         "identity": lambda: (("identity",), []),
-        "warm": lambda: (("unread",), [("p_raw",), ("identity",)]),
+        "warm": lambda: (("unread",), [("identity",)]),
         "flip_dz": lambda: (("bank",) + job, [("dz",) + a[:2], ("identity",)]),
         "flip_w": lambda: (("bank",) + job, [("w_raw",) + a[:2], ("identity",)]),
         "drain_dz": lambda: (("dz_flip",) + a[:3], [("bank", "flip_dz") + a]),
@@ -268,9 +268,9 @@ def tile_enhancedmathematicalreasoning_pa_v_kernel(
             elif kind == "warm":
                 if (written, "") not in tiles:
                     tiles[written, ""] = psum.tile([P, HALF], F32, name="sum03", tag="sum03")
-                any_column = src[:, 0, 0:1].bitcast(BF16)[:, 1:2].to_broadcast([P, P])
-                any_rows = tiles[read[1], ""][:].bitcast(BF16).unsqueeze(1).to_broadcast([P, 2, 2 * P])
-                nc.tensor.matmul(out=tiles[written, ""][:], lhsT=any_column, rhs=any_rows, start=True, stop=True)
+                halves = src[:].bitcast(BF16)
+                twice = halves.unsqueeze(1).to_broadcast([P, 2, 2 * P])
+                nc.tensor.matmul(out=tiles[written, ""][:], lhsT=halves[:, :P], rhs=twice, start=True, stop=True)
             elif kind == "scale":
                 e, g, s = job[1:]
                 row = src[:, span(s - read[0][2], HO)]

@@ -215,7 +215,7 @@ def tile_enhancedmathematicalreasoning_pa_v_kernel(
                 if item[0] in ("bank", "sum0"):
                     tiles[item, part] = psum.tile(shape, dtype, name=tag, tag=tag)
                 else:
-                    tiles[item, part] = sbuf.tile(shape, dtype, name=tag, tag=tag, align_bytes=64)
+                    tiles[item, part] = sbuf.tile(shape, dtype, name=tag, tag=tag, align_bytes=256)
             return tiles[item, part]
 
         def copy(job, out, in_):

@@ -18,7 +18,8 @@ FLOPS = 2 * 2 * T * H * E * HO
 BYTES = 2 * (T * H + E * H * HO + T * HO) + 4 * T * E + 4 * (T * H + E * H * HO)
 
 DEPTH = {"w_raw": 4, "dz": 7, "dz_flip": 4, "w_flip": 3, "dz_weave": 2, "dz_feat": 5, "dz_tok": 4,
-         "bank": 4, "sum0": 4, "stage": 8}
+         "bank": 4, "sum0": 4}
+FRESH = 6
 AHEAD = 3
 SPACER = 2
 WARM_FIRST = 5
@@ -158,17 +159,7 @@ def buffers_of(job, loads):
     return table[kind]()
 
 
-def tile_enhancedmathematicalreasoning_pa_v_kernel(
-    tc, hidden_states, op_logits, We, be, op_w, grad_out, out_0, out_1
-):
-    nc = tc.nc
-    h_view = hidden_states.flatten_outer_dims().rearrange("(g p s) i -> g p (s i)", g=2, s=SLOTS)
-    g_view = grad_out.flatten_outer_dims().rearrange("(g p s) j -> g p (s j)", g=2, s=SLOTS)
-    p_view = op_w.flatten_outer_dims().rearrange("(g p s) e -> p g (s e)", g=2, s=SLOTS)
-    w_view = We.rearrange("e (a p) j -> e p a j", p=P)
-    out0_view = out_0.flatten_outer_dims().rearrange("(g p s) i -> g s p i", g=2, s=SLOTS)
-    out1_view = out_1.rearrange("e (m p) j -> e m p j", p=P)
-
+def plan():
     loads, tensor, vector, scalar, stores = job_lists()
     queues = [loads[:1] + [("identity",)] + loads[1:] + stores, tensor, vector, scalar]
     jobs = [job for queue in queues for job in queue]
@@ -180,7 +171,7 @@ def tile_enhancedmathematicalreasoning_pa_v_kernel(
             readers.setdefault(item, []).append(job)
 
     turns = {}
-    for item in [uses[job][1][0] for job in stores] + [uses[job][0] for job in loads + tensor + vector + scalar]:
+    for item in [uses[job][0] for job in loads + tensor + vector + scalar]:
         if item[0] in DEPTH and item not in turns.setdefault(item[0], []):
             turns[item[0]].append(item)
     place, replaces = {}, {}
@@ -190,7 +181,16 @@ def tile_enhancedmathematicalreasoning_pa_v_kernel(
             if n >= DEPTH[kind]:
                 replaces[item] = items[n - DEPTH[kind]]
 
-    def needs(job):
+    hosts = [(("fresh", n), 1) for n in range(FRESH)] + [(("g_raw", 0, s, 1), 1) for s in range(SLOTS)]
+    hosts += [(item, 2) for item in turns["w_raw"][-DEPTH["w_raw"]:] + turns["w_flip"][-DEPTH["w_flip"]:]]
+    hosts += [((kind, g), 2) for kind in ("h_raw", "h_weave") for g in (0, 1)] + [(("dz", 0, 1), 4), (("dz", 1, 0), 4)]
+    rooms = [(host, count, n) for host, count in hosts for n in range(count)]
+    room = {uses[job][1][0]: rooms[n] for n, job in enumerate(stores)}
+    for item in room:
+        if room[item][0][0] != "fresh":
+            replaces[item] = room[item][0]
+
+    def needs_of(job):
         written, read = uses[job]
         before = list(readers[replaces[written]]) if written in replaces else []
         for item in read:
@@ -204,14 +204,42 @@ def tile_enhancedmathematicalreasoning_pa_v_kernel(
             before.extend(makers)
         return before
 
+    needs = {job: needs_of(job) for job in jobs}
+    return {"queues": queues, "uses": uses, "place": place, "needs": needs, "stores": stores, "room": room}
+
+
+def tile_enhancedmathematicalreasoning_pa_v_kernel(
+    tc, hidden_states, op_logits, We, be, op_w, grad_out, out_0, out_1
+):
+    nc = tc.nc
+    h_view = hidden_states.flatten_outer_dims().rearrange("(g p s) i -> g p (s i)", g=2, s=SLOTS)
+    g_view = grad_out.flatten_outer_dims().rearrange("(g p s) j -> g p (s j)", g=2, s=SLOTS)
+    p_view = op_w.flatten_outer_dims().rearrange("(g p s) e -> p g (s e)", g=2, s=SLOTS)
+    w_view = We.rearrange("e (a p) j -> e p a j", p=P)
+    out0_view = out_0.flatten_outer_dims().rearrange("(g p s) i -> g s p i", g=2, s=SLOTS)
+    out1_view = out_1.rearrange("e (m p) j -> e m p j", p=P)
+
+    work = plan()
+    queues, uses, place, needs, stores = (work[key] for key in ("queues", "uses", "place", "needs", "stores"))
+    vector, room = queues[2], work["room"]
+
     with ExitStack() as ctx:
         sbuf = ctx.enter_context(tc.tile_pool(name="sbuf", bufs=1))
         psum = ctx.enter_context(tc.psum_pool(name="psum", bufs=1))
         tiles = {}
 
+        def tag_of(item):
+            return f"{item[0]}{place[item]}" if item in place else "".join(str(x) for x in item)
+
+        def stage_of(item):
+            host, count, n = room[item]
+            if (host, "stage") not in tiles:
+                tiles[host, "stage"] = sbuf.tile([P, count * HALF], F32, name=tag_of(host), tag=tag_of(host), align_bytes=256)
+            return tiles[host, "stage"][:, n * HALF : (n + 1) * HALF]
+
         def tile_of(item, shape, dtype, part=""):
             if (item, part) not in tiles:
-                tag = f"{item[0]}{place[item]}{part}" if item in place else "".join(str(x) for x in item) + part
+                tag = tag_of(item) + part
                 if item[0] in ("bank", "sum0"):
                     tiles[item, part] = psum.tile(shape, dtype, name=tag, tag=tag)
                 else:
@@ -250,7 +278,7 @@ def tile_enhancedmathematicalreasoning_pa_v_kernel(
         def emit(job):
             kind = job[0]
             written, read = uses[job]
-            src = tiles[read[0], ""] if read else None
+            src = stage_of(read[0]) if kind == "store" else tiles[read[0], ""] if read else None
             if kind == "identity":
                 make_identity(nc, tile_of(written, [P, P], F32)[:])
             elif kind == "load_p":
@@ -325,9 +353,9 @@ def tile_enhancedmathematicalreasoning_pa_v_kernel(
                 pieces = LAST_PIECES if ("store",) + job == stores[-1] else 1
                 for n in range(pieces):
                     cols = span(n, HALF // pieces)
-                    copy(job, tile_of(written, [P, HALF], F32)[:, cols], src[:, cols])
+                    copy(job, stage_of(written)[:, cols], src[:, cols])
             elif kind == "drain1":
-                copy(job, tile_of(written, [P, HALF], F32)[:].rearrange("p (w u x) -> p w u x", u=2, x=2),
+                copy(job, stage_of(written).rearrange("p (w u x) -> p w u x", u=2, x=2),
                      src[:].rearrange("p (u w x) -> p w u x", u=2, x=2))
             else:
                 if job[1] == "drain0":
@@ -342,10 +370,10 @@ def tile_enhancedmathematicalreasoning_pa_v_kernel(
         with tc.manual_schedule():
             done = set()
             heads = [0] * len(queues)
-            while len(done) < len(jobs):
+            while len(done) < len(uses):
                 count = len(done)
                 for q, queue in enumerate(queues):
-                    while heads[q] < len(queue) and all(other in done for other in needs(queue[heads[q]])):
+                    while heads[q] < len(queue) and all(other in done for other in needs[queue[heads[q]]]):
                         emit(queue[heads[q]])
                         done.add(queue[heads[q]])
                         heads[q] = heads[q] + 1

@@ -14,198 +14,230 @@ P = 128
 E, H, HO, T = 4, 512, 1024, 1024
 SLOTS = 4
 HALF = 512
+BANKS = 8
 FLOPS = 2 * 2 * T * H * E * HO
 BYTES = 2 * (T * H + E * H * HO + T * HO) + 4 * T * E + 4 * (T * H + E * H * HO)
-
-DEPTH = {"w_raw": 4, "dz": 7, "dz_flip": 4, "w_flip": 3, "dz_weave": 2, "dz_feat": 5, "dz_tok": 4,
-         "bank": 4, "sum0": 4}
-FRESH = 6
-AHEAD = 3
-SPACER = 2
-WARM_FIRST = 5
+FIRST = 2
+DEPTH = {"w_raw": 4, "dz": 8, "first_flip": 4, "slot_flip": 2, "slot_codes": 2, "first_codes": 7, "w_flip": 5, "woven": 2,
+         "t_codes": 3, "stage": 3}
+STAGE_IN = ("stage", "first_flip", "w_flip", "w_raw")
+WARM_FIRST = 3
 H_PIECES = 4
-LAST_PIECES = 2
 
 
 def job_lists():
-    def scale(e, g, slots=range(SLOTS)):
-        return [("scale", e, g, s) for s in slots]
+    both = (0, 1)
+    halves = [(e, c) for e in range(E) for c in both]
 
-    def flip_dz(e, g, c, pairs=(0, 1)):
-        return [("flip_dz", e, g, c, pair) for pair in pairs]
+    def scale(experts, slots, cs=both):
+        return [("scale", e, n, cs) for e in experts for n in slots]
 
-    def flip_w(e, c):
-        return [("flip_w", e, c, pair) for pair in (0, 1)]
+    def flip_w(k, rows=both):
+        return [("flip_w",) + halves[k] + (x,) for x in rows]
 
-    def mm0(e, g, c):
-        return [("mm0", e, g, c, s) for s in range(SLOTS)]
+    def flip_z(e, n):
+        return [("flip_z", (e, n, 0), (e, n, 1))]
 
-    def mm1(e, c):
-        return [("mm1", e, c, m, g) for m in range(H // P) for g in (0, 1)]
+    def passes(k, rows=both, slots=range(FIRST)):
+        return [("mm0",) + halves[k] + (n, rows) for n in slots]
 
-    def weave(e, g, c, us=(0, 1)):
-        return [("weave", e, g, c, us)]
+    def q_w(k, rows=both):
+        return [("q_w",) + halves[k] + (x,) for x in rows]
 
-    def weave_h(g, pieces):
+    def q_z(e, n):
+        return [("q_z", ("first", e, n), 0, 2)]
+
+    def slot_flips(n):
+        return [("flip_z", (e, n, 0), (e, n, 1)) for e in range(E)]
+
+    def q_slot(n, parts=both):
+        return [("q_z", ("slot", n), E * x, E * x + E) for x in parts]
+
+    def weave(k, gs=both):
+        return [("weave",) + halves[k] + (g,) for g in gs]
+
+    def q_t(k, gs=both):
+        return [("q_t",) + halves[k] + ((g,),) for g in gs]
+
+    def groups(k, ms=range(H // P)):
+        return [("mm1",) + halves[k] + (m, g) for m in ms for g in both]
+
+    def weave_h(g, pieces=range(H_PIECES)):
         return [("weave_h", g, n) for n in pieces]
 
-    def token_side(e, c):
-        return weave(e, 0, c) + weave(e, 1, c) + [("q_tok", e, 0, c), ("q_tok", e, 1, c)]
+    def drain(jobs):
+        return drain_of(jobs[-1])
 
-    passes = [(e, g, c) for g in (0, 1) for e in range(E) for c in (0, 1)]
-    w_halves = [(e, c) for e in range(E) for c in (0, 1)]
+    lo, hi = (0,), (1,)
+    loads = [("load_p",), ("load_w", 0, 0, lo), ("load_g", (0,), both), ("load_w", 0, 1, lo), ("load_g", (1,), both)]
+    loads += [("load_w", 0, 0, hi), ("load_w", 0, 1, hi), ("load_w", 1, 0, both), ("load_g", (2, 3), both), ("load_w", 1, 1, both)]
+    loads += [("load_w", 2, 0, both), ("load_w", 2, 1, both), ("load_h", 0), ("load_g", (4, 5), both), ("load_g", (6, 7), both)]
+    loads += [("load_w", 3, 0, both), ("load_h", 1), ("load_w", 3, 1, both)]
 
-    loads = [("load_p",), ("load_g", 0, 0, 1), ("load_g", 0, 1, 1), ("load_w", 0, 0), ("load_g", 0, 2, 1)]
-    loads += [("load_g", 0, 3, 1), ("load_w", 0, 1), ("load_w", 1, 0), ("load_h", 0), ("load_w", 1, 1)]
-    loads += [("load_g", 1, 0, 2), ("load_g", 1, 2, 2), ("load_w", 2, 0), ("load_w", 2, 1), ("load_h", 1)]
-    loads += [("load_w", 3, 0), ("load_w", 3, 1)]
-
+    whole = [[("mm0",) + halves[k] + (n, both) for k in range(2 * E)] for n in range(2 * SLOTS - 1)]
+    last = [[("mm0",) + halves[k] + (2 * SLOTS - 1, rows) for k in range(2 * E)] for rows in (lo, hi)]
     tensor = [("warm", n) for n in range(WARM_FIRST)]
-    head = [flip_dz(0, 0, 0, (0,)) + flip_dz(0, 0, 1, (0,)), flip_w(0, 0),
-            flip_dz(0, 0, 0, (1,)) + flip_dz(0, 0, 1, (1,)), flip_w(0, 1) + flip_dz(*passes[2])]
-    for n, banks in enumerate(head):
-        tensor += banks + ([("warm", WARM_FIRST + n)] if n + 1 < len(head) else [])
-    for n in range(6):
-        tensor += mm0(*passes[n]) + flip_w(*w_halves[n + 2]) + flip_dz(*passes[n + AHEAD])
-    for e in range(E):
-        first, second = mm0(*passes[2 * e + 6]), mm0(*passes[2 * e + 7])
-        flips = [job for item in passes[2 * e + 6 + AHEAD : 2 * e + 8 + AHEAD] for job in flip_dz(*item)]
-        if e == 0:
-            tensor += first[:SPACER] + mm1(e, 0) + first[SPACER:] + flips
-            tensor += second[:SPACER] + mm1(e, 1) + second[SPACER:]
-        elif e < E - 1:
-            tensor += mm1(e, 0) + first + mm1(e, 1) + second[:SPACER] + flips + second[SPACER:]
-        else:
-            tensor += mm1(e, 0) + first[:SPACER] + flips + first[SPACER:] + mm1(e, 1)
-    tensor += [("mm0",) + item + (s,) for s in range(SLOTS) for item in passes[13:]]
+    tensor += flip_w(0, lo) + [("warm", 3)] + flip_z(0, 0) + flip_w(0, hi) + flip_z(1, 0) + [("warm", 4)] + flip_z(0, 1) + flip_z(2, 0) + flip_w(1)
+    tensor += passes(0) + flip_z(1, 1) + flip_z(3, 0) + flip_w(2, lo) + flip_w(3, lo)
+    tensor += passes(1) + flip_w(2, hi) + flip_w(3, hi) + flip_z(2, 1) + flip_z(3, 1) + flip_w(4, lo)
+    tensor += passes(2) + flip_w(5, lo) + flip_w(4, hi) + flip_w(5, hi) + passes(3) + slot_flips(2) + passes(4) + passes(5)
+    tensor += flip_w(6, lo) + flip_w(7, lo) + slot_flips(3)[:2] + whole[2][:4] + flip_w(6, hi) + flip_w(7, hi) + slot_flips(3)[2:]
+    tensor += whole[2][4:6] + whole[3][:4] + passes(6) + passes(7) + whole[2][6:] + groups(0, (0, 1))
+    tensor += slot_flips(4) + whole[3][4:6] + groups(0, (2, 3)) + whole[3][6:] + groups(1)
+    tensor += slot_flips(5) + whole[4][:4] + groups(2) + whole[4][4:] + groups(3) + whole[5][:4]
+    tensor += slot_flips(6) + whole[5][4:] + groups(4) + whole[6][:2]
+    tensor += slot_flips(7) + whole[6][2:4] + groups(5) + whole[6][4:] + groups(6)
+    tensor += last[0][:4] + last[1][:4] + groups(7) + last[0][4:] + last[1][4:]
 
-    vector = [job for e in range(E) for job in scale(e, 0, (0, 1))]
-    vector += [job for e in range(E - 1) for job in scale(e, 0, (2, 3))]
-    vector += [("q_w", 0, 0), ("q_feat", 0, 0, 0), ("q_feat", 0, 0, 1)] + weave(0, 0, 0)
-    vector += [("q_w", 0, 1), ("q_tok", 0, 0, 0), ("q_feat", 1, 0, 0)] + weave(0, 0, 1)
-    fill = [
-        [("q_tok", 0, 0, 1)] + scale(0, 1),
-        scale(3, 0, (2, 3)) + weave(0, 1, 0),
-        [("q_tok", 0, 1, 0)] + weave(0, 1, 1),
-        weave_h(1, (3,)) + [("q_h", 0), ("q_h", 1)],
-        scale(1, 1) + [("q_tok", 0, 1, 1)] + token_side(1, 0)[:1],
-        token_side(1, 0)[1:],
-    ]
-    for n in range(6):
-        vector += [("q_w",) + w_halves[n + 2], ("q_feat",) + passes[n + AHEAD]] + fill[n]
-    vector += token_side(1, 1) + [("q_feat",) + passes[9]] + scale(2, 1)
-    vector += token_side(2, 0) + [("q_feat",) + passes[10]] + token_side(2, 1) + [("q_feat",) + passes[11]]
-    vector += scale(3, 1) + weave(3, 0, 0, (1,)) + token_side(3, 0)[1:] + [("q_feat",) + passes[12]]
-    vector += token_side(3, 1) + [("q_feat",) + item for item in passes[13:]]
-    vector += [("drain0", 1, 1), ("drain0", 1, 3)]
+    vector = scale(range(E), (0,)) + q_w(0, lo) + scale([0], (1,)) + q_z(0, 0)
+    vector += scale([1], (1,)) + q_w(0, hi) + scale([2], (1,)) + q_z(1, 0) + q_z(0, 1) + scale([3], (1,))
+    vector += q_z(2, 0) + q_w(1) + scale([0], (2, 3)) + q_z(1, 1) + scale([1], (2,)) + q_z(3, 0)
+    vector += scale([2], (2,)) + q_w(2, lo) + scale([3], (2,)) + q_w(3, lo) + scale([1], (3,)) + q_w(2, hi) + q_w(3, hi) + weave(0, lo) + q_z(2, 1) + scale([2], (3,)) + q_z(3, 1)
+    vector += scale([3], (3,)) + q_w(4, lo) + q_t(0, lo) + q_w(5, lo) + q_w(4, hi) + scale([0], (4,)) + q_w(5, hi) + scale([0], (5,))
+    vector += scale([0], (6, 7)) + weave(1, lo) + q_slot(2, lo) + weave(0, hi) + q_slot(2, hi)
+    vector += q_w(6, lo) + q_w(7, lo) + q_t(0, hi) + q_slot(3, lo) + [("q_h", 0)] + scale([1, 2], (4,)) + q_w(6, hi) + scale([3], (4,)) + q_w(7, hi)
+    vector += weave(1, hi) + [("q_h", 1)] + scale([1, 2, 3], (5,)) + q_slot(3, hi) + q_t(1) + scale([1], (6, 7)) + weave(2) + q_slot(4)
+    vector += q_t(2) + weave(3) + scale([2, 3], (6,)) + q_t(3) + q_slot(5) + scale([2], (7,))
+    vector += weave(4) + scale([3], (7,)) + q_t(4) + weave(5) + q_slot(6) + q_t(5) + weave(6) + q_t(6) + q_slot(7, lo)
+    vector += weave(7) + q_t(7) + q_slot(7, hi) + [drain(groups(7, (2,))), drain(last[0])]
 
     behind = {
-        ("drain_dz", 1, 0, 0, 1): weave_h(0, (0,)),
-        ("drain_dz", 1, 0, 1, 1): weave_h(0, (1, 2)),
-        ("drain_dz", 2, 0, 0, 1): weave_h(0, (3,)),
-        ("drain_dz", 2, 0, 1, 1): weave_h(1, (0, 1)),
-        ("drain_dz", 3, 0, 0, 1): weave_h(1, (2,)),
-        ("drain1", 0, 1, 3): [("drain0", 0, 0), ("drain0", 0, 1)],
-        ("drain1", 2, 0, 3): weave(3, 0, 0, (0,)),
+        drain(flip_w(5, hi)): weave_h(0, (0, 1)),
+        drain(slot_flips(2)): weave_h(0, (2, 3)),
+        drain(slot_flips(3)[:2]): weave_h(1, (0, 1)),
+        drain(flip_w(7, hi)): weave_h(1, (2, 3)),
     }
+
     closing = [drain_of(job) for job in tensor if drain_of(job)]
-    moved = [job for extra in behind.values() for job in extra]
-    scalar = [job for drain in closing if drain not in moved for job in [drain] + behind.get(drain, [])]
+    scalar = [job for x in closing for job in [x] + behind.get(x, [])]
     stores = [("store",) + job for job in scalar if job[0] in ("drain0", "drain1")]
     scalar = [job for job in scalar if job not in vector]
     return loads, tensor, vector, scalar, stores
 
 
+def place_of_row(e, n, c):
+    if n < FIRST:
+        return ("first", e, n), c
+    return ("slot", n), 2 * e + c
+
+
+def sum_of(job):
+    n, halves = job[3:]
+    return (n,), halves
+
+
 def drain_of(job):
-    if job[0] == "flip_dz":
-        return ("drain_dz",) + job[1:]
+    if job[0] == "flip_z":
+        return ("drain_z",) + job[1:]
     if job[0] == "flip_w":
         return ("drain_w",) + job[1:]
     if job[0] == "mm1" and job[4] == 1:
         return ("drain1",) + job[1:4]
-    if job[0] == "mm0" and job[1] == E - 1 and job[3] == 1:
-        return ("drain0", job[2], job[4])
+    if job[0] == "mm0" and job[1:3] == (E - 1, 1):
+        return ("drain0",) + sum_of(job)
     return None
 
 
-def buffers_of(job, loads):
+def uses_of(job, loads):
     kind, a = job[0], job[1:]
+    whole = (0,)
+    ident = (("identity",), whole)
+    if kind.startswith("load_"):
+        return [((kind[5:] + "_raw",) + a, whole)], []
+    if kind == "identity":
+        return [ident], []
+    if kind == "warm":
+        return [(("bank", "unread"), whole)], [ident]
     if kind == "scale":
-        g_piece = [("g_raw",) + x[1:] for x in loads if x[0] == "load_g" and x[1] == a[1] and x[2] <= a[2] < x[2] + x[3]]
-        return ("dz",) + a[:2], g_piece + [("p_raw",)]
-    table = {
-        "load_p": lambda: (("p_raw",), []),
-        "load_g": lambda: (("g_raw",) + a, []),
-        "load_w": lambda: (("w_raw",) + a, []),
-        "load_h": lambda: (("h_raw",) + a, []),
-        "identity": lambda: (("identity",), []),
-        "warm": lambda: (("unread",), [("identity",)]),
-        "flip_dz": lambda: (("bank",) + job, [("dz",) + a[:2], ("identity",)]),
-        "flip_w": lambda: (("bank",) + job, [("w_raw",) + a[:2], ("identity",)]),
-        "drain_dz": lambda: (("dz_flip",) + a[:3], [("bank", "flip_dz") + a]),
-        "drain_w": lambda: (("w_flip",) + a[:2], [("bank", "flip_w") + a]),
-        "weave": lambda: (("dz_weave", a[0], a[2]), [("dz",) + a[:2]]),
-        "weave_h": lambda: (("h_weave", a[0]), [("h_raw", a[0])]),
-        "q_feat": lambda: (("dz_feat",) + a, [("dz_flip",) + a]),
-        "q_tok": lambda: (("dz_tok", a[0], a[2]), [("dz_weave", a[0], a[2])]),
-        "q_w": lambda: (("w_codes",) + a, [("w_flip",) + a]),
-        "q_h": lambda: (("h_codes",) + a, [("h_weave",) + a]),
-        "mm0": lambda: (("sum0", a[1], a[3]), [("dz_feat",) + a[:3], ("w_codes", a[0], a[2])]),
-        "mm1": lambda: (("bank", "mm1") + a[:3], [("dz_tok",) + a[:2], ("h_codes", a[3])]),
-        "drain0": lambda: (("stage",) + job, [("sum0",) + a]),
-        "drain1": lambda: (("stage",) + job, [("bank", "mm1") + a]),
-        "store": lambda: (None, [("stage",) + a]),
-    }
-    return table[kind]()
+        e, n, cs = a
+        piece = [x for x in loads if x[0] == "load_g" and n in x[1] and cs[0] in x[2]][0]
+        return [(("dz", e, n // SLOTS), [(n, c) for c in cs])], [(("g_raw",) + piece[1:], whole), (("p_raw",), whole)]
+    if kind == "flip_w":
+        piece = [x for x in loads if x[0] == "load_w" and x[1:3] == (a[0], a[2]) and a[1] in x[3]][0]
+        return [(("bank",) + job, whole)], [(("w_raw",) + piece[1:], whole), ident]
+    if kind == "drain_w":
+        return [(("w_flip",) + a, whole)], [(("bank", "flip_w") + a, whole)]
+    if kind == "q_w":
+        return [(("w_codes",) + a[:2], a[2:])], [(("w_flip",) + a, whole)]
+    if kind == "flip_z":
+        return [(("bank",) + job, whole)], [(("dz", e, n // SLOTS), [(n, c)]) for e, n, c in a] + [ident]
+    if kind == "drain_z":
+        key, row = place_of_row(*a[0])
+        return [((key[0] + "_flip",) + key, (row, row + 1))], [(("bank", "flip_z") + a, whole)]
+    if kind == "q_z":
+        rows = range(a[1], a[2])
+        return [((a[0][0] + "_codes",) + a[0], rows)], [((a[0][0] + "_flip",) + a[0], rows)]
+    if kind == "mm0":
+        e, c, n, halves = a
+        key, row = place_of_row(e, n, c)
+        return [(("bank", "sum") + sum_of(job), whole)], [((key[0] + "_codes",) + key, (row,)), (("w_codes", e, c), halves)]
+    if kind == "weave":
+        e, c, g = a
+        return [(("woven", e, c), (g,))], [(("dz", e, g), [(SLOTS * g + s, c) for s in range(SLOTS)])]
+    if kind == "q_t":
+        return [(("t_codes",) + a[:2], a[2])], [(("woven",) + a[:2], a[2])]
+    if kind == "weave_h":
+        return [(("h_woven", a[0]), (a[1],))], [(("h_raw", a[0]), whole)]
+    if kind == "q_h":
+        return [(("h_codes",) + a, whole)], [(("h_woven",) + a, range(H_PIECES))]
+    if kind == "mm1":
+        e, c, m, g = a
+        return [(("bank", "mm1", e, c, m), whole)], [(("t_codes", e, c), (g,)), (("h_codes", g), whole)]
+    if kind == "drain0":
+        return [(("stage",) + job, whole)], [(("bank", "sum") + a, whole)]
+    if kind == "drain1":
+        return [(("stage",) + job, whole)], [(("bank", "mm1") + a, whole)]
+    return [], [(("stage",) + a, whole)]
 
 
 def plan():
     loads, tensor, vector, scalar, stores = job_lists()
     queues = [loads[:1] + [("identity",)] + loads[1:] + stores, tensor, vector, scalar]
     jobs = [job for queue in queues for job in queue]
-    uses = {job: buffers_of(job, loads) for job in jobs}
+    assert len(set(jobs)) == len(jobs)
+    uses = {job: uses_of(job, loads) for job in jobs}
     writers, readers = {}, {}
     for job in jobs:
-        writers.setdefault(uses[job][0], []).append(job)
-        for item in uses[job][1]:
+        for item, parts in uses[job][0]:
+            writers.setdefault(item, []).append((job, set(parts)))
+        for item, parts in uses[job][1]:
             readers.setdefault(item, []).append(job)
 
-    turns = {}
-    for item in [uses[job][0] for job in loads + tensor + vector + scalar]:
-        if item[0] in DEPTH and item not in turns.setdefault(item[0], []):
-            turns[item[0]].append(item)
-    place, replaces = {}, {}
-    for kind, items in turns.items():
-        for n, item in enumerate(items):
-            place[item] = n % DEPTH[kind]
-            if n >= DEPTH[kind]:
-                replaces[item] = items[n - DEPTH[kind]]
+    place, holder, replaces, count = {}, {}, {}, {}
 
-    hosts = [(("fresh", n), 1) for n in range(FRESH)] + [(("g_raw", 0, s, 1), 1) for s in range(SLOTS)]
-    hosts += [(item, 2) for item in turns["w_raw"][-DEPTH["w_raw"]:] + turns["w_flip"][-DEPTH["w_flip"]:]]
-    hosts += [((kind, g), 2) for kind in ("h_raw", "h_weave") for g in (0, 1)] + [(("dz", 0, 1), 4), (("dz", 1, 0), 4)]
-    rooms = [(host, count, n) for host, count in hosts for n in range(count)]
-    room = {uses[job][1][0]: rooms[n] for n, job in enumerate(stores)}
-    for item in room:
-        if room[item][0][0] != "fresh":
-            replaces[item] = room[item][0]
+    def put(item, spot):
+        place[item] = spot
+        if spot in holder:
+            replaces[item] = holder[spot]
+        holder[spot] = item
+
+    spots = {kind: [f"{kind}{n}" for n in range(depth)] for kind, depth in DEPTH.items()}
+    spots["stage"] = [spot for kind in STAGE_IN for spot in spots[kind]]
+    drains = [store[1:] for store in stores]
+    for job in [job for job in loads + vector + scalar if job not in drains] + drains:
+        for item, parts in uses[job][0]:
+            if item[0] in DEPTH and item not in place:
+                put(item, spots[item[0]][count.get(item[0], 0) % len(spots[item[0]])])
+                count[item[0]] = count.get(item[0], 0) + 1
+    free = [f"bank{n}" for n in range(BANKS)]
+    last_warm = [job for job in tensor if job[0] == "warm"][-1:]
+    for job in tensor:
+        item = uses[job][0][0][0]
+        if item not in place:
+            put(item, free.pop(-1 if job[0] == "warm" else 0))
+        if drain_of(job) or job in last_warm:
+            free.append(place[item])
 
     def needs_of(job):
-        written, read = uses[job]
-        before = list(readers[replaces[written]]) if written in replaces else []
-        for item in read:
-            makers = writers[item]
-            if item[0] == "dz" and job[0] == "flip_dz":
-                makers = [other for other in makers if other[3] // 2 == job[4]]
-            if item[0] == "dz_weave":
-                makers = [other for other in makers if other[2] == job[2]]
-            if item[0] == "dz_tok":
-                makers = [other for other in makers if other[2] == job[4]]
-            before.extend(makers)
+        before = []
+        for item, parts in uses[job][0]:
+            if item in replaces:
+                before.extend(readers.get(replaces[item], []) + [other for other, p in writers[replaces[item]]])
+        for item, parts in uses[job][1]:
+            before.extend(other for other, p in writers[item] if p & set(parts))
         return before
 
-    needs = {job: needs_of(job) for job in jobs}
-    return {"queues": queues, "uses": uses, "place": place, "needs": needs, "stores": stores, "room": room}
+    return queues, uses, place, {job: needs_of(job) for job in jobs}
 
 
 def tile_enhancedmathematicalreasoning_pa_v_kernel(
@@ -213,38 +245,32 @@ def tile_enhancedmathematicalreasoning_pa_v_kernel(
 ):
     nc = tc.nc
     h_view = hidden_states.flatten_outer_dims().rearrange("(g p s) i -> g p (s i)", g=2, s=SLOTS)
-    g_view = grad_out.flatten_outer_dims().rearrange("(g p s) j -> g p (s j)", g=2, s=SLOTS)
+    g_view = grad_out.flatten_outer_dims().rearrange("(g p s) j -> g p s j", g=2, s=SLOTS)
     p_view = op_w.flatten_outer_dims().rearrange("(g p s) e -> p g (s e)", g=2, s=SLOTS)
     w_view = We.rearrange("e (a p) j -> e p a j", p=P)
-    out0_view = out_0.flatten_outer_dims().rearrange("(g p s) i -> g s p i", g=2, s=SLOTS)
+    out0_view = out_0.flatten_outer_dims().rearrange("(g p s) i -> g p s i", g=2, s=SLOTS)
     out1_view = out_1.rearrange("e (m p) j -> e m p j", p=P)
-
-    work = plan()
-    queues, uses, place, needs, stores = (work[key] for key in ("queues", "uses", "place", "needs", "stores"))
-    vector, room = queues[2], work["room"]
+    queues, uses, place, needs = plan()
+    vector = queues[2]
 
     with ExitStack() as ctx:
         sbuf = ctx.enter_context(tc.tile_pool(name="sbuf", bufs=1))
         psum = ctx.enter_context(tc.psum_pool(name="psum", bufs=1))
         tiles = {}
 
-        def tag_of(item):
-            return f"{item[0]}{place[item]}" if item in place else "".join(str(x) for x in item)
-
-        def stage_of(item):
-            host, count, n = room[item]
-            if (host, "stage") not in tiles:
-                tiles[host, "stage"] = sbuf.tile([P, count * HALF], F32, name=tag_of(host), tag=tag_of(host), align_bytes=256)
-            return tiles[host, "stage"][:, n * HALF : (n + 1) * HALF]
-
-        def tile_of(item, shape, dtype, part=""):
+        def tile_of(item, width, dtype, part=""):
             if (item, part) not in tiles:
-                tag = tag_of(item) + part
-                if item[0] in ("bank", "sum0"):
-                    tiles[item, part] = psum.tile(shape, dtype, name=tag, tag=tag)
+                tag = place[item] if item in place else "".join(str(x) for x in item)
+                tag = tag.replace("(", "").replace(")", "").replace(", ", "").replace(",", "") + part
+                if item[0] == "bank":
+                    tiles[item, part] = psum.tile([P, width], dtype, name=tag, tag=tag)
                 else:
-                    tiles[item, part] = sbuf.tile(shape, dtype, name=tag, tag=tag, align_bytes=256)
+                    tiles[item, part] = sbuf.tile([P, width], dtype, name=tag, tag=tag,
+                                                  align_bytes=256 if "codes" in tag else 64)
             return tiles[item, part]
+
+        def span(n, width, count=1):
+            return slice(n * width, (n + count) * width)
 
         def copy(job, out, in_):
             if job in vector:
@@ -256,116 +282,116 @@ def tile_enhancedmathematicalreasoning_pa_v_kernel(
             copy(job, dst.rearrange("p (o w x s) -> p o w s x", o=2, x=4, s=SLOTS),
                  src.rearrange("p o (w x) s -> p o w s x", x=4))
 
+        def mx_operand(item, cols, fmt):
+            both = tiles[item, ""]
+            width = both.shape[1] // 5
+            return both[:, : 4 * width].bitcast(U32)[:, cols].bitcast(fmt), both[:, 4 * width :][:, cols]
+
         def quantize(item, width, cols, src, fmt):
-            codes = tile_of(item, [P, width], U32)
-            scales = tile_of(item, [P, width], U8, "_scales")
-            nc.vector.quantize_mx(out=codes[:, cols].bitcast(fmt), scales=scales[:, cols], in_=src)
+            tile_of(item, 5 * width, U8)
+            codes, scales = mx_operand(item, cols, fmt)
+            nc.vector.quantize_mx(out=codes, scales=scales, in_=src)
 
         def matmul_mx(out, lhs, lhs_cols, lhs_fmt, rhs, rhs_cols, rhs_fmt, start, stop):
-            nc.tensor.matmul_mx(
-                out=out,
-                lhsT=tiles[lhs, ""][:, lhs_cols].bitcast(lhs_fmt),
-                lhsT_scale=tiles[lhs, "_scales"][:, lhs_cols],
-                rhs=tiles[rhs, ""][:, rhs_cols].bitcast(rhs_fmt),
-                rhs_scale=tiles[rhs, "_scales"][:, rhs_cols],
-                start=start,
-                stop=stop,
-            )
+            lhs_codes, lhs_scales = mx_operand(lhs, lhs_cols, lhs_fmt)
+            rhs_codes, rhs_scales = mx_operand(rhs, rhs_cols, rhs_fmt)
+            nc.tensor.matmul_mx(out=out, lhsT=lhs_codes, lhsT_scale=lhs_scales, rhs=rhs_codes, rhs_scale=rhs_scales,
+                                start=start, stop=stop)
 
-        def span(n, width):
-            return slice(n * width, (n + 1) * width)
+        def flip(bank, blocks):
+            for n, block in enumerate(blocks):
+                nc.tensor.transpose(bank[:, span(n, P)], block, tiles[("identity",), ""][:])
 
         def emit(job):
-            kind = job[0]
-            written, read = uses[job]
-            src = stage_of(read[0]) if kind == "store" else tiles[read[0], ""] if read else None
+            kind, a = job[0], job[1:]
+            written = uses[job][0][0][0] if uses[job][0] else None
+            read = [item for item, parts in uses[job][1]]
+            src = tiles[read[0], ""] if read else None
             if kind == "identity":
-                make_identity(nc, tile_of(written, [P, P], F32)[:])
+                make_identity(nc, tile_of(written, P, F32)[:])
             elif kind == "load_p":
-                nc.scalar.dma_start(out=tile_of(written, [P, 2, SLOTS * E], F32)[:], in_=p_view)
+                nc.scalar.dma_start(out=tile_of(written, 2 * SLOTS * E, F32)[:].rearrange("p (g x) -> p g x", g=2), in_=p_view)
             elif kind == "load_g":
-                g, s, count = job[1:]
-                nc.sync.dma_start(out=tile_of(written, [P, count * HO], BF16)[:],
-                                  in_=g_view[g, :, s * HO : (s + count) * HO])
+                slots, cs = a
+                g, s = divmod(slots[0], SLOTS)
+                raw = tile_of(written, len(slots) * len(cs) * HALF, BF16)
+                nc.sync.dma_start(out=raw[:].rearrange("p (s j) -> p s j", s=len(slots)),
+                                  in_=g_view[g][:, s : s + len(slots), span(cs[0], HALF, len(cs))])
             elif kind == "load_w":
-                e, c = job[1:]
-                raw = tile_of(written, [P, SLOTS * HALF], BF16)
-                nc.sync.dma_start(out=raw[:].rearrange("p (a j) -> p a j", j=HALF), in_=w_view[e][:, :, span(c, HALF)])
+                e, half, cs = a
+                raw = tile_of(written, 2 * len(cs) * HALF, BF16)
+                nc.sync.dma_start(out=raw[:].rearrange("p (a j) -> p a j", a=2),
+                                  in_=w_view[e][:, span(half, 2), span(cs[0], HALF, len(cs))])
             elif kind == "load_h":
-                nc.sync.dma_start(out=tile_of(written, [P, SLOTS * H], BF16)[:], in_=h_view[job[1]])
+                nc.sync.dma_start(out=tile_of(written, SLOTS * H, BF16)[:], in_=h_view[a[0]])
             elif kind == "warm":
-                if (written, "") not in tiles:
-                    tiles[written, ""] = psum.tile([P, HALF], F32, name="sum03", tag="sum03")
                 halves = src[:].bitcast(BF16)
                 twice = halves.unsqueeze(1).to_broadcast([P, 2, 2 * P])
-                nc.tensor.matmul(out=tiles[written, ""][:], lhsT=halves[:, :P], rhs=twice, start=True, stop=True)
+                nc.tensor.matmul(out=tile_of(written, HALF, F32)[:], lhsT=halves[:, :P], rhs=twice, start=True, stop=True)
             elif kind == "scale":
-                e, g, s = job[1:]
-                row = src[:, span(s - read[0][2], HO)]
+                e, n, cs = a
+                slots, have = read[0][1:]
+                first = slots.index(n) * len(have) + have.index(cs[0])
+                row = tile_of(written, SLOTS * HO, BF16)[:, span(n % SLOTS, HO)].rearrange("p (u w x) -> p u w x", u=2, x=2)
                 nc.vector.tensor_scalar(
-                    out=tile_of(written, [P, SLOTS * HO], BF16)[:, span(s, HO)].rearrange("p (u w x) -> p u w x", u=2, x=2),
-                    in0=row.rearrange("p (w u x) -> p u w x", u=2, x=2),
-                    scalar1=tiles[read[1], ""][:, g, E * s + e : E * s + e + 1],
+                    out=row[:, :, span(cs[0], P, len(cs))],
+                    in0=src[:, span(first, HALF, len(cs))].rearrange("p (w u x) -> p u w x", u=2, x=2),
+                    scalar1=tiles[read[1], ""][:, span(E * n + e, 1)],
                     scalar2=None,
                     op0=mybir.AluOpType.mult,
                 )
-            elif kind in ("flip_dz", "flip_w"):
-                c, pair = job[-2:]
-                bank = tile_of(written, [P, HALF], F32)
+            elif kind == "flip_w":
                 words = src[:].bitcast(F32)
-                for r in range(2):
-                    for u in range(2):
-                        if kind == "flip_dz":
-                            start = (2 * pair + r) * (HO // 2) + u * (HO // 4) + c * P
-                            block = words[:, start : start + P]
-                        else:
-                            start = (2 * pair + r) * (HALF // 2) + u
-                            block = words[:, start : start + 2 * P - 1 : 2]
-                        nc.tensor.transpose(bank[:, span(2 * r + u, P)], block, tiles[read[1], ""][:])
-            elif kind in ("drain_dz", "drain_w"):
-                words = tile_of(written, [P, SLOTS * HALF], BF16)[:].bitcast(F32)[:, span(job[-1], HALF)]
+                have = read[0][3]
+                starts = [(r * len(have) + have.index(a[1])) * (HALF // 2) + u for r in range(2) for u in range(2)]
+                flip(tile_of(written, HALF, F32), [words[:, x : x + 2 * P - 1 : 2] for x in starts])
+            elif kind == "flip_z":
+                blocks = [tiles[item, ""][:].bitcast(F32)[:, span(4 * (n % SLOTS) + 2 * u + c, P)]
+                          for item, (e, n, c) in zip(read, a) for u in range(2)]
+                flip(tile_of(written, HALF, F32), blocks)
+            elif kind in ("drain_z", "drain_w"):
+                rows = 2 if kind == "drain_w" else 2 * E if written[1] == "slot" else FIRST
+                first = uses[job][0][0][1][0]
+                words = tile_of(written, rows * HALF, BF16)[:].bitcast(F32)[:, span(first, HALF // 2, 2)]
                 copy(job, words.rearrange("p (r n u) -> p r n u", r=2, u=2),
                      src[:].rearrange("p (r u n) -> p r n u", r=2, u=2))
+            elif kind == "q_z":
+                rows = 2 * E if a[0][0] == "slot" else FIRST
+                quantize(written, rows * P, span(a[1], P, a[2] - a[1]), src[:, span(a[1], HALF, a[2] - a[1])], E5M2)
+            elif kind == "q_w":
+                quantize(written, HALF, span(a[2], HALF // 2), src[:], E4M3)
+            elif kind == "q_h":
+                quantize(written, HALF, span(0, HALF), src[:], E4M3)
             elif kind == "weave":
-                g, c, us = job[2:]
-                dst = tile_of(written, [P, 2 * SLOTS * HALF], BF16)[:, span(g, SLOTS * HALF)]
-                if len(us) == 2:
-                    weave_copy(job, dst, src[:].rearrange("p (s u c w) -> p c u w s", s=SLOTS, u=2, c=2)[:, c])
-                else:
-                    cols = src[:].rearrange("p (s u c o w) -> p c u o w s", s=SLOTS, u=2, c=2, o=2)[:, c, us[0]]
-                    weave_copy(job, dst[:, span(us[0], SLOTS * HALF // 2)], cols)
+                e, c, g = a
+                dst = tile_of(written, 2 * SLOTS * HALF, BF16)[:, span(g, SLOTS * HALF)]
+                weave_copy(job, dst, src[:].rearrange("p (s u c w) -> p c u w s", s=SLOTS, u=2, c=2)[:, c])
             elif kind == "weave_h":
-                cols = src[:].rearrange("p (s n o w) -> p n o w s", s=SLOTS, n=H_PIECES, o=2)[:, job[2]]
-                weave_copy(job, tile_of(written, [P, SLOTS * H], BF16)[:, span(job[2], SLOTS * H // H_PIECES)], cols)
-            elif kind == "q_tok":
-                quantize(written, 2 * HALF, span(job[2], HALF), src[:, span(job[2], SLOTS * HALF)], E5M2)
-            elif kind in ("q_feat", "q_w", "q_h"):
-                quantize(written, HALF, span(0, HALF), src[:], E5M2 if kind == "q_feat" else E4M3)
+                cols = src[:].rearrange("p (s n o w) -> p n o w s", s=SLOTS, n=H_PIECES, o=2)[:, a[1]]
+                weave_copy(job, tile_of(written, SLOTS * H, BF16)[:, span(a[1], SLOTS * H // H_PIECES)], cols)
+            elif kind == "q_t":
+                gs = a[2]
+                quantize(written, 2 * HALF, span(gs[0], HALF, len(gs)), src[:, span(gs[0], SLOTS * HALF, len(gs))], E5M2)
             elif kind == "mm0":
-                e, g, c, s = job[1:]
-                matmul_mx(tile_of(written, [P, HALF], F32)[:], read[0], span(s, P), E5M2, read[1], span(0, HALF), E4M3,
+                e, c, n, halves = a
+                out = tile_of(written, HALF // 2 * len(halves), F32)[:]
+                matmul_mx(out, read[0], span(place_of_row(e, n, c)[1], P), E5M2,
+                          read[1], span(halves[0], HALF // 2, len(halves)), E4M3,
                           (e, c) == (0, 0), (e, c) == (E - 1, 1))
             elif kind == "mm1":
-                m, g = job[3:]
-                matmul_mx(tile_of(written, [P, HALF], F32)[:], read[1], span(m, P), E4M3, read[0], span(g, HALF), E5M2,
+                m, g = a[2:]
+                matmul_mx(tile_of(written, HALF, F32)[:], read[1], span(m, P), E4M3, read[0], span(g, HALF), E5M2,
                           g == 0, g == 1)
             elif kind == "drain0":
-                pieces = LAST_PIECES if ("store",) + job == stores[-1] else 1
-                for n in range(pieces):
-                    cols = span(n, HALF // pieces)
-                    copy(job, stage_of(written)[:, cols], src[:, cols])
+                copy(job, tile_of(written, HALF // 2 * len(a[1]), F32)[:], src[:])
             elif kind == "drain1":
-                copy(job, stage_of(written).rearrange("p (w u x) -> p w u x", u=2, x=2),
+                copy(job, tile_of(written, HALF, F32)[:].rearrange("p (w u x) -> p w u x", u=2, x=2),
                      src[:].rearrange("p (u w x) -> p w u x", u=2, x=2))
+            elif a[0] == "drain0":
+                g, s = divmod(a[1][0], SLOTS)
+                nc.sync.dma_start(out=out0_view[g][:, s, span(a[2][0], HALF // 2, len(a[2]))], in_=src[:])
             else:
-                if job[1] == "drain0":
-                    dst = out0_view[job[2], job[3]]
-                else:
-                    dst = out1_view[job[2], job[4]][:, span(job[3], HALF)]
-                pieces = LAST_PIECES if job == stores[-1] else 1
-                for n in range(pieces):
-                    cols = span(n, HALF // pieces)
-                    nc.sync.dma_start(out=dst[:, cols], in_=src[:, cols])
+                nc.sync.dma_start(out=out1_view[a[1], a[3]][:, span(a[2], HALF)], in_=src[:])
 
         with tc.manual_schedule():
             done = set()
@@ -377,4 +403,4 @@ def tile_enhancedmathematicalreasoning_pa_v_kernel(
                         emit(queue[heads[q]])
                         done.add(queue[heads[q]])
                         heads[q] = heads[q] + 1
-                assert len(done) > count, "the job lists wait for each other"
+                assert len(done) > count, [queue[n : n + 1] for queue, n in zip(queues, heads)]

@@ -18,10 +18,10 @@ BANKS = 8
 FLOPS = 2 * 2 * T * H * E * HO
 BYTES = 2 * (T * H + E * H * HO + T * HO) + 4 * T * E + 4 * (T * H + E * H * HO)
 FIRST = 2
-DEPTH = {"w_raw": 4, "dz": 8, "first_flip": 4, "slot_flip": 2, "slot_codes": 2, "first_codes": 7, "w_flip": 5, "woven": 2,
-         "t_codes": 3, "stage": 3}
+DEPTH = {"w_raw": 4, "dz": 8, "first_flip": 2, "slot_flip": 2, "slot_codes": 3, "first_codes": 3, "w_flip": 3, "woven": 2,
+         "t_codes": 3, "stage": 1}
 STAGE_IN = ("stage", "first_flip", "w_flip", "w_raw")
-WARM_FIRST = 3
+WARM_FIRST = 4
 H_PIECES = 4
 
 
@@ -41,23 +41,23 @@ def job_lists():
     def passes(k, rows=both, slots=range(FIRST)):
         return [("mm0",) + halves[k] + (n, rows) for n in slots]
 
-    def q_w(k, rows=both):
-        return [("q_w",) + halves[k] + (x,) for x in rows]
+    def q_w(k):
+        return [("q_w",) + halves[k]]
 
-    def q_z(e, n):
-        return [("q_z", ("first", e, n), 0, 2)]
+    def q_z(e, slots=both):
+        return [("q_z", ("first", e), 2 * slots[0], 2 * slots[-1] + 2)]
 
     def slot_flips(n):
         return [("flip_z", (e, n, 0), (e, n, 1)) for e in range(E)]
 
     def q_slot(n, parts=both):
-        return [("q_z", ("slot", n), E * x, E * x + E) for x in parts]
+        return [("q_z", ("slot", n), E * parts[0], E * parts[-1] + E)]
 
-    def weave(k, gs=both):
-        return [("weave",) + halves[k] + (g,) for g in gs]
+    def weave(k, gs=both, us=both):
+        return [("weave",) + halves[k] + (g, us) for g in gs]
 
     def q_t(k, gs=both):
-        return [("q_t",) + halves[k] + ((g,),) for g in gs]
+        return [("q_t",) + halves[k] + (gs,)]
 
     def groups(k, ms=range(H // P)):
         return [("mm1",) + halves[k] + (m, g) for m in ms for g in both]
@@ -69,43 +69,43 @@ def job_lists():
         return drain_of(jobs[-1])
 
     lo, hi = (0,), (1,)
-    loads = [("load_p",), ("load_w", 0, 0, lo), ("load_g", (0,), both), ("load_w", 0, 1, lo), ("load_g", (1,), both)]
-    loads += [("load_w", 0, 0, hi), ("load_w", 0, 1, hi), ("load_w", 1, 0, both), ("load_g", (2, 3), both), ("load_w", 1, 1, both)]
-    loads += [("load_w", 2, 0, both), ("load_w", 2, 1, both), ("load_h", 0), ("load_g", (4, 5), both), ("load_g", (6, 7), both)]
-    loads += [("load_w", 3, 0, both), ("load_h", 1), ("load_w", 3, 1, both)]
+    loads = [("load_p",), ("load_g", (0,), both), ("load_w", 0, lo, lo), ("load_g", (1,), both), ("load_w", 0, hi, lo)]
+    loads += [("load_g", (2,), both), ("load_w", 0, lo, hi), ("load_w", 0, hi, hi), ("load_w", 1, both, lo), ("load_g", (3,), both)]
+    loads += [("load_w", 1, both, hi), ("load_w", 2, both, lo), ("load_g", (4, 5), both), ("load_w", 2, both, hi), ("load_h", 0)]
+    loads += [("load_g", (6, 7), both), ("load_w", 3, both, lo), ("load_h", 1), ("load_w", 3, both, hi)]
 
     whole = [[("mm0",) + halves[k] + (n, both) for k in range(2 * E)] for n in range(2 * SLOTS - 1)]
     last = [[("mm0",) + halves[k] + (2 * SLOTS - 1, rows) for k in range(2 * E)] for rows in (lo, hi)]
     tensor = [("warm", n) for n in range(WARM_FIRST)]
-    tensor += flip_w(0, lo) + [("warm", 3)] + flip_z(0, 0) + flip_w(0, hi) + flip_z(1, 0) + [("warm", 4)] + flip_z(0, 1) + flip_z(2, 0) + flip_w(1)
-    tensor += passes(0) + flip_z(1, 1) + flip_z(3, 0) + flip_w(2, lo) + flip_w(3, lo)
-    tensor += passes(1) + flip_w(2, hi) + flip_w(3, hi) + flip_z(2, 1) + flip_z(3, 1) + flip_w(4, lo)
-    tensor += passes(2) + flip_w(5, lo) + flip_w(4, hi) + flip_w(5, hi) + passes(3) + slot_flips(2) + passes(4) + passes(5)
-    tensor += flip_w(6, lo) + flip_w(7, lo) + slot_flips(3)[:2] + whole[2][:4] + flip_w(6, hi) + flip_w(7, hi) + slot_flips(3)[2:]
-    tensor += whole[2][4:6] + whole[3][:4] + passes(6) + passes(7) + whole[2][6:] + groups(0, (0, 1))
-    tensor += slot_flips(4) + whole[3][4:6] + groups(0, (2, 3)) + whole[3][6:] + groups(1)
-    tensor += slot_flips(5) + whole[4][:4] + groups(2) + whole[4][4:] + groups(3) + whole[5][:4]
-    tensor += slot_flips(6) + whole[5][4:] + groups(4) + whole[6][:2]
-    tensor += slot_flips(7) + whole[6][2:4] + groups(5) + whole[6][4:] + groups(6)
-    tensor += last[0][:4] + last[1][:4] + groups(7) + last[0][4:] + last[1][4:]
+    tensor += flip_z(0, 0) + flip_w(0, lo) + [("warm", 4)] + flip_z(0, 1) + flip_w(0, hi) + flip_z(1, 0) + flip_z(1, 1) + flip_w(1) + flip_z(2, 0)
+    tensor += passes(0) + flip_z(2, 1) + flip_w(2) + passes(1)
+    tensor += flip_w(3) + flip_z(3, 0) + flip_z(3, 1) + slot_flips(2)[:2] + passes(2)
+    tensor += flip_w(4) + slot_flips(2)[2:] + passes(3) + whole[2][:2]
+    tensor += flip_w(5) + slot_flips(3)[:2] + passes(4) + whole[2][2:4]
+    tensor += flip_w(6) + slot_flips(3)[2:] + slot_flips(4)[:1] + passes(5) + whole[2][4:6]
+    tensor += flip_w(7) + slot_flips(4)[1:] + passes(6) + whole[2][6:7] + whole[3][:7]
+    tensor += whole[0][7:] + whole[1][7:] + groups(0, (0,)) + whole[2][7:] + whole[3][7:] + groups(0, (1,)) + whole[4][:4]
+    tensor += slot_flips(5) + whole[4][4:6] + groups(0, (2, 3)) + whole[4][6:] + groups(1)
+    tensor += slot_flips(6) + whole[5][:4] + groups(2) + whole[5][4:] + groups(3) + whole[6][:4] + groups(4)
+    tensor += slot_flips(7) + whole[6][4:6] + groups(5) + whole[6][6:] + groups(6) + last[0][:4] + last[1][:4]
+    tensor += groups(7, (0, 1)) + last[0][4:6] + groups(7, (2,)) + last[1][4:6] + groups(7, (3,)) + last[0][6:] + last[1][6:]
 
-    vector = scale(range(E), (0,)) + q_w(0, lo) + scale([0], (1,)) + q_z(0, 0)
-    vector += scale([1], (1,)) + q_w(0, hi) + scale([2], (1,)) + q_z(1, 0) + q_z(0, 1) + scale([3], (1,))
-    vector += q_z(2, 0) + q_w(1) + scale([0], (2, 3)) + q_z(1, 1) + scale([1], (2,)) + q_z(3, 0)
-    vector += scale([2], (2,)) + q_w(2, lo) + scale([3], (2,)) + q_w(3, lo) + scale([1], (3,)) + q_w(2, hi) + q_w(3, hi) + weave(0, lo) + q_z(2, 1) + scale([2], (3,)) + q_z(3, 1)
-    vector += scale([3], (3,)) + q_w(4, lo) + q_t(0, lo) + q_w(5, lo) + q_w(4, hi) + scale([0], (4,)) + q_w(5, hi) + scale([0], (5,))
-    vector += scale([0], (6, 7)) + weave(1, lo) + q_slot(2, lo) + weave(0, hi) + q_slot(2, hi)
-    vector += q_w(6, lo) + q_w(7, lo) + q_t(0, hi) + q_slot(3, lo) + [("q_h", 0)] + scale([1, 2], (4,)) + q_w(6, hi) + scale([3], (4,)) + q_w(7, hi)
-    vector += weave(1, hi) + [("q_h", 1)] + scale([1, 2, 3], (5,)) + q_slot(3, hi) + q_t(1) + scale([1], (6, 7)) + weave(2) + q_slot(4)
-    vector += q_t(2) + weave(3) + scale([2, 3], (6,)) + q_t(3) + q_slot(5) + scale([2], (7,))
-    vector += weave(4) + scale([3], (7,)) + q_t(4) + weave(5) + q_slot(6) + q_t(5) + weave(6) + q_t(6) + q_slot(7, lo)
-    vector += weave(7) + q_t(7) + q_slot(7, hi) + [drain(groups(7, (2,))), drain(last[0])]
+    vector = scale(range(E), (0,)) + scale(range(E), (1,)) + scale([0, 1], (2,)) + q_z(0) + q_w(0) + scale([2, 3], (2,))
+    vector += q_z(1) + q_w(1) + scale([0, 1], (3,)) + q_z(2) + weave(0, lo) + q_w(2) + scale([2, 3], (3,)) + scale([0], (4,)) + q_w(3)
+    vector += q_z(3) + scale([0], (5,)) + q_slot(2, lo) + weave(1, lo) + q_w(4) + scale([1], (4,)) + q_slot(2, hi) + scale([0], (6, 7))
+    vector += q_w(5) + scale([2, 3], (4,)) + weave(0, hi) + [("q_h", 0)] + q_w(6) + scale([1], (5,)) + q_slot(3) + weave(1, hi)
+    vector += q_w(7) + q_t(0) + [("q_h", 1)] + q_slot(4) + scale([2, 3], (5,)) + scale([1], (6, 7)) + q_t(1) + scale([2, 3], (6,))
+    vector += weave(2) + q_slot(5) + q_t(2) + weave(3) + scale([2, 3], (7,)) + q_t(3)
+    vector += weave(4, hi) + q_slot(6) + q_t(4) + weave(5) + weave(6, lo) + q_t(5) + weave(6, hi) + weave(7, lo) + q_t(6)
+    vector += q_slot(7) + weave(7, hi) + q_t(7, lo) + q_t(7, hi) + [drain(groups(7, (2,))), drain(last[0])]
 
     behind = {
-        drain(flip_w(5, hi)): weave_h(0, (0, 1)),
-        drain(slot_flips(2)): weave_h(0, (2, 3)),
-        drain(slot_flips(3)[:2]): weave_h(1, (0, 1)),
-        drain(flip_w(7, hi)): weave_h(1, (2, 3)),
+        drain(slot_flips(2)): weave_h(0, (0, 1)),
+        drain(slot_flips(3)[:2]): weave_h(0, (2, 3)),
+        drain(slot_flips(4)[:1]): weave_h(1, (0, 1)),
+        drain(flip_w(7)): weave_h(1, (2, 3)),
+        drain(groups(1)): weave(4, lo, lo),
+        drain(slot_flips(6)): weave(4, lo, hi),
     }
 
     closing = [drain_of(job) for job in tensor if drain_of(job)]
@@ -117,7 +117,7 @@ def job_lists():
 
 def place_of_row(e, n, c):
     if n < FIRST:
-        return ("first", e, n), c
+        return ("first", e), 2 * n + c
     return ("slot", n), 2 * e + c
 
 
@@ -153,12 +153,12 @@ def uses_of(job, loads):
         piece = [x for x in loads if x[0] == "load_g" and n in x[1] and cs[0] in x[2]][0]
         return [(("dz", e, n // SLOTS), [(n, c) for c in cs])], [(("g_raw",) + piece[1:], whole), (("p_raw",), whole)]
     if kind == "flip_w":
-        piece = [x for x in loads if x[0] == "load_w" and x[1:3] == (a[0], a[2]) and a[1] in x[3]][0]
+        piece = [x for x in loads if x[0] == "load_w" and x[1] == a[0] and a[2] in x[2] and a[1] in x[3]][0]
         return [(("bank",) + job, whole)], [(("w_raw",) + piece[1:], whole), ident]
     if kind == "drain_w":
-        return [(("w_flip",) + a, whole)], [(("bank", "flip_w") + a, whole)]
+        return [(("w_flip",) + a[:2], a[2:])], [(("bank", "flip_w") + a, whole)]
     if kind == "q_w":
-        return [(("w_codes",) + a[:2], a[2:])], [(("w_flip",) + a, whole)]
+        return [(("w_codes", a[0]), a[1:])], [(("w_flip",) + a, (0, 1))]
     if kind == "flip_z":
         return [(("bank",) + job, whole)], [(("dz", e, n // SLOTS), [(n, c)]) for e, n, c in a] + [ident]
     if kind == "drain_z":
@@ -170,12 +170,12 @@ def uses_of(job, loads):
     if kind == "mm0":
         e, c, n, halves = a
         key, row = place_of_row(e, n, c)
-        return [(("bank", "sum") + sum_of(job), whole)], [((key[0] + "_codes",) + key, (row,)), (("w_codes", e, c), halves)]
+        return [(("bank", "sum") + sum_of(job), whole)], [((key[0] + "_codes",) + key, (row,)), (("w_codes", e), (c,))]
     if kind == "weave":
-        e, c, g = a
-        return [(("woven", e, c), (g,))], [(("dz", e, g), [(SLOTS * g + s, c) for s in range(SLOTS)])]
+        e, c, g, us = a
+        return [(("woven", e, c), [(g, u) for u in us])], [(("dz", e, g), [(SLOTS * g + s, c) for s in range(SLOTS)])]
     if kind == "q_t":
-        return [(("t_codes",) + a[:2], a[2])], [(("woven",) + a[:2], a[2])]
+        return [(("t_codes",) + a[:2], a[2])], [(("woven",) + a[:2], [(g, u) for g in a[2] for u in (0, 1)])]
     if kind == "weave_h":
         return [(("h_woven", a[0]), (a[1],))], [(("h_raw", a[0]), whole)]
     if kind == "q_h":
@@ -266,7 +266,7 @@ def tile_enhancedmathematicalreasoning_pa_v_kernel(
                     tiles[item, part] = psum.tile([P, width], dtype, name=tag, tag=tag)
                 else:
                     tiles[item, part] = sbuf.tile([P, width], dtype, name=tag, tag=tag,
-                                                  align_bytes=256 if "codes" in tag else 64)
+                                                  align_bytes=64 if item[0] == "p_raw" else 256)
             return tiles[item, part]
 
         def span(n, width, count=1):
@@ -318,10 +318,10 @@ def tile_enhancedmathematicalreasoning_pa_v_kernel(
                 nc.sync.dma_start(out=raw[:].rearrange("p (s j) -> p s j", s=len(slots)),
                                   in_=g_view[g][:, s : s + len(slots), span(cs[0], HALF, len(cs))])
             elif kind == "load_w":
-                e, half, cs = a
-                raw = tile_of(written, 2 * len(cs) * HALF, BF16)
-                nc.sync.dma_start(out=raw[:].rearrange("p (a j) -> p a j", a=2),
-                                  in_=w_view[e][:, span(half, 2), span(cs[0], HALF, len(cs))])
+                e, halves, cs = a
+                raw = tile_of(written, 2 * len(halves) * len(cs) * HALF, BF16)
+                nc.sync.dma_start(out=raw[:].rearrange("p (a j) -> p a j", a=2 * len(halves)),
+                                  in_=w_view[e][:, span(halves[0], 2, len(halves)), span(cs[0], HALF, len(cs))])
             elif kind == "load_h":
                 nc.sync.dma_start(out=tile_of(written, SLOTS * H, BF16)[:], in_=h_view[a[0]])
             elif kind == "warm":
@@ -342,30 +342,34 @@ def tile_enhancedmathematicalreasoning_pa_v_kernel(
                 )
             elif kind == "flip_w":
                 words = src[:].bitcast(F32)
-                have = read[0][3]
-                starts = [(r * len(have) + have.index(a[1])) * (HALF // 2) + u for r in range(2) for u in range(2)]
+                halves, cs = read[0][2:]
+                rows = [2 * halves.index(a[2]) + r for r in range(2)]
+                starts = [(row * len(cs) + cs.index(a[1])) * (HALF // 2) + u for row in rows for u in range(2)]
                 flip(tile_of(written, HALF, F32), [words[:, x : x + 2 * P - 1 : 2] for x in starts])
             elif kind == "flip_z":
                 blocks = [tiles[item, ""][:].bitcast(F32)[:, span(4 * (n % SLOTS) + 2 * u + c, P)]
                           for item, (e, n, c) in zip(read, a) for u in range(2)]
                 flip(tile_of(written, HALF, F32), blocks)
             elif kind in ("drain_z", "drain_w"):
-                rows = 2 if kind == "drain_w" else 2 * E if written[1] == "slot" else FIRST
-                first = uses[job][0][0][1][0]
+                rows = {"first_flip": 2 * FIRST, "slot_flip": 2 * E, "w_flip": SLOTS}[written[0]]
+                first = uses[job][0][0][1][0] * (2 if kind == "drain_w" else 1)
                 words = tile_of(written, rows * HALF, BF16)[:].bitcast(F32)[:, span(first, HALF // 2, 2)]
                 copy(job, words.rearrange("p (r n u) -> p r n u", r=2, u=2),
                      src[:].rearrange("p (r u n) -> p r n u", r=2, u=2))
             elif kind == "q_z":
-                rows = 2 * E if a[0][0] == "slot" else FIRST
+                rows = 2 * E if a[0][0] == "slot" else 2 * FIRST
                 quantize(written, rows * P, span(a[1], P, a[2] - a[1]), src[:, span(a[1], HALF, a[2] - a[1])], E5M2)
             elif kind == "q_w":
-                quantize(written, HALF, span(a[2], HALF // 2), src[:], E4M3)
+                quantize(written, HO, span(a[1], HALF), src[:], E4M3)
             elif kind == "q_h":
                 quantize(written, HALF, span(0, HALF), src[:], E4M3)
             elif kind == "weave":
-                e, c, g = a
-                dst = tile_of(written, 2 * SLOTS * HALF, BF16)[:, span(g, SLOTS * HALF)]
-                weave_copy(job, dst, src[:].rearrange("p (s u c w) -> p c u w s", s=SLOTS, u=2, c=2)[:, c])
+                e, c, g, us = a
+                dst = tile_of(written, 2 * SLOTS * HALF, BF16)[:, span(2 * g + us[0], HO, len(us))]
+                if len(us) == 2:
+                    weave_copy(job, dst, src[:].rearrange("p (s u c w) -> p c u w s", s=SLOTS, u=2, c=2)[:, c])
+                else:
+                    weave_copy(job, dst, src[:].rearrange("p (s u c o w) -> p c u o w s", s=SLOTS, u=2, c=2, o=2)[:, c, us[0]])
             elif kind == "weave_h":
                 cols = src[:].rearrange("p (s n o w) -> p n o w s", s=SLOTS, n=H_PIECES, o=2)[:, a[1]]
                 weave_copy(job, tile_of(written, SLOTS * H, BF16)[:, span(a[1], SLOTS * H // H_PIECES)], cols)
@@ -376,7 +380,7 @@ def tile_enhancedmathematicalreasoning_pa_v_kernel(
                 e, c, n, halves = a
                 out = tile_of(written, HALF // 2 * len(halves), F32)[:]
                 matmul_mx(out, read[0], span(place_of_row(e, n, c)[1], P), E5M2,
-                          read[1], span(halves[0], HALF // 2, len(halves)), E4M3,
+                          read[1], span(2 * c + halves[0], HALF // 2, len(halves)), E4M3,
                           (e, c) == (0, 0), (e, c) == (E - 1, 1))
             elif kind == "mm1":
                 m, g = a[2:]

@@ -20,7 +20,8 @@ BYTES = 2 * (T * H + E * H * HO + T * HO) + 4 * T * E + 4 * (T * H + E * H * HO)
 FIRST = 2
 DEPTH = {"w_raw": 4, "dz": 8, "first_flip": 2, "slot_flip": 2, "slot_codes": 3, "first_codes": 3, "w_flip": 3, "woven": 2,
          "t_codes": 3, "stage": 1}
-STAGE_IN = ("stage", "first_flip", "w_flip", "w_raw")
+EARLY = ("stage", "first_flip", "w_flip", "w_raw", "h_raw", "h_woven")
+STAGE_IN = (EARLY, EARLY, ("g_raw",), EARLY)
 WARM_FIRST = 4
 H_PIECES = 4
 
@@ -28,6 +29,7 @@ H_PIECES = 4
 def job_lists():
     both = (0, 1)
     halves = [(e, c) for e in range(E) for c in both]
+    units = [item + (both,) for item in halves[:-1]] + [halves[-1] + ((x,),) for x in both]
 
     def scale(experts, slots, cs=both):
         return [("scale", e, n, cs) for e in experts for n in slots]
@@ -54,16 +56,19 @@ def job_lists():
         return [("q_z", ("slot", n), E * parts[0], E * parts[-1] + E)]
 
     def weave(k, gs=both, us=both):
-        return [("weave",) + halves[k] + (g, us) for g in gs]
+        return [("weave", units[k], g, us) for g in gs]
 
     def q_t(k, gs=both):
-        return [("q_t",) + halves[k] + (gs,)]
+        return [("q_t", units[k], gs)]
 
     def groups(k, ms=range(H // P)):
-        return [("mm1",) + halves[k] + (m, g) for m in ms for g in both]
+        return [("mm1", units[k], m, g) for m in ms for g in both]
 
-    def weave_h(g, pieces=range(H_PIECES)):
-        return [("weave_h", g, n) for n in pieces]
+    def weave_h(g, pieces=(0, 1, 2, 3)):
+        return [("weave_h", g, pieces)]
+
+    def braid(g, half):
+        return [("braid", g, half)]
 
     def drain(jobs):
         return drain_of(jobs[-1])
@@ -74,42 +79,42 @@ def job_lists():
     loads += [("load_w", 1, both, hi), ("load_w", 2, both, lo), ("load_g", (4, 5), both), ("load_w", 2, both, hi), ("load_h", 0)]
     loads += [("load_g", (6, 7), both), ("load_w", 3, both, lo), ("load_h", 1), ("load_w", 3, both, hi)]
 
-    whole = [[("mm0",) + halves[k] + (n, both) for k in range(2 * E)] for n in range(2 * SLOTS - 1)]
-    last = [[("mm0",) + halves[k] + (2 * SLOTS - 1, rows) for k in range(2 * E)] for rows in (lo, hi)]
+    whole = [[("mm0",) + halves[k] + (n, both) for k in range(2 * E)] for n in range(2 * SLOTS)]
     tensor = [("warm", n) for n in range(WARM_FIRST)]
-    tensor += flip_z(0, 0) + flip_w(0, lo) + [("warm", 4)] + flip_z(0, 1) + flip_w(0, hi) + flip_z(1, 0) + flip_z(1, 1) + flip_w(1) + flip_z(2, 0)
-    tensor += passes(0) + flip_z(2, 1) + flip_w(2) + passes(1)
-    tensor += flip_w(3) + flip_z(3, 0) + flip_z(3, 1) + slot_flips(2)[:2] + passes(2)
-    tensor += flip_w(4) + slot_flips(2)[2:] + passes(3) + whole[2][:2]
-    tensor += flip_w(5) + slot_flips(3)[:2] + passes(4) + whole[2][2:4]
+    tensor += flip_z(0, 0) + flip_w(0, lo) + [("warm", 4)] + flip_z(0, 1) + flip_w(0, hi) + flip_z(1, 0) + flip_z(1, 1) + flip_w(1) + flip_z(2, 0) + flip_z(2, 1)
+    tensor += passes(0) + flip_w(2) + flip_z(3, 0) + passes(1)
+    tensor += flip_w(3) + flip_z(3, 1) + slot_flips(2)[:2] + passes(2)
+    tensor += flip_w(4) + slot_flips(2)[2:] + passes(3)
+    tensor += flip_w(5) + slot_flips(3)[:2] + whole[2][:4] + passes(4)
     tensor += flip_w(6) + slot_flips(3)[2:] + slot_flips(4)[:1] + passes(5) + whole[2][4:6]
     tensor += flip_w(7) + slot_flips(4)[1:] + passes(6) + whole[2][6:7] + whole[3][:7]
-    tensor += whole[0][7:] + whole[1][7:] + groups(0, (0,)) + whole[2][7:] + whole[3][7:] + groups(0, (1,)) + whole[4][:4]
-    tensor += slot_flips(5) + whole[4][4:6] + groups(0, (2, 3)) + whole[4][6:] + groups(1)
+    tensor += whole[0][7:] + whole[1][7:] + whole[2][7:] + whole[3][7:]
+    tensor += slot_flips(5) + whole[4][:4] + groups(0) + whole[4][4:] + groups(1)
     tensor += slot_flips(6) + whole[5][:4] + groups(2) + whole[5][4:] + groups(3) + whole[6][:4] + groups(4)
-    tensor += slot_flips(7) + whole[6][4:6] + groups(5) + whole[6][6:] + groups(6) + last[0][:4] + last[1][:4]
-    tensor += groups(7, (0, 1)) + last[0][4:6] + groups(7, (2,)) + last[1][4:6] + groups(7, (3,)) + last[0][6:] + last[1][6:]
+    tensor += slot_flips(7) + whole[6][4:6] + groups(5) + whole[6][6:] + whole[7][:2] + groups(6) + whole[7][2:6] + groups(7) + whole[7][6:] + groups(8)
 
-    vector = scale(range(E), (0,)) + scale(range(E), (1,)) + scale([0, 1], (2,)) + q_z(0) + q_w(0) + scale([2, 3], (2,))
-    vector += q_z(1) + q_w(1) + scale([0, 1], (3,)) + q_z(2) + weave(0, lo) + q_w(2) + scale([2, 3], (3,)) + scale([0], (4,)) + q_w(3)
-    vector += q_z(3) + scale([0], (5,)) + q_slot(2, lo) + weave(1, lo) + q_w(4) + scale([1], (4,)) + q_slot(2, hi) + scale([0], (6, 7))
-    vector += q_w(5) + scale([2, 3], (4,)) + weave(0, hi) + [("q_h", 0)] + q_w(6) + scale([1], (5,)) + q_slot(3) + weave(1, hi)
-    vector += q_w(7) + q_t(0) + [("q_h", 1)] + q_slot(4) + scale([2, 3], (5,)) + scale([1], (6, 7)) + q_t(1) + scale([2, 3], (6,))
-    vector += weave(2) + q_slot(5) + q_t(2) + weave(3) + scale([2, 3], (7,)) + q_t(3)
-    vector += weave(4, hi) + q_slot(6) + q_t(4) + weave(5) + weave(6, lo) + q_t(5) + weave(6, hi) + weave(7, lo) + q_t(6)
-    vector += q_slot(7) + weave(7, hi) + q_t(7, lo) + q_t(7, hi) + [drain(groups(7, (2,))), drain(last[0])]
+    vector = scale(range(E), (0,)) + scale(range(E), (1,)) + scale([0, 1, 2], (2,)) + q_z(0) + q_w(0) + scale([3], (2,))
+    vector += q_z(1) + scale([0], (3,)) + q_w(1) + scale([1], (3,)) + q_z(2) + weave(0, lo) + q_w(2) + scale([2, 3], (3,)) + scale([0], (4,)) + q_w(3)
+    vector += q_z(3) + q_slot(2, lo) + scale([0], (5,)) + weave(1, lo) + q_w(4) + scale([1], (4,)) + q_slot(2, hi) + scale([0], (6, 7))
+    vector += scale([2], (4,)) + q_w(5) + scale([3], (4,)) + weave(0, hi) + weave_h(0, (2, 3)) + q_w(6) + scale([1], (5,)) + [("q_h", 0)] + q_slot(3)
+    vector += q_t(0) + q_w(7) + scale([2, 3], (5,)) + weave(1, hi) + q_slot(4) + [("q_h", 1)] + scale([1], (6, 7)) + q_t(1)
+    vector += weave(2, lo, hi) + weave(2, hi) + q_slot(5) + scale([2, 3], (6,)) + q_t(2) + weave(3) + scale([2], (7,)) + q_t(3)
+    vector += weave(4, hi) + q_slot(6) + q_t(4) + weave(5) + scale([3], (7,)) + q_t(5) + weave(6) + q_slot(7, lo) + q_t(6)
+    vector += weave(7) + q_slot(7, hi) + weave(8, lo) + q_t(7) + weave(8, hi) + q_t(8)
+    vector += [drain(groups(7, (0,))), drain(groups(7, (2,))), drain(whole[7]), drain(groups(8, (1,))), drain(groups(8, (3,)))]
+    ahead = []
 
     behind = {
+        drain(slot_flips(4)): weave(2, lo, lo),
         drain(slot_flips(2)): weave_h(0, (0, 1)),
-        drain(slot_flips(3)[:2]): weave_h(0, (2, 3)),
-        drain(slot_flips(4)[:1]): weave_h(1, (0, 1)),
-        drain(flip_w(7)): weave_h(1, (2, 3)),
+        drain(slot_flips(3)[:2]): weave_h(1, (0, 1)),
+        drain(slot_flips(4)[:1]): weave_h(1, (2, 3)),
         drain(groups(1)): weave(4, lo, lo),
         drain(slot_flips(6)): weave(4, lo, hi),
     }
 
     closing = [drain_of(job) for job in tensor if drain_of(job)]
-    scalar = [job for x in closing for job in [x] + behind.get(x, [])]
+    scalar = ahead + [job for x in closing for job in [x] + behind.get(x, [])]
     stores = [("store",) + job for job in scalar if job[0] in ("drain0", "drain1")]
     scalar = [job for job in scalar if job not in vector]
     return loads, tensor, vector, scalar, stores
@@ -131,8 +136,10 @@ def drain_of(job):
         return ("drain_z",) + job[1:]
     if job[0] == "flip_w":
         return ("drain_w",) + job[1:]
-    if job[0] == "mm1" and job[4] == 1:
-        return ("drain1",) + job[1:4]
+    if job[0] == "braid":
+        return ("drain_h",) + job[1:]
+    if job[0] == "mm1" and job[3] == 1:
+        return ("drain1",) + job[1:3]
     if job[0] == "mm0" and job[1:3] == (E - 1, 1):
         return ("drain0",) + sum_of(job)
     return None
@@ -172,17 +179,23 @@ def uses_of(job, loads):
         key, row = place_of_row(e, n, c)
         return [(("bank", "sum") + sum_of(job), whole)], [((key[0] + "_codes",) + key, (row,)), (("w_codes", e), (c,))]
     if kind == "weave":
-        e, c, g, us = a
-        return [(("woven", e, c), [(g, u) for u in us])], [(("dz", e, g), [(SLOTS * g + s, c) for s in range(SLOTS)])]
+        unit, g, us = a
+        return [(("woven", unit), [(g, u) for u in us])], [(("dz", unit[0], g), [(SLOTS * g + s, unit[1]) for s in range(SLOTS)])]
     if kind == "q_t":
-        return [(("t_codes",) + a[:2], a[2])], [(("woven",) + a[:2], [(g, u) for g in a[2] for u in (0, 1)])]
+        return [(("t_codes", a[0]), a[1])], [(("woven", a[0]), [(g, u) for g in a[1] for u in (0, 1)])]
     if kind == "weave_h":
-        return [(("h_woven", a[0]), (a[1],))], [(("h_raw", a[0]), whole)]
+        return [(("h_woven", a[0]), a[1])], [(("h_raw", a[0]), whole)]
+    if kind == "braid":
+        return [(("bank",) + job, whole)], [(("h_raw", a[0]), whole), (("identity16",), whole)]
+    if kind == "drain_h":
+        return [(("h_woven", a[0]), (2 * a[1], 2 * a[1] + 1))], [(("bank", "braid") + a, whole)]
+    if kind == "identity16":
+        return [(job, whole)], []
     if kind == "q_h":
         return [(("h_codes",) + a, whole)], [(("h_woven",) + a, range(H_PIECES))]
     if kind == "mm1":
-        e, c, m, g = a
-        return [(("bank", "mm1", e, c, m), whole)], [(("t_codes", e, c), (g,)), (("h_codes", g), whole)]
+        unit, m, g = a
+        return [(("bank", "mm1", unit, m), whole)], [(("t_codes", unit), (g,)), (("h_codes", g), whole)]
     if kind == "drain0":
         return [(("stage",) + job, whole)], [(("bank", "sum") + a, whole)]
     if kind == "drain1":
@@ -192,7 +205,7 @@ def uses_of(job, loads):
 
 def plan():
     loads, tensor, vector, scalar, stores = job_lists()
-    queues = [loads[:1] + [("identity",)] + loads[1:] + stores, tensor, vector, scalar]
+    queues = [loads[:1] + [("identity",)] + [("identity16",) for job in tensor if job == ("braid", 0, 0)] + loads[1:] + stores, tensor, vector, scalar]
     jobs = [job for queue in queues for job in queue]
     assert len(set(jobs)) == len(jobs)
     uses = {job: uses_of(job, loads) for job in jobs}
@@ -211,14 +224,16 @@ def plan():
             replaces[item] = holder[spot]
         holder[spot] = item
 
-    spots = {kind: [f"{kind}{n}" for n in range(depth)] for kind, depth in DEPTH.items()}
-    spots["stage"] = [spot for kind in STAGE_IN for spot in spots[kind]]
     drains = [store[1:] for store in stores]
-    for job in [job for job in loads + vector + scalar if job not in drains] + drains:
+    for job in [job for job in queues[0] + vector + scalar if job not in drains]:
         for item, parts in uses[job][0]:
-            if item[0] in DEPTH and item not in place:
-                put(item, spots[item[0]][count.get(item[0], 0) % len(spots[item[0]])])
-                count[item[0]] = count.get(item[0], 0) + 1
+            if item not in place:
+                n = count.get(item[0], 0)
+                put(item, f"{item[0]}{n % DEPTH.get(item[0], len(jobs))}")
+                count[item[0]] = n + 1
+    rooms = [f"{kind}{n}" for kinds in STAGE_IN for kind in kinds for n in range(DEPTH.get(kind, count.get(kind)))]
+    for n, job in enumerate(drains):
+        put(uses[job][0][0][0], rooms[n])
     free = [f"bank{n}" for n in range(BANKS)]
     last_warm = [job for job in tensor if job[0] == "warm"][-1:]
     for job in tensor:
@@ -260,13 +275,12 @@ def tile_enhancedmathematicalreasoning_pa_v_kernel(
 
         def tile_of(item, width, dtype, part=""):
             if (item, part) not in tiles:
-                tag = place[item] if item in place else "".join(str(x) for x in item)
-                tag = tag.replace("(", "").replace(")", "").replace(", ", "").replace(",", "") + part
+                tag = place[item]
                 if item[0] == "bank":
                     tiles[item, part] = psum.tile([P, width], dtype, name=tag, tag=tag)
                 else:
                     tiles[item, part] = sbuf.tile([P, width], dtype, name=tag, tag=tag,
-                                                  align_bytes=64 if item[0] == "p_raw" else 256)
+                                                  align_bytes=64 if item[0] in ("p_raw", "identity", "identity16") else 256)
             return tiles[item, part]
 
         def span(n, width, count=1):
@@ -309,6 +323,16 @@ def tile_enhancedmathematicalreasoning_pa_v_kernel(
             src = tiles[read[0], ""] if read else None
             if kind == "identity":
                 make_identity(nc, tile_of(written, P, F32)[:])
+            elif kind == "identity16":
+                make_identity(nc, tile_of(written, P, BF16)[:])
+            elif kind == "braid":
+                bank = tile_of(written, HO, BF16)[:].rearrange("p (i r s) -> p r i s", r=2, s=2)
+                rows = src[:].rearrange("p (r s i) -> p r i s", r=2, s=2)
+                for r in range(2):
+                    nc.tensor.matmul(out=bank[:, r], lhsT=tiles[read[1], ""][:], rhs=rows[:, r, span(a[1], H // 2)],
+                                     start=True, stop=True)
+            elif kind == "drain_h":
+                copy(job, tile_of(written, SLOTS * H, BF16)[:, span(a[1], HO)], src[:])
             elif kind == "load_p":
                 nc.scalar.dma_start(out=tile_of(written, 2 * SLOTS * E, F32)[:].rearrange("p (g x) -> p g x", g=2), in_=p_view)
             elif kind == "load_g":
@@ -333,13 +357,13 @@ def tile_enhancedmathematicalreasoning_pa_v_kernel(
                 slots, have = read[0][1:]
                 first = slots.index(n) * len(have) + have.index(cs[0])
                 row = tile_of(written, SLOTS * HO, BF16)[:, span(n % SLOTS, HO)].rearrange("p (u w x) -> p u w x", u=2, x=2)
-                nc.vector.tensor_scalar(
-                    out=row[:, :, span(cs[0], P, len(cs))],
-                    in0=src[:, span(first, HALF, len(cs))].rearrange("p (w u x) -> p u w x", u=2, x=2),
-                    scalar1=tiles[read[1], ""][:, span(E * n + e, 1)],
-                    scalar2=None,
-                    op0=mybir.AluOpType.mult,
-                )
+                out = row[:, :, span(cs[0], P, len(cs))]
+                in_ = src[:, span(first, HALF, len(cs))].rearrange("p (w u x) -> p u w x", u=2, x=2)
+                factor = tiles[read[1], ""][:, span(E * n + e, 1)]
+                if job in vector:
+                    nc.vector.tensor_scalar(out=out, in0=in_, scalar1=factor, scalar2=None, op0=mybir.AluOpType.mult)
+                else:
+                    nc.scalar.activation(out=out, in_=in_, func=mybir.ActivationFunctionType.Copy, scale=factor)
             elif kind == "flip_w":
                 words = src[:].bitcast(F32)
                 halves, cs = read[0][2:]
@@ -364,18 +388,19 @@ def tile_enhancedmathematicalreasoning_pa_v_kernel(
             elif kind == "q_h":
                 quantize(written, HALF, span(0, HALF), src[:], E4M3)
             elif kind == "weave":
-                e, c, g, us = a
-                dst = tile_of(written, 2 * SLOTS * HALF, BF16)[:, span(2 * g + us[0], HO, len(us))]
-                if len(us) == 2:
-                    weave_copy(job, dst, src[:].rearrange("p (s u c w) -> p c u w s", s=SLOTS, u=2, c=2)[:, c])
-                else:
-                    weave_copy(job, dst, src[:].rearrange("p (s u c o w) -> p c u o w s", s=SLOTS, u=2, c=2, o=2)[:, c, us[0]])
+                (e, c, parts), g, us = a
+                width = len(parts) * HALF // 2
+                dst = tile_of(written, 2 * SLOTS * width, BF16)[:, span(2 * g + us[0], 2 * width, len(us))]
+                cols = src[:].rearrange("p (s u c w) -> p c u w s", s=SLOTS, u=2, c=2)[:, c, :, span(parts[0], P, len(parts))]
+                weave_copy(job, dst, cols if len(us) == 2 else cols[:, us[0]].rearrange("p (o w) s -> p o w s", o=2))
             elif kind == "weave_h":
-                cols = src[:].rearrange("p (s n o w) -> p n o w s", s=SLOTS, n=H_PIECES, o=2)[:, a[1]]
-                weave_copy(job, tile_of(written, SLOTS * H, BF16)[:, span(a[1], SLOTS * H // H_PIECES)], cols)
+                first, count = a[1][0], len(a[1])
+                cols = src[:].rearrange("p (s i) -> p i s", s=SLOTS)[:, span(first, H // H_PIECES, count)]
+                weave_copy(job, tile_of(written, SLOTS * H, BF16)[:, span(first, SLOTS * H // H_PIECES, count)],
+                           cols.rearrange("p (o w) s -> p o w s", o=2))
             elif kind == "q_t":
-                gs = a[2]
-                quantize(written, 2 * HALF, span(gs[0], HALF, len(gs)), src[:, span(gs[0], SLOTS * HALF, len(gs))], E5M2)
+                width, gs = len(a[0][2]) * HALF // 2, a[1]
+                quantize(written, 2 * width, span(gs[0], width, len(gs)), src[:, span(gs[0], SLOTS * width, len(gs))], E5M2)
             elif kind == "mm0":
                 e, c, n, halves = a
                 out = tile_of(written, HALF // 2 * len(halves), F32)[:]
@@ -383,19 +408,20 @@ def tile_enhancedmathematicalreasoning_pa_v_kernel(
                           read[1], span(2 * c + halves[0], HALF // 2, len(halves)), E4M3,
                           (e, c) == (0, 0), (e, c) == (E - 1, 1))
             elif kind == "mm1":
-                m, g = a[2:]
-                matmul_mx(tile_of(written, HALF, F32)[:], read[1], span(m, P), E4M3, read[0], span(g, HALF), E5M2,
+                width, m, g = len(a[0][2]) * HALF // 2, a[1], a[2]
+                matmul_mx(tile_of(written, width, F32)[:], read[1], span(m, P), E4M3, read[0], span(g, width), E5M2,
                           g == 0, g == 1)
             elif kind == "drain0":
                 copy(job, tile_of(written, HALF // 2 * len(a[1]), F32)[:], src[:])
             elif kind == "drain1":
-                copy(job, tile_of(written, HALF, F32)[:].rearrange("p (w u x) -> p w u x", u=2, x=2),
+                copy(job, tile_of(written, src.shape[1], F32)[:].rearrange("p (w u x) -> p w u x", u=2, x=2),
                      src[:].rearrange("p (u w x) -> p w u x", u=2, x=2))
             elif a[0] == "drain0":
                 g, s = divmod(a[1][0], SLOTS)
                 nc.sync.dma_start(out=out0_view[g][:, s, span(a[2][0], HALF // 2, len(a[2]))], in_=src[:])
             else:
-                nc.sync.dma_start(out=out1_view[a[1], a[3]][:, span(a[2], HALF)], in_=src[:])
+                e, c, parts = a[1]
+                nc.sync.dma_start(out=out1_view[e, a[2]][:, span(2 * c + parts[0], HALF // 2, len(parts))], in_=src[:])
 
         with tc.manual_schedule():
             done = set()

@@ -29,7 +29,7 @@ H_PIECES = 4
 def job_lists():
     both = (0, 1)
     halves = [(e, c) for e in range(E) for c in both]
-    units = [item + (both,) for item in halves[:-1]] + [halves[-1] + ((x,),) for x in both]
+    units = [item + (both,) for item in halves]
 
     def scale(experts, slots, cs=both):
         return [("scale", e, n, cs) for e in experts for n in slots]
@@ -79,38 +79,38 @@ def job_lists():
     loads += [("load_w", 1, both, hi), ("load_w", 2, both, lo), ("load_g", (4, 5), both), ("load_w", 2, both, hi), ("load_h", 0)]
     loads += [("load_g", (6, 7), both), ("load_w", 3, both, lo), ("load_h", 1), ("load_w", 3, both, hi)]
 
-    whole = [[("mm0",) + halves[k] + (n, both) for k in range(2 * E)] for n in range(2 * SLOTS)]
+    whole = [[("mm0",) + halves[k] + (n, both) for k in range(2 * E)] for n in range(2 * SLOTS - 1)]
+    last = [[("mm0",) + halves[k] + (2 * SLOTS - 1, rows) for k in range(2 * E)] for rows in (lo, hi)]
     tensor = [("warm", n) for n in range(WARM_FIRST)]
-    tensor += flip_z(0, 0) + flip_w(0, lo) + [("warm", 4)] + flip_z(0, 1) + flip_w(0, hi) + flip_z(1, 0) + flip_z(1, 1) + flip_w(1) + flip_z(2, 0) + flip_z(2, 1)
+    tensor += flip_z(0, 0) + flip_w(0, lo) + [("warm", 4)] + flip_z(0, 1) + flip_w(0, hi) + flip_z(1, 0) + flip_z(1, 1) + flip_w(1, lo) + [("warm", 5)] + flip_w(1, hi) + flip_z(2, 0) + flip_z(2, 1)
     tensor += passes(0) + flip_w(2) + flip_z(3, 0) + passes(1)
-    tensor += flip_w(3) + flip_z(3, 1) + slot_flips(2)[:2] + passes(2)
-    tensor += flip_w(4) + slot_flips(2)[2:] + passes(3)
-    tensor += flip_w(5) + slot_flips(3)[:2] + whole[2][:4] + passes(4)
-    tensor += flip_w(6) + slot_flips(3)[2:] + slot_flips(4)[:1] + passes(5) + whole[2][4:6]
-    tensor += flip_w(7) + slot_flips(4)[1:] + passes(6) + whole[2][6:7] + whole[3][:7]
-    tensor += whole[0][7:] + whole[1][7:] + whole[2][7:] + whole[3][7:]
-    tensor += slot_flips(5) + whole[4][:4] + groups(0) + whole[4][4:] + groups(1)
+    tensor += flip_w(3) + flip_z(3, 1) + slot_flips(2)[:1] + passes(2)
+    tensor += flip_w(4) + slot_flips(2)[1:3] + passes(3)
+    tensor += flip_w(5) + slot_flips(2)[3:] + slot_flips(3)[:1] + passes(4) + whole[2][:4]
+    tensor += flip_w(6) + slot_flips(3)[1:3] + passes(5) + whole[2][4:6]
+    tensor += flip_w(7) + slot_flips(3)[3:] + slot_flips(4)[:1] + passes(6) + whole[2][6:7] + whole[3][:4]
+    tensor += slot_flips(4)[1:] + whole[3][4:7] + whole[0][7:] + whole[1][7:] + whole[2][7:] + whole[3][7:] + groups(0, (0, 1))
+    tensor += slot_flips(5) + whole[4][:4] + groups(0, (2, 3)) + whole[4][4:] + groups(1)
     tensor += slot_flips(6) + whole[5][:4] + groups(2) + whole[5][4:] + groups(3) + whole[6][:4] + groups(4)
-    tensor += slot_flips(7) + whole[6][4:6] + groups(5) + whole[6][6:] + whole[7][:2] + groups(6) + whole[7][2:6] + groups(7) + whole[7][6:] + groups(8)
+    tensor += slot_flips(7) + whole[6][4:6] + groups(5) + whole[6][6:] + groups(6) + last[0][:4] + last[1][:4]
+    tensor += groups(7) + last[0][4:] + last[1][4:]
 
     vector = scale(range(E), (0,)) + scale(range(E), (1,)) + scale([0, 1, 2], (2,)) + q_z(0) + q_w(0) + scale([3], (2,))
-    vector += q_z(1) + scale([0], (3,)) + q_w(1) + scale([1], (3,)) + q_z(2) + weave(0, lo) + q_w(2) + scale([2, 3], (3,)) + scale([0], (4,)) + q_w(3)
-    vector += q_z(3) + q_slot(2, lo) + scale([0], (5,)) + weave(1, lo) + q_w(4) + scale([1], (4,)) + q_slot(2, hi) + scale([0], (6, 7))
-    vector += scale([2], (4,)) + q_w(5) + scale([3], (4,)) + weave(0, hi) + weave_h(0, (2, 3)) + q_w(6) + scale([1], (5,)) + [("q_h", 0)] + q_slot(3)
-    vector += q_t(0) + q_w(7) + scale([2, 3], (5,)) + weave(1, hi) + q_slot(4) + [("q_h", 1)] + scale([1], (6, 7)) + q_t(1)
-    vector += weave(2, lo, hi) + weave(2, hi) + q_slot(5) + scale([2, 3], (6,)) + q_t(2) + weave(3) + scale([2], (7,)) + q_t(3)
-    vector += weave(4, hi) + q_slot(6) + q_t(4) + weave(5) + scale([3], (7,)) + q_t(5) + weave(6) + q_slot(7, lo) + q_t(6)
-    vector += weave(7) + q_slot(7, hi) + weave(8, lo) + q_t(7) + weave(8, hi) + q_t(8)
-    vector += [drain(groups(7, (0,))), drain(groups(7, (2,))), drain(whole[7]), drain(groups(8, (1,))), drain(groups(8, (3,)))]
+    vector += q_z(1) + scale([0], (3,)) + q_w(1) + scale([1], (3,)) + q_z(2) + q_w(2) + weave(0, lo) + scale([2, 3], (3,)) + scale([0], (4,)) + q_w(3)
+    vector += q_z(3) + scale([0], (5,)) + weave(1, lo) + q_w(4) + q_slot(2, lo) + scale([1], (4,)) + scale([0], (6, 7))
+    vector += scale([2, 3], (4,)) + q_w(5) + q_slot(2, hi) + weave(0, hi) + weave_h(0, (2, 3)) + q_w(6) + q_slot(3, lo) + [("q_h", 0)]
+    vector += q_t(0) + q_w(7) + q_slot(3, hi) + [("q_h", 1)] + scale([1, 2, 3], (5,)) + weave(1, hi) + scale([1], (6,)) + q_slot(4) + scale([1], (7,)) + q_t(1)
+    vector += weave(2, lo, hi) + weave(2, hi) + scale([2, 3], (6,)) + q_t(2) + q_slot(5) + weave(3) + scale([2], (7,)) + q_t(3)
+    vector += weave(4, lo, hi) + weave(4, hi) + q_slot(6) + q_t(4) + weave(5) + scale([3], (7,)) + q_t(5) + weave(6) + q_slot(7, lo) + q_t(6)
+    vector += weave(7) + q_t(7, lo) + q_t(7, hi) + q_slot(7, hi) + [drain(groups(7, (1,))), drain(groups(7, (3,))), drain(last[1])]
     ahead = []
 
     behind = {
         drain(slot_flips(4)): weave(2, lo, lo),
-        drain(slot_flips(2)): weave_h(0, (0, 1)),
-        drain(slot_flips(3)[:2]): weave_h(1, (0, 1)),
-        drain(slot_flips(4)[:1]): weave_h(1, (2, 3)),
+        drain(slot_flips(2)[:3]): weave_h(0, (0, 1)),
+        drain(slot_flips(3)[:1]): weave_h(1, (0, 1)),
+        drain(slot_flips(3)[:3]): weave_h(1, (2, 3)),
         drain(groups(1)): weave(4, lo, lo),
-        drain(slot_flips(6)): weave(4, lo, hi),
     }
 
     closing = [drain_of(job) for job in tensor if drain_of(job)]

from contextlib import ExitStack

import concourse.mybir as mybir
from concourse.masks import make_identity

F32 = mybir.dt.float32
BF16 = mybir.dt.bfloat16
U32 = mybir.dt.uint32
U8 = mybir.dt.uint8
E4M3 = mybir.dt.float8_e4m3fn_x4
E5M2 = mybir.dt.float8_e5m2_x4

P = 128
E, H, HO, T = 4, 512, 1024, 1024
SLOTS = 4
HALF = 512
BANKS = 8
FLOPS = 2 * 2 * T * H * E * HO
BYTES = 2 * (T * H + E * H * HO + T * HO) + 4 * T * E + 4 * (T * H + E * H * HO)
FIRST = 2
DEPTH = {"w_raw": 4, "dz": 8, "first_flip": 2, "slot_flip": 2, "slot_codes": 3, "first_codes": 3, "w_flip": 3, "woven": 2,
         "t_codes": 3, "stage": 1}
EARLY = ("stage", "first_flip", "w_flip", "w_raw", "h_raw", "h_woven")
STAGE_IN = (EARLY, EARLY, ("g_raw",), EARLY)
WARM_FIRST = 4
H_PIECES = 4


def job_lists():
    both = (0, 1)
    halves = [(e, c) for e in range(E) for c in both]
    units = [item + (both,) for item in halves]

    def scale(experts, slots, cs=both):
        return [("scale", e, n, cs) for e in experts for n in slots]

    def flip_w(k, rows=both):
        return [("flip_w",) + halves[k] + (x,) for x in rows]

    def flip_z(e, n):
        return [("flip_z", (e, n, 0), (e, n, 1))]

    def passes(k, rows=both, slots=range(FIRST)):
        return [("mm0",) + halves[k] + (n, rows) for n in slots]

    def q_w(k):
        return [("q_w",) + halves[k]]

    def q_z(e, slots=both):
        return [("q_z", ("first", e), 2 * slots[0], 2 * slots[-1] + 2)]

    def slot_flips(n):
        return [("flip_z", (e, n, 0), (e, n, 1)) for e in range(E)]

    def q_slot(n, parts=both):
        return [("q_z", ("slot", n), E * parts[0], E * parts[-1] + E)]

    def weave(k, gs=both, us=both):
        return [("weave", units[k], g, us) for g in gs]

    def q_t(k, gs=both):
        return [("q_t", units[k], gs)]

    def groups(k, ms=range(H // P)):
        return [("mm1", units[k], m, g) for m in ms for g in both]

    def weave_h(g, pieces=(0, 1, 2, 3)):
        return [("weave_h", g, pieces)]

    def braid(g, half):
        return [("braid", g, half)]

    def drain(jobs):
        return drain_of(jobs[-1])

    lo, hi = (0,), (1,)
    loads = [("load_p",), ("load_g", (0,), both), ("load_w", 0, lo, lo), ("load_g", (1,), both), ("load_w", 0, hi, lo)]
    loads += [("load_g", (2,), both), ("load_w", 0, lo, hi), ("load_w", 0, hi, hi), ("load_w", 1, both, lo), ("load_g", (3,), both)]
    loads += [("load_w", 1, both, hi), ("load_w", 2, both, lo), ("load_g", (4, 5), both), ("load_w", 2, both, hi), ("load_h", 0)]
    loads += [("load_g", (6, 7), both), ("load_w", 3, both, lo), ("load_h", 1), ("load_w", 3, both, hi)]

    whole = [[("mm0",) + halves[k] + (n, both) for k in range(2 * E)] for n in range(2 * SLOTS - 1)]
    last = [[("mm0",) + halves[k] + (2 * SLOTS - 1, rows) for k in range(2 * E)] for rows in (lo, hi)]
    tensor = [("warm", n) for n in range(WARM_FIRST)]
    tensor += flip_z(0, 0) + flip_w(0, lo) + [("warm", 4)] + flip_z(0, 1) + flip_w(0, hi) + flip_z(1, 0) + flip_z(1, 1) + flip_w(1, lo) + [("warm", 5)] + flip_w(1, hi) + flip_z(2, 0) + flip_z(2, 1)
    tensor += passes(0) + flip_w(2) + flip_z(3, 0) + passes(1)
    tensor += flip_w(3) + flip_z(3, 1) + slot_flips(2)[:1] + passes(2)
    tensor += flip_w(4) + slot_flips(2)[1:3] + passes(3)
    tensor += flip_w(5) + slot_flips(2)[3:] + slot_flips(3)[:1] + passes(4) + whole[2][:4]
    tensor += flip_w(6) + slot_flips(3)[1:3] + passes(5) + whole[2][4:6]
    tensor += flip_w(7) + slot_flips(3)[3:] + slot_flips(4)[:1] + passes(6) + whole[2][6:7] + whole[3][:4]
    tensor += slot_flips(4)[1:] + whole[3][4:7] + whole[0][7:] + whole[1][7:] + whole[2][7:] + whole[3][7:] + groups(0, (0, 1))
    tensor += slot_flips(5) + whole[4][:4] + groups(0, (2, 3)) + whole[4][4:] + groups(1)
    tensor += slot_flips(6) + whole[5][:4] + groups(2) + whole[5][4:] + groups(3) + whole[6][:4] + groups(4)
    tensor += slot_flips(7) + whole[6][4:6] + groups(5) + whole[6][6:] + groups(6) + last[0][:4] + last[1][:4]
    tensor += groups(7) + last[0][4:] + last[1][4:]

    vector = scale(range(E), (0,)) + scale(range(E), (1,)) + scale([0, 1, 2], (2,)) + q_z(0) + q_w(0) + scale([3], (2,))
    vector += q_z(1) + scale([0], (3,)) + q_w(1) + scale([1], (3,)) + q_z(2) + q_w(2) + weave(0, lo) + scale([2, 3], (3,)) + scale([0], (4,)) + q_w(3)
    vector += q_z(3) + scale([0], (5,)) + weave(1, lo) + q_w(4) + q_slot(2, lo) + scale([1], (4,)) + scale([0], (6, 7))
    vector += scale([2, 3], (4,)) + q_w(5) + q_slot(2, hi) + weave(0, hi) + weave_h(0, (2, 3)) + q_w(6) + q_slot(3, lo) + [("q_h", 0)]
    vector += q_t(0) + q_w(7) + q_slot(3, hi) + [("q_h", 1)] + scale([1, 2, 3], (5,)) + weave(1, hi) + scale([1], (6,)) + q_slot(4) + scale([1], (7,)) + q_t(1)
    vector += weave(2, lo, hi) + weave(2, hi) + scale([2, 3], (6,)) + q_t(2) + q_slot(5) + weave(3) + scale([2], (7,)) + q_t(3)
    vector += weave(4, lo, hi) + weave(4, hi) + q_slot(6) + q_t(4) + weave(5) + scale([3], (7,)) + q_t(5) + weave(6) + q_slot(7, lo) + q_t(6)
    vector += weave(7) + q_t(7, lo) + q_t(7, hi) + q_slot(7, hi) + [drain(groups(7, (1,))), drain(groups(7, (3,))), drain(last[1])]
    ahead = []

    behind = {
        drain(slot_flips(4)): weave(2, lo, lo),
        drain(slot_flips(2)[:3]): weave_h(0, (0, 1)),
        drain(slot_flips(3)[:1]): weave_h(1, (0, 1)),
        drain(slot_flips(3)[:3]): weave_h(1, (2, 3)),
        drain(groups(1)): weave(4, lo, lo),
    }

    closing = [drain_of(job) for job in tensor if drain_of(job)]
    scalar = ahead + [job for x in closing for job in [x] + behind.get(x, [])]
    stores = [("store",) + job for job in scalar if job[0] in ("drain0", "drain1")]
    scalar = [job for job in scalar if job not in vector]
    return loads, tensor, vector, scalar, stores


def place_of_row(e, n, c):
    if n < FIRST:
        return ("first", e), 2 * n + c
    return ("slot", n), 2 * e + c


def sum_of(job):
    n, halves = job[3:]
    return (n,), halves


def drain_of(job):
    if job[0] == "flip_z":
        return ("drain_z",) + job[1:]
    if job[0] == "flip_w":
        return ("drain_w",) + job[1:]
    if job[0] == "braid":
        return ("drain_h",) + job[1:]
    if job[0] == "mm1" and job[3] == 1:
        return ("drain1",) + job[1:3]
    if job[0] == "mm0" and job[1:3] == (E - 1, 1):
        return ("drain0",) + sum_of(job)
    return None


def uses_of(job, loads):
    kind, a = job[0], job[1:]
    whole = (0,)
    ident = (("identity",), whole)
    if kind.startswith("load_"):
        return [((kind[5:] + "_raw",) + a, whole)], []
    if kind == "identity":
        return [ident], []
    if kind == "warm":
        return [(("bank", "unread"), whole)], [ident]
    if kind == "scale":
        e, n, cs = a
        piece = [x for x in loads if x[0] == "load_g" and n in x[1] and cs[0] in x[2]][0]
        return [(("dz", e, n // SLOTS), [(n, c) for c in cs])], [(("g_raw",) + piece[1:], whole), (("p_raw",), whole)]
    if kind == "flip_w":
        piece = [x for x in loads if x[0] == "load_w" and x[1] == a[0] and a[2] in x[2] and a[1] in x[3]][0]
        return [(("bank",) + job, whole)], [(("w_raw",) + piece[1:], whole), ident]
    if kind == "drain_w":
        return [(("w_flip",) + a[:2], a[2:])], [(("bank", "flip_w") + a, whole)]
    if kind == "q_w":
        return [(("w_codes", a[0]), a[1:])], [(("w_flip",) + a, (0, 1))]
    if kind == "flip_z":
        return [(("bank",) + job, whole)], [(("dz", e, n // SLOTS), [(n, c)]) for e, n, c in a] + [ident]
    if kind == "drain_z":
        key, row = place_of_row(*a[0])
        return [((key[0] + "_flip",) + key, (row, row + 1))], [(("bank", "flip_z") + a, whole)]
    if kind == "q_z":
        rows = range(a[1], a[2])
        return [((a[0][0] + "_codes",) + a[0], rows)], [((a[0][0] + "_flip",) + a[0], rows)]
    if kind == "mm0":
        e, c, n, halves = a
        key, row = place_of_row(e, n, c)
        return [(("bank", "sum") + sum_of(job), whole)], [((key[0] + "_codes",) + key, (row,)), (("w_codes", e), (c,))]
    if kind == "weave":
        unit, g, us = a
        return [(("woven", unit), [(g, u) for u in us])], [(("dz", unit[0], g), [(SLOTS * g + s, unit[1]) for s in range(SLOTS)])]
    if kind == "q_t":
        return [(("t_codes", a[0]), a[1])], [(("woven", a[0]), [(g, u) for g in a[1] for u in (0, 1)])]
    if kind == "weave_h":
        return [(("h_woven", a[0]), a[1])], [(("h_raw", a[0]), whole)]
    if kind == "braid":
        return [(("bank",) + job, whole)], [(("h_raw", a[0]), whole), (("identity16",), whole)]
    if kind == "drain_h":
        return [(("h_woven", a[0]), (2 * a[1], 2 * a[1] + 1))], [(("bank", "braid") + a, whole)]
    if kind == "identity16":
        return [(job, whole)], []
    if kind == "q_h":
        return [(("h_codes",) + a, whole)], [(("h_woven",) + a, range(H_PIECES))]
    if kind == "mm1":
        unit, m, g = a
        return [(("bank", "mm1", unit, m), whole)], [(("t_codes", unit), (g,)), (("h_codes", g), whole)]
    if kind == "drain0":
        return [(("stage",) + job, whole)], [(("bank", "sum") + a, whole)]
    if kind == "drain1":
        return [(("stage",) + job, whole)], [(("bank", "mm1") + a, whole)]
    return [], [(("stage",) + a, whole)]


def plan():
    loads, tensor, vector, scalar, stores = job_lists()
    queues = [loads[:1] + [("identity",)] + [("identity16",) for job in tensor if job == ("braid", 0, 0)] + loads[1:] + stores, tensor, vector, scalar]
    jobs = [job for queue in queues for job in queue]
    assert len(set(jobs)) == len(jobs)
    uses = {job: uses_of(job, loads) for job in jobs}
    writers, readers = {}, {}
    for job in jobs:
        for item, parts in uses[job][0]:
            writers.setdefault(item, []).append((job, set(parts)))
        for item, parts in uses[job][1]:
            readers.setdefault(item, []).append(job)

    place, holder, replaces, count = {}, {}, {}, {}

    def put(item, spot):
        place[item] = spot
        if spot in holder:
            replaces[item] = holder[spot]
        holder[spot] = item

    drains = [store[1:] for store in stores]
    for job in [job for job in queues[0] + vector + scalar if job not in drains]:
        for item, parts in uses[job][0]:
            if item not in place:
                n = count.get(item[0], 0)
                put(item, f"{item[0]}{n % DEPTH.get(item[0], len(jobs))}")
                count[item[0]] = n + 1
    rooms = [f"{kind}{n}" for kinds in STAGE_IN for kind in kinds for n in range(DEPTH.get(kind, count.get(kind)))]
    for n, job in enumerate(drains):
        put(uses[job][0][0][0], rooms[n])
    free = [f"bank{n}" for n in range(BANKS)]
    last_warm = [job for job in tensor if job[0] == "warm"][-1:]
    for job in tensor:
        item = uses[job][0][0][0]
        if item not in place:
            put(item, free.pop(-1 if job[0] == "warm" else 0))
        if drain_of(job) or job in last_warm:
            free.append(place[item])

    def needs_of(job):
        before = []
        for item, parts in uses[job][0]:
            if item in replaces:
                before.extend(readers.get(replaces[item], []) + [other for other, p in writers[replaces[item]]])
        for item, parts in uses[job][1]:
            before.extend(other for other, p in writers[item] if p & set(parts))
        return before

    return queues, uses, place, {job: needs_of(job) for job in jobs}


def tile_enhancedmathematicalreasoning_pa_v_kernel(
    tc, hidden_states, op_logits, We, be, op_w, grad_out, out_0, out_1
):
    nc = tc.nc
    h_view = hidden_states.flatten_outer_dims().rearrange("(g p s) i -> g p (s i)", g=2, s=SLOTS)
    g_view = grad_out.flatten_outer_dims().rearrange("(g p s) j -> g p s j", g=2, s=SLOTS)
    p_view = op_w.flatten_outer_dims().rearrange("(g p s) e -> p g (s e)", g=2, s=SLOTS)
    w_view = We.rearrange("e (a p) j -> e p a j", p=P)
    out0_view = out_0.flatten_outer_dims().rearrange("(g p s) i -> g p s i", g=2, s=SLOTS)
    out1_view = out_1.rearrange("e (m p) j -> e m p j", p=P)
    queues, uses, place, needs = plan()
    vector = queues[2]

    with ExitStack() as ctx:
        sbuf = ctx.enter_context(tc.tile_pool(name="sbuf", bufs=1))
        psum = ctx.enter_context(tc.psum_pool(name="psum", bufs=1))
        tiles = {}

        def tile_of(item, width, dtype, part=""):
            if (item, part) not in tiles:
                tag = place[item]
                if item[0] == "bank":
                    tiles[item, part] = psum.tile([P, width], dtype, name=tag, tag=tag)
                else:
                    tiles[item, part] = sbuf.tile([P, width], dtype, name=tag, tag=tag,
                                                  align_bytes=64 if item[0] in ("p_raw", "identity", "identity16") else 256)
            return tiles[item, part]

        def span(n, width, count=1):
            return slice(n * width, (n + count) * width)

        def copy(job, out, in_):
            if job in vector:
                nc.vector.tensor_copy(out=out, in_=in_)
            else:
                nc.scalar.copy(out=out, in_=in_)

        def weave_copy(job, dst, src):
            copy(job, dst.rearrange("p (o w x s) -> p o w s x", o=2, x=4, s=SLOTS),
                 src.rearrange("p o (w x) s -> p o w s x", x=4))

        def mx_operand(item, cols, fmt):
            both = tiles[item, ""]
            width = both.shape[1] // 5
            return both[:, : 4 * width].bitcast(U32)[:, cols].bitcast(fmt), both[:, 4 * width :][:, cols]

        def quantize(item, width, cols, src, fmt):
            tile_of(item, 5 * width, U8)
            codes, scales = mx_operand(item, cols, fmt)
            nc.vector.quantize_mx(out=codes, scales=scales, in_=src)

        def matmul_mx(out, lhs, lhs_cols, lhs_fmt, rhs, rhs_cols, rhs_fmt, start, stop):
            lhs_codes, lhs_scales = mx_operand(lhs, lhs_cols, lhs_fmt)
            rhs_codes, rhs_scales = mx_operand(rhs, rhs_cols, rhs_fmt)
            nc.tensor.matmul_mx(out=out, lhsT=lhs_codes, lhsT_scale=lhs_scales, rhs=rhs_codes, rhs_scale=rhs_scales,
                                start=start, stop=stop)

        def flip(bank, blocks):
            for n, block in enumerate(blocks):
                nc.tensor.transpose(bank[:, span(n, P)], block, tiles[("identity",), ""][:])

        def emit(job):
            kind, a = job[0], job[1:]
            written = uses[job][0][0][0] if uses[job][0] else None
            read = [item for item, parts in uses[job][1]]
            src = tiles[read[0], ""] if read else None
            if kind == "identity":
                make_identity(nc, tile_of(written, P, F32)[:])
            elif kind == "identity16":
                make_identity(nc, tile_of(written, P, BF16)[:])
            elif kind == "braid":
                bank = tile_of(written, HO, BF16)[:].rearrange("p (i r s) -> p r i s", r=2, s=2)
                rows = src[:].rearrange("p (r s i) -> p r i s", r=2, s=2)
                for r in range(2):
                    nc.tensor.matmul(out=bank[:, r], lhsT=tiles[read[1], ""][:], rhs=rows[:, r, span(a[1], H // 2)],
                                     start=True, stop=True)
            elif kind == "drain_h":
                copy(job, tile_of(written, SLOTS * H, BF16)[:, span(a[1], HO)], src[:])
            elif kind == "load_p":
                nc.scalar.dma_start(out=tile_of(written, 2 * SLOTS * E, F32)[:].rearrange("p (g x) -> p g x", g=2), in_=p_view)
            elif kind == "load_g":
                slots, cs = a
                g, s = divmod(slots[0], SLOTS)
                raw = tile_of(written, len(slots) * len(cs) * HALF, BF16)
                nc.sync.dma_start(out=raw[:].rearrange("p (s j) -> p s j", s=len(slots)),
                                  in_=g_view[g][:, s : s + len(slots), span(cs[0], HALF, len(cs))])
            elif kind == "load_w":
                e, halves, cs = a
                raw = tile_of(written, 2 * len(halves) * len(cs) * HALF, BF16)
                nc.sync.dma_start(out=raw[:].rearrange("p (a j) -> p a j", a=2 * len(halves)),
                                  in_=w_view[e][:, span(halves[0], 2, len(halves)), span(cs[0], HALF, len(cs))])
            elif kind == "load_h":
                nc.sync.dma_start(out=tile_of(written, SLOTS * H, BF16)[:], in_=h_view[a[0]])
            elif kind == "warm":
                halves = src[:].bitcast(BF16)
                twice = halves.unsqueeze(1).to_broadcast([P, 2, 2 * P])
                nc.tensor.matmul(out=tile_of(written, HALF, F32)[:], lhsT=halves[:, :P], rhs=twice, start=True, stop=True)
            elif kind == "scale":
                e, n, cs = a
                slots, have = read[0][1:]
                first = slots.index(n) * len(have) + have.index(cs[0])
                row = tile_of(written, SLOTS * HO, BF16)[:, span(n % SLOTS, HO)].rearrange("p (u w x) -> p u w x", u=2, x=2)
                out = row[:, :, span(cs[0], P, len(cs))]
                in_ = src[:, span(first, HALF, len(cs))].rearrange("p (w u x) -> p u w x", u=2, x=2)
                factor = tiles[read[1], ""][:, span(E * n + e, 1)]
                if job in vector:
                    nc.vector.tensor_scalar(out=out, in0=in_, scalar1=factor, scalar2=None, op0=mybir.AluOpType.mult)
                else:
                    nc.scalar.activation(out=out, in_=in_, func=mybir.ActivationFunctionType.Copy, scale=factor)
            elif kind == "flip_w":
                words = src[:].bitcast(F32)
                halves, cs = read[0][2:]
                rows = [2 * halves.index(a[2]) + r for r in range(2)]
                starts = [(row * len(cs) + cs.index(a[1])) * (HALF // 2) + u for row in rows for u in range(2)]
                flip(tile_of(written, HALF, F32), [words[:, x : x + 2 * P - 1 : 2] for x in starts])
            elif kind == "flip_z":
                blocks = [tiles[item, ""][:].bitcast(F32)[:, span(4 * (n % SLOTS) + 2 * u + c, P)]
                          for item, (e, n, c) in zip(read, a) for u in range(2)]
                flip(tile_of(written, HALF, F32), blocks)
            elif kind in ("drain_z", "drain_w"):
                rows = {"first_flip": 2 * FIRST, "slot_flip": 2 * E, "w_flip": SLOTS}[written[0]]
                first = uses[job][0][0][1][0] * (2 if kind == "drain_w" else 1)
                words = tile_of(written, rows * HALF, BF16)[:].bitcast(F32)[:, span(first, HALF // 2, 2)]
                copy(job, words.rearrange("p (r n u) -> p r n u", r=2, u=2),
                     src[:].rearrange("p (r u n) -> p r n u", r=2, u=2))
            elif kind == "q_z":
                rows = 2 * E if a[0][0] == "slot" else 2 * FIRST
                quantize(written, rows * P, span(a[1], P, a[2] - a[1]), src[:, span(a[1], HALF, a[2] - a[1])], E5M2)
            elif kind == "q_w":
                quantize(written, HO, span(a[1], HALF), src[:], E4M3)
            elif kind == "q_h":
                quantize(written, HALF, span(0, HALF), src[:], E4M3)
            elif kind == "weave":
                (e, c, parts), g, us = a
                width = len(parts) * HALF // 2
                dst = tile_of(written, 2 * SLOTS * width, BF16)[:, span(2 * g + us[0], 2 * width, len(us))]
                cols = src[:].rearrange("p (s u c w) -> p c u w s", s=SLOTS, u=2, c=2)[:, c, :, span(parts[0], P, len(parts))]
                weave_copy(job, dst, cols if len(us) == 2 else cols[:, us[0]].rearrange("p (o w) s -> p o w s", o=2))
            elif kind == "weave_h":
                first, count = a[1][0], len(a[1])
                cols = src[:].rearrange("p (s i) -> p i s", s=SLOTS)[:, span(first, H // H_PIECES, count)]
                weave_copy(job, tile_of(written, SLOTS * H, BF16)[:, span(first, SLOTS * H // H_PIECES, count)],
                           cols.rearrange("p (o w) s -> p o w s", o=2))
            elif kind == "q_t":
                width, gs = len(a[0][2]) * HALF // 2, a[1]
                quantize(written, 2 * width, span(gs[0], width, len(gs)), src[:, span(gs[0], SLOTS * width, len(gs))], E5M2)
            elif kind == "mm0":
                e, c, n, halves = a
                out = tile_of(written, HALF // 2 * len(halves), F32)[:]
                matmul_mx(out, read[0], span(place_of_row(e, n, c)[1], P), E5M2,
                          read[1], span(2 * c + halves[0], HALF // 2, len(halves)), E4M3,
                          (e, c) == (0, 0), (e, c) == (E - 1, 1))
            elif kind == "mm1":
                width, m, g = len(a[0][2]) * HALF // 2, a[1], a[2]
                matmul_mx(tile_of(written, width, F32)[:], read[1], span(m, P), E4M3, read[0], span(g, width), E5M2,
                          g == 0, g == 1)
            elif kind == "drain0":
                copy(job, tile_of(written, HALF // 2 * len(a[1]), F32)[:], src[:])
            elif kind == "drain1":
                copy(job, tile_of(written, src.shape[1], F32)[:].rearrange("p (w u x) -> p w u x", u=2, x=2),
                     src[:].rearrange("p (u w x) -> p w u x", u=2, x=2))
            elif a[0] == "drain0":
                g, s = divmod(a[1][0], SLOTS)
                nc.sync.dma_start(out=out0_view[g][:, s, span(a[2][0], HALF // 2, len(a[2]))], in_=src[:])
            else:
                e, c, parts = a[1]
                nc.sync.dma_start(out=out1_view[e, a[2]][:, span(2 * c + parts[0], HALF // 2, len(parts))], in_=src[:])

        with tc.manual_schedule():
            done = set()
            heads = [0] * len(queues)
            while len(done) < len(uses):
                count = len(done)
                for q, queue in enumerate(queues):
                    while heads[q] < len(queue) and all(other in done for other in needs[queue[heads[q]]]):
                        emit(queue[heads[q]])
                        done.add(queue[heads[q]])
                        heads[q] = heads[q] + 1
                assert len(done) > count, [queue[n : n + 1] for queue, n in zip(queues, heads)]
